import numpy as np
import ml_dtypes


def mxq(x, axis, fmt="e4m3"):
    dtype, down = {"e4m3": (ml_dtypes.float8_e4m3fn, 7), "e5m2": (ml_dtypes.float8_e5m2, 14)}[fmt]
    v = np.moveaxis(np.asarray(x, np.float32).astype(ml_dtypes.bfloat16).astype(np.float64), axis, -1)
    blocks = v.reshape(v.shape[:-1] + (-1, 32))
    amax = np.abs(blocks).max(-1, keepdims=True)
    byte = np.maximum(np.where(amax > 0, np.frexp(amax)[1] - 1 + 127, 0) - down, 1)
    scale = np.exp2(byte - 127.0)
    codes = (blocks / scale).astype(np.float32).astype(dtype).astype(np.float64)
    return np.moveaxis((codes * scale).reshape(v.shape), -1, axis)


WIDE = False


def mx_kscale(k):
    if not WIDE:
        return np.ones(k)
    levels = np.array([10, -10, 5, -5, 0])
    a = np.random.permutation(np.resize(levels, k // 512 * 4)).reshape(k // 512, 4)
    idx = np.arange(k)
    return np.exp2(a[idx // 512, idx % 128 // 32])


BF16 = ml_dtypes.bfloat16


def bf(x):
    return np.asarray(x, np.float32).astype(BF16)


def f64(x):
    return np.asarray(x).astype(np.float64)


B, S, HID, H, G = 1, 512, 2048, 16, 1
D = HID // H
NEG = -1e9


def setup_inputs():
    u = mx_kscale(HID)
    t = np.where(np.arange(D) < D // 2, u.max(), u.min())
    pad = np.where(np.random.random((B, S)) < 0.25, 1.0, 0.0)
    pad[:, 0] = 0.0
    sgn = np.where(np.random.random(G * D) < 0.5, -1.0, 1.0)
    return {"q": bf(np.random.standard_normal((B, S, HID)) * 1.5),
            "k": bf(np.random.standard_normal((B, S, G * D)) * 1.5),
            "v": bf((0.25 + 1.5 * np.random.random((B, S, G * D))) * sgn * np.tile(t, G)),
            "causal_mask": bf(np.triu(np.ones((1, 1, S, S)), k=1)),
            "padding_mask": bf(pad),
            "Wo": bf(np.random.standard_normal((HID, HID)) * 2.0 / np.sqrt(HID) / np.tile(t, H)[None, :]),
            "bo": bf(np.random.standard_normal(HID) * 0.1)}


def reference(q, k, v, causal_mask, padding_mask, Wo, bo):
    qh = f64(q).reshape(B, S, H, D).transpose(0, 2, 1, 3)
    kh = f64(k).reshape(B, S, G, D).transpose(0, 2, 1, 3)
    vh = f64(v).reshape(B, S, G, D).transpose(0, 2, 1, 3)
    scores = qh @ kh.transpose(0, 1, 3, 2) / np.sqrt(D)
    scores = scores + f64(causal_mask) * NEG
    scores = scores + f64(padding_mask)[:, None, None, :] * NEG
    e = np.exp(scores - scores.max(-1, keepdims=True))
    o = (mxq(e, 3, "e4m3") @ mxq(vh, 2, "e4m3")) / e.sum(-1, keepdims=True)
    o = o.transpose(0, 2, 1, 3).reshape(B, S, H * D)
    return (mxq(o, 2, "e4m3") @ mxq(f64(Wo), 1, "e4m3").T) + f64(bo)

@@ -1,0 +1,325 @@
+import math
+from contextlib import ExitStack
+
+import concourse.mybir as mybir
+from concourse.masks import make_identity
+
+BF16 = mybir.dt.bfloat16
+F32 = mybir.dt.float32
+U32 = mybir.dt.uint32
+U8 = mybir.dt.uint8
+FP8X4 = mybir.dt.float8_e4m3fn_x4
+ALU = mybir.AluOpType
+ACT = mybir.ActivationFunctionType
+
+P = 128
+S = 512
+HEADS = 16
+HID = HEADS * P
+Q_TILES = S // P
+GROUP = 4
+GROUPS = HEADS // GROUP
+BANK_F32 = 512
+N_SLICES = HID // BANK_F32
+NEG = -1.0e9
+SCALE = 1.0 / math.sqrt(P)
+E_PAIRS = 3
+PAIRS_PER_TILE = HEADS // 2
+PAIRS = Q_TILES * PAIRS_PER_TILE
+ALL_GROUPS = Q_TILES * GROUPS
+WEIGHT_UNITS = N_SLICES * GROUPS
+LAG_E_TRANSPOSE = 2
+LAG_E_QUANTISE = 3
+LAG_NORMALISE = 5
+LAG_O_TRANSPOSE = 6
+WEIGHT_LAG = 2
+PROJECT_LAG = 18
+STEPS = (Q_TILES - 1) * PAIRS_PER_TILE + PROJECT_LAG + N_SLICES
+
+FLOPS = 2 * 2 * HEADS * S * S * P + 2 * S * HID * HID
+
+
+def due(index, count):
+    return 0 <= index < count
+
+
+def tile_groupqueryattention_pa_kernel(tc, q, k, v, causal_mask, padding_mask, Wo, bo, out):
+    nc = tc.nc
+    with ExitStack() as ctx:
+        keep = ctx.enter_context(tc.tile_pool(name="keep", bufs=1))
+        work = ctx.enter_context(tc.tile_pool(name="work", bufs=3))
+        stats = ctx.enter_context(tc.tile_pool(name="stats", bufs=4))
+        psum_s = ctx.enter_context(tc.psum_pool(name="psum_s", bufs=3))
+        psum_b = ctx.enter_context(tc.psum_pool(name="psum_b", bufs=4))
+        psum_o = ctx.enter_context(tc.psum_pool(name="psum_o", bufs=1))
+        ctx.enter_context(tc.manual_schedule())
+
+        k_raw = keep.tile([P, Q_TILES, P], BF16)
+        nc.sync.dma_start(out=k_raw[:], in_=k[0].rearrange("(t p) d -> p t d", p=P))
+        q_raw = []
+        for qt in range(Q_TILES):
+            q_tile = keep.tile([P, HID], BF16, name="q_raw%d" % qt)
+            q_raw.append(q_tile)
+        wo_raw = []
+        for nt in range(HID // P):
+            w_tile = keep.tile([P, HID], BF16, name="wo_raw%d" % nt)
+            wo_raw.append(w_tile)
+        nc.sync.dma_start(out=q_raw[0][:], in_=q[0, 0:P, :])
+        pad_all = keep.tile([P, S], BF16)
+        nc.sync.dma_start(out=pad_all[:], in_=padding_mask[0].partition_broadcast(P))
+        causal_raw = []
+        for qt in range(Q_TILES):
+            n_keys = P * (qt + 1)
+            c_tile = keep.tile([P, n_keys], BF16, name="causal_raw%d" % qt)
+            nc.sync.dma_start(out=c_tile[:], in_=causal_mask[0, 0, qt * P : (qt + 1) * P, 0:n_keys])
+            causal_raw.append(c_tile)
+        v_raw = keep.tile([P, 4, P], BF16)
+        nc.sync.dma_start(
+            out=v_raw[:].rearrange("p (u e) d -> p u (e d)", u=2),
+            in_=v[0].rearrange("(u p e) d -> p u (e d)", u=2, e=2),
+        )
+        for n_slice in range(N_SLICES):
+            for i in range(4):
+                nt = 4 * n_slice + i
+                nc.sync.dma_start(out=wo_raw[nt][:], in_=Wo[nt * P : (nt + 1) * P, :])
+            if n_slice + 1 < Q_TILES:
+                qt = n_slice + 1
+                nc.sync.dma_start(out=q_raw[qt][:], in_=q[0, qt * P : (qt + 1) * P, :])
+        bias_all = keep.tile([P, HID], BF16)
+        nc.sync.dma_start(out=bias_all[:], in_=bo.partition_broadcast(P))
+
+        ident_bf = keep.tile([P, P], BF16)
+        make_identity(nc, ident_bf[:])
+        ident_f32 = keep.tile([P, P], F32)
+        make_identity(nc, ident_f32[:])
+        e_pairs = []
+        for i in range(E_PAIRS):
+            e_tile = keep.tile([P, 2 * S], BF16, name="e_pair%d" % i)
+            nc.vector.memset(e_tile[:], 0.0)
+            e_pairs.append(e_tile)
+
+        kT = keep.tile([P, S], BF16)
+        kT_ps = psum_b.tile([P, Q_TILES, P], BF16, tag="bank")
+        for t in range(Q_TILES):
+            nc.tensor.transpose(kT_ps[:, t, :], k_raw[:, t, :], ident_bf[:])
+        nc.scalar.copy(out=kT[:], in_=kT_ps[:].rearrange("p t c -> p (t c)"))
+
+        mask_neg = []
+        for qt in range(Q_TILES):
+            n_keys = P * (qt + 1)
+            m_tile = keep.tile([P, n_keys], BF16, name="mask_neg%d" % qt)
+            nc.vector.tensor_tensor(out=m_tile[:], in0=causal_raw[qt][:], in1=pad_all[:, 0:n_keys], op=ALU.add)
+            nc.vector.tensor_scalar_mul(m_tile[:], m_tile[:], NEG)
+            mask_neg.append(m_tile)
+
+        v_grouped = keep.tile([P, 4 * P], BF16, align_bytes=64)
+        nc.vector.tensor_copy(
+            out=v_grouped[:].rearrange("p (d t) -> p d t", t=4), in_=v_raw[:].rearrange("p t d -> p d t")
+        )
+        v_codes = keep.tile([P, P], U32, align_bytes=64)
+        v_scales = keep.tile([P, P], U8, align_bytes=64)
+        nc.vector.quantize_mx(out=v_codes[:].bitcast(FP8X4), scales=v_scales[:], in_=v_grouped[:])
+
+        o_codes = keep.tile([P, GROUPS * S], U32, align_bytes=64)
+        o_scales = keep.tile([P, GROUPS * S], U8, align_bytes=64)
+        w_codes = keep.tile([P, GROUPS * HID], U32, align_bytes=64)
+        w_scales = keep.tile([P, GROUPS * HID], U8, align_bytes=64)
+
+        qT_of = {}
+        rowsum_of = {}
+        e_grouped_of = {}
+        e_codes_of = {}
+        o_ps_of = {}
+        o_sb_of = {}
+        o_grouped_of = {}
+        w_grouped_of = {}
+
+        def transpose_queries(qt, half):
+            if half == 0:
+                qT_new = work.tile([P, HID], BF16, name="qT", bufs=2)
+                qT_of[qt] = qT_new
+            qT_ps = psum_b.tile([P, 8, P], BF16, tag="bank")
+            for i in range(8):
+                h = 8 * half + i
+                nc.tensor.transpose(qT_ps[:, i, :], q_raw[qt][:, h * P : (h + 1) * P], ident_bf[:])
+            nc.scalar.copy(
+                out=qT_of[qt][:, half * 8 * P : (half + 1) * 8 * P], in_=qT_ps[:].rearrange("p i c -> p (i c)")
+            )
+
+        def exponentials(pair, i):
+            qt, pair_in_tile = divmod(pair, PAIRS_PER_TILE)
+            h = 2 * pair_in_tile + i
+            n_keys = P * (qt + 1)
+            group, second = divmod(pair, 2)
+            if second == 0 and i == 0:
+                rowsum_new = stats.tile([P, GROUP], F32, name="rowsum")
+                rowsum_of[group] = rowsum_new
+            scores = psum_s.tile([P, n_keys], F32, tag="scores")
+            nc.tensor.matmul(
+                scores[:], lhsT=qT_of[qt][:, h * P : (h + 1) * P], rhs=kT[:, 0:n_keys], start=True, stop=False
+            )
+            nc.tensor.matmul(scores[:], lhsT=ident_bf[:], rhs=mask_neg[qt][:], start=False, stop=True)
+            top = stats.tile([P, 1], F32)
+            nc.vector.tensor_reduce(out=top[:], in_=scores[:], axis=mybir.AxisListType.X, op=ALU.max)
+            shift = stats.tile([P, 1], F32)
+            nc.scalar.mul(out=shift[:], in_=top[:], mul=-SCALE)
+            j = 2 * second + i
+            nc.scalar.activation(
+                out=e_pairs[pair % E_PAIRS][:, i * S : i * S + n_keys],
+                in_=scores[:],
+                func=ACT.Exp,
+                bias=shift[:],
+                scale=SCALE,
+                accum_out=rowsum_of[group][:, j : j + 1],
+            )
+
+        def transpose_e(pair):
+            e_words = e_pairs[pair % E_PAIRS][:].bitcast(F32)
+            eT_ps = psum_b.tile([P, 2, 2, P], F32, tag="bank")
+            for i in range(2):
+                for u in range(2):
+                    first_word = i * (S // 2) + u * P
+                    nc.tensor.transpose(eT_ps[:, i, u, :], e_words[:, first_word : first_word + P], ident_f32[:])
+            e_grouped = work.tile([P, 2 * P * 4], BF16, align_bytes=64)
+            nc.scalar.copy(
+                out=e_grouped[:].bitcast(F32).rearrange("p (i r u) -> p i r u", i=2, u=2),
+                in_=eT_ps[:].rearrange("p i u r -> p i r u"),
+            )
+            e_grouped_of[pair] = e_grouped
+
+        def quantise_e(pair):
+            e_codes = work.tile([P, 2 * P], U32, align_bytes=64)
+            e_scales = work.tile([P, 2 * P], U8, align_bytes=64)
+            nc.vector.quantize_mx(out=e_codes[:].bitcast(FP8X4), scales=e_scales[:], in_=e_grouped_of[pair][:])
+            e_codes_of[pair] = (e_codes, e_scales)
+
+        def attend_values(pair):
+            group, second = divmod(pair, 2)
+            if second == 0:
+                o_ps_new = psum_o.tile([P, GROUP, P], F32, name="o_ps")
+                o_ps_of[group] = o_ps_new
+            e_codes, e_scales = e_codes_of[pair]
+            for i in range(2):
+                nc.tensor.matmul_mx(
+                    out=o_ps_of[group][:, 2 * second + i, :],
+                    lhsT=e_codes[:, i * P : (i + 1) * P].bitcast(FP8X4),
+                    lhsT_scale=e_scales[:, i * P : (i + 1) * P],
+                    rhs=v_codes[:].bitcast(FP8X4),
+                    rhs_scale=v_scales[:],
+                    start=True,
+                    stop=True,
+                )
+
+        def normalise(group):
+            recip = stats.tile([P, GROUP], F32)
+            nc.vector.reciprocal(recip[:], rowsum_of[group][:])
+            o_sb = work.tile([P, GROUP * P], BF16)
+            nc.vector.tensor_tensor(
+                out=o_sb[:].rearrange("p (t d) -> p t d", t=GROUP),
+                in0=o_ps_of[group][:],
+                in1=recip[:].unsqueeze(2).to_broadcast([P, GROUP, P]),
+                op=ALU.mult,
+            )
+            o_sb_of[group] = o_sb
+
+        def transpose_o(group):
+            o_words = o_sb_of[group][:].bitcast(F32)
+            oT_ps = psum_b.tile([P, 2, P], F32, tag="bank")
+            for u in range(2):
+                nc.tensor.transpose(oT_ps[:, u, :], o_words[:, u * P : (u + 1) * P], ident_f32[:])
+            o_grouped = work.tile([P, P * 4], BF16, align_bytes=64)
+            nc.scalar.copy(
+                out=o_grouped[:].bitcast(F32).rearrange("p (r u) -> p r u", u=2),
+                in_=oT_ps[:].rearrange("p u r -> p r u"),
+            )
+            o_grouped_of[group] = o_grouped
+
+        def quantise_o(group):
+            qt, g = divmod(group, GROUPS)
+            cols = slice(g * S + qt * P, g * S + (qt + 1) * P)
+            nc.vector.quantize_mx(
+                out=o_codes[:, cols].bitcast(FP8X4), scales=o_scales[:, cols], in_=o_grouped_of[group][:]
+            )
+
+        def transpose_weights(unit):
+            n_slice, g = divmod(unit, GROUPS)
+            w_grouped = work.tile([P, BANK_F32 * 4], BF16, align_bytes=64)
+            for half in range(2):
+                wT_ps = psum_b.tile([P, 2, 2, P], F32, tag="bank")
+                for i in range(2):
+                    words = wo_raw[4 * n_slice + 2 * half + i][:].bitcast(F32)
+                    for u in range(2):
+                        first_word = g * 2 * P + u * P
+                        nc.tensor.transpose(wT_ps[:, i, u, :], words[:, first_word : first_word + P], ident_f32[:])
+                nc.scalar.copy(
+                    out=w_grouped[:, half * 1024 : (half + 1) * 1024]
+                    .bitcast(F32)
+                    .rearrange("p (i n u) -> p i n u", i=2, u=2),
+                    in_=wT_ps[:].rearrange("p i u n -> p i n u"),
+                )
+            w_grouped_of[unit] = w_grouped
+
+        def quantise_weights(unit):
+            n_slice, g = divmod(unit, GROUPS)
+            cols = slice(g * HID + n_slice * BANK_F32, g * HID + (n_slice + 1) * BANK_F32)
+            nc.vector.quantize_mx(
+                out=w_codes[:, cols].bitcast(FP8X4), scales=w_scales[:, cols], in_=w_grouped_of[unit][:]
+            )
+
+        def project(qt, n_slice):
+            y_ps = psum_b.tile([P, BANK_F32], F32, tag="bank")
+            for g in range(GROUPS):
+                o_cols = slice(g * S + qt * P, g * S + (qt + 1) * P)
+                w_cols = slice(g * HID + n_slice * BANK_F32, g * HID + (n_slice + 1) * BANK_F32)
+                nc.tensor.matmul_mx(
+                    out=y_ps[:],
+                    lhsT=o_codes[:, o_cols].bitcast(FP8X4),
+                    lhsT_scale=o_scales[:, o_cols],
+                    rhs=w_codes[:, w_cols].bitcast(FP8X4),
+                    rhs_scale=w_scales[:, w_cols],
+                    start=(g == 0),
+                    stop=(g == GROUPS - 1),
+                )
+            return y_ps
+
+        def add_bias_and_store(qt, n_slice, y_ps):
+            n_cols = slice(n_slice * BANK_F32, (n_slice + 1) * BANK_F32)
+            y_sb = work.tile([P, BANK_F32], F32)
+            nc.vector.tensor_tensor(out=y_sb[:], in0=y_ps[:], in1=bias_all[:, n_cols], op=ALU.add)
+            nc.sync.dma_start(out=out[0, qt * P : (qt + 1) * P, n_cols], in_=y_sb[:])
+
+        transpose_queries(0, 0)
+        transpose_queries(0, 1)
+        for step in range(STEPS):
+            if due(step - LAG_E_TRANSPOSE, PAIRS):
+                transpose_e(step - LAG_E_TRANSPOSE)
+            group, odd = divmod(step - LAG_O_TRANSPOSE, 2)
+            if odd == 0 and due(group, ALL_GROUPS):
+                transpose_o(group)
+            if due(step - WEIGHT_LAG, WEIGHT_UNITS):
+                transpose_weights(step - WEIGHT_LAG)
+            next_qt, steps_into_tile = divmod(step + 2, PAIRS_PER_TILE)
+            if steps_into_tile < 2 and due(next_qt - 1, Q_TILES - 1):
+                transpose_queries(next_qt, steps_into_tile)
+            if due(step - LAG_E_QUANTISE, PAIRS):
+                quantise_e(step - LAG_E_QUANTISE)
+            group, odd = divmod(step - LAG_NORMALISE, 2)
+            if odd == 0 and due(group, ALL_GROUPS):
+                normalise(group)
+            if due(step - WEIGHT_LAG - 1, WEIGHT_UNITS):
+                quantise_weights(step - WEIGHT_LAG - 1)
+            group, odd = divmod(step - LAG_O_TRANSPOSE, 2)
+            if odd == 0 and due(group, ALL_GROUPS):
+                quantise_o(group)
+            if step < PAIRS:
+                exponentials(step, 0)
+            if due(step - LAG_E_QUANTISE, PAIRS):
+                attend_values(step - LAG_E_QUANTISE)
+            qt, n_slice = divmod(step - PROJECT_LAG, PAIRS_PER_TILE)
+            projecting = due(qt, Q_TILES) and n_slice < N_SLICES
+            if projecting:
+                y_ps = project(qt, n_slice)
+            if step < PAIRS:
+                exponentials(step, 1)
+            if projecting:
+                add_bias_and_store(qt, n_slice, y_ps)

@@ -29,14 +29,21 @@ PAIRS = Q_TILES * PAIRS_PER_TILE
 ALL_GROUPS = Q_TILES * GROUPS
 WEIGHT_UNITS = N_SLICES * GROUPS
 LAG_E_TRANSPOSE = 2
-LAG_E_QUANTISE = 3
-LAG_NORMALISE = 5
-LAG_O_TRANSPOSE = 6
+LAG_E_QUANTISE = 4
+LAG_ATTEND = 5
+LAG_O_TRANSPOSE = 8
+LAG_O_QUANTISE = 10
 WEIGHT_LAG = 2
-PROJECT_LAG = 18
-STEPS = (Q_TILES - 1) * PAIRS_PER_TILE + PROJECT_LAG + N_SLICES
+WEIGHT_QUANTISE_LAG = 4
+PROJECT_LAG = 17
+WEIGHTS_READY = 20
+STEPS = (Q_TILES - 1) * PAIRS_PER_TILE + PROJECT_LAG + N_SLICES + 1
 
 FLOPS = 2 * 2 * HEADS * S * S * P + 2 * S * HID * HID
+
+
+def first_project_step(qt):
+    return max(qt * PAIRS_PER_TILE + PROJECT_LAG, WEIGHTS_READY + qt * N_SLICES)
 
 
 def due(index, count):
@@ -49,9 +56,7 @@ def tile_groupqueryattention_pa_kernel(tc, q, k, v, causal_mask, padding_mask, W
         keep = ctx.enter_context(tc.tile_pool(name="keep", bufs=1))
         work = ctx.enter_context(tc.tile_pool(name="work", bufs=3))
         stats = ctx.enter_context(tc.tile_pool(name="stats", bufs=4))
-        psum_s = ctx.enter_context(tc.psum_pool(name="psum_s", bufs=3))
-        psum_b = ctx.enter_context(tc.psum_pool(name="psum_b", bufs=4))
-        psum_o = ctx.enter_context(tc.psum_pool(name="psum_o", bufs=1))
+        psum_b = ctx.enter_context(tc.psum_pool(name="psum_b", bufs=8))
         ctx.enter_context(tc.manual_schedule())
 
         k_raw = keep.tile([P, Q_TILES, P], BF16)
@@ -129,8 +134,8 @@ def tile_groupqueryattention_pa_kernel(tc, q, k, v, causal_mask, padding_mask, W
         rowsum_of = {}
         e_grouped_of = {}
         e_codes_of = {}
-        o_ps_of = {}
         o_sb_of = {}
+        o_ps_of = {}
         o_grouped_of = {}
         w_grouped_of = {}
 
@@ -146,32 +151,40 @@ def tile_groupqueryattention_pa_kernel(tc, q, k, v, causal_mask, padding_mask, W
                 out=qT_of[qt][:, half * 8 * P : (half + 1) * 8 * P], in_=qT_ps[:].rearrange("p i c -> p (i c)")
             )
 
-        def exponentials(pair, i):
+        def exponentials(pair):
             qt, pair_in_tile = divmod(pair, PAIRS_PER_TILE)
-            h = 2 * pair_in_tile + i
             n_keys = P * (qt + 1)
-            group, second = divmod(pair, 2)
-            if second == 0 and i == 0:
-                rowsum_new = stats.tile([P, GROUP], F32, name="rowsum")
-                rowsum_of[group] = rowsum_new
-            scores = psum_s.tile([P, n_keys], F32, tag="scores")
-            nc.tensor.matmul(
-                scores[:], lhsT=qT_of[qt][:, h * P : (h + 1) * P], rhs=kT[:, 0:n_keys], start=True, stop=False
-            )
-            nc.tensor.matmul(scores[:], lhsT=ident_bf[:], rhs=mask_neg[qt][:], start=False, stop=True)
-            top = stats.tile([P, 1], F32)
-            nc.vector.tensor_reduce(out=top[:], in_=scores[:], axis=mybir.AxisListType.X, op=ALU.max)
-            shift = stats.tile([P, 1], F32)
-            nc.scalar.mul(out=shift[:], in_=top[:], mul=-SCALE)
-            j = 2 * second + i
-            nc.scalar.activation(
-                out=e_pairs[pair % E_PAIRS][:, i * S : i * S + n_keys],
-                in_=scores[:],
-                func=ACT.Exp,
-                bias=shift[:],
-                scale=SCALE,
-                accum_out=rowsum_of[group][:, j : j + 1],
-            )
+            heads_per_bank = min(2, BANK_F32 // n_keys)
+            top = stats.tile([P, 2], F32)
+            shift = stats.tile([P, 2], F32)
+            rowsum = stats.tile([P, 2], F32, bufs=8)
+            rowsum_of[pair] = rowsum
+            scores_of = []
+            for first in range(0, 2, heads_per_bank):
+                scores = psum_b.tile([P, heads_per_bank, n_keys], F32, tag="bank")
+                for i in range(heads_per_bank):
+                    h = 2 * pair_in_tile + first + i
+                    nc.tensor.matmul(
+                        scores[:, i, :],
+                        lhsT=qT_of[qt][:, h * P : (h + 1) * P],
+                        rhs=kT[:, 0:n_keys],
+                        start=True,
+                        stop=False,
+                    )
+                    nc.tensor.matmul(scores[:, i, :], lhsT=ident_bf[:], rhs=mask_neg[qt][:], start=False, stop=True)
+                    scores_of.append(scores[:, i, :])
+                cols = slice(first, first + heads_per_bank)
+                nc.vector.tensor_reduce(out=top[:, cols], in_=scores[:], axis=mybir.AxisListType.X, op=ALU.max)
+                nc.scalar.mul(out=shift[:, cols], in_=top[:, cols], mul=-SCALE)
+            for i in range(2):
+                nc.scalar.activation(
+                    out=e_pairs[pair % E_PAIRS][:, i * S : i * S + n_keys],
+                    in_=scores_of[i],
+                    func=ACT.Exp,
+                    bias=shift[:, i : i + 1],
+                    scale=SCALE,
+                    accum_out=rowsum[:, i : i + 1],
+                )
 
         def transpose_e(pair):
             e_words = e_pairs[pair % E_PAIRS][:].bitcast(F32)
@@ -196,12 +209,13 @@ def tile_groupqueryattention_pa_kernel(tc, q, k, v, causal_mask, padding_mask, W
         def attend_values(pair):
             group, second = divmod(pair, 2)
             if second == 0:
-                o_ps_new = psum_o.tile([P, GROUP, P], F32, name="o_ps")
-                o_ps_of[group] = o_ps_new
+                o_sb_new = work.tile([P, GROUP * P], BF16, name="o_sb")
+                o_sb_of[group] = o_sb_new
+            o_ps = psum_b.tile([P, 2, P], F32, tag="bank")
             e_codes, e_scales = e_codes_of[pair]
             for i in range(2):
                 nc.tensor.matmul_mx(
-                    out=o_ps_of[group][:, 2 * second + i, :],
+                    out=o_ps[:, i, :],
                     lhsT=e_codes[:, i * P : (i + 1) * P].bitcast(FP8X4),
                     lhsT_scale=e_scales[:, i * P : (i + 1) * P],
                     rhs=v_codes[:].bitcast(FP8X4),
@@ -209,18 +223,19 @@ def tile_groupqueryattention_pa_kernel(tc, q, k, v, causal_mask, padding_mask, W
                     start=True,
                     stop=True,
                 )
+            o_ps_of[pair] = o_ps
 
-        def normalise(group):
-            recip = stats.tile([P, GROUP], F32)
-            nc.vector.reciprocal(recip[:], rowsum_of[group][:])
-            o_sb = work.tile([P, GROUP * P], BF16)
+        def normalise(pair):
+            group, second = divmod(pair, 2)
+            o_ps = o_ps_of[pair]
+            recip = stats.tile([P, 2], F32)
+            nc.vector.reciprocal(recip[:], rowsum_of[pair][:])
             nc.vector.tensor_tensor(
-                out=o_sb[:].rearrange("p (t d) -> p t d", t=GROUP),
-                in0=o_ps_of[group][:],
-                in1=recip[:].unsqueeze(2).to_broadcast([P, GROUP, P]),
+                out=o_sb_of[group][:, second * 2 * P : (second + 1) * 2 * P].rearrange("p (t d) -> p t d", t=2),
+                in0=o_ps[:],
+                in1=recip[:].unsqueeze(2).to_broadcast([P, 2, P]),
                 op=ALU.mult,
             )
-            o_sb_of[group] = o_sb
 
         def transpose_o(group):
             o_words = o_sb_of[group][:].bitcast(F32)
@@ -290,7 +305,15 @@ def tile_groupqueryattention_pa_kernel(tc, q, k, v, causal_mask, padding_mask, W
 
         transpose_queries(0, 0)
         transpose_queries(0, 1)
+        y_waiting = []
         for step in range(STEPS):
+            if due(step - LAG_ATTEND - 1, PAIRS):
+                normalise(step - LAG_ATTEND - 1)
+            for qt, n_slice, y_ps in y_waiting:
+                add_bias_and_store(qt, n_slice, y_ps)
+            y_waiting = []
+            if step < PAIRS:
+                exponentials(step)
             if due(step - LAG_E_TRANSPOSE, PAIRS):
                 transpose_e(step - LAG_E_TRANSPOSE)
             group, odd = divmod(step - LAG_O_TRANSPOSE, 2)
@@ -301,25 +324,16 @@ def tile_groupqueryattention_pa_kernel(tc, q, k, v, causal_mask, padding_mask, W
             next_qt, steps_into_tile = divmod(step + 2, PAIRS_PER_TILE)
             if steps_into_tile < 2 and due(next_qt - 1, Q_TILES - 1):
                 transpose_queries(next_qt, steps_into_tile)
+            if due(step - LAG_ATTEND, PAIRS):
+                attend_values(step - LAG_ATTEND)
+            for qt in range(Q_TILES):
+                n_slice = step - first_project_step(qt)
+                if due(n_slice, N_SLICES):
+                    y_waiting.append((qt, n_slice, project(qt, n_slice)))
             if due(step - LAG_E_QUANTISE, PAIRS):
                 quantise_e(step - LAG_E_QUANTISE)
-            group, odd = divmod(step - LAG_NORMALISE, 2)
-            if odd == 0 and due(group, ALL_GROUPS):
-                normalise(group)
-            if due(step - WEIGHT_LAG - 1, WEIGHT_UNITS):
-                quantise_weights(step - WEIGHT_LAG - 1)
-            group, odd = divmod(step - LAG_O_TRANSPOSE, 2)
+            if due(step - WEIGHT_QUANTISE_LAG, WEIGHT_UNITS):
+                quantise_weights(step - WEIGHT_QUANTISE_LAG)
+            group, odd = divmod(step - LAG_O_QUANTISE, 2)
             if odd == 0 and due(group, ALL_GROUPS):
                 quantise_o(group)
-            if step < PAIRS:
-                exponentials(step, 0)
-            if due(step - LAG_E_QUANTISE, PAIRS):
-                attend_values(step - LAG_E_QUANTISE)
-            qt, n_slice = divmod(step - PROJECT_LAG, PAIRS_PER_TILE)
-            projecting = due(qt, Q_TILES) and n_slice < N_SLICES
-            if projecting:
-                y_ps = project(qt, n_slice)
-            if step < PAIRS:
-                exponentials(step, 1)
-            if projecting:
-                add_bias_and_store(qt, n_slice, y_ps)

@@ -57,7 +57,6 @@ def tile_groupqueryattention_pa_kernel(tc, q, k, v, causal_mask, padding_mask, W
         work = ctx.enter_context(tc.tile_pool(name="work", bufs=3))
         stats = ctx.enter_context(tc.tile_pool(name="stats", bufs=4))
         psum_b = ctx.enter_context(tc.psum_pool(name="psum_b", bufs=8))
-        ctx.enter_context(tc.manual_schedule())
 
         k_raw = keep.tile([P, Q_TILES, P], BF16)
         nc.sync.dma_start(out=k_raw[:], in_=k[0].rearrange("(t p) d -> p t d", p=P))

@@ -23,31 +23,55 @@ BANK_F32 = 512
 N_SLICES = HID // BANK_F32
 NEG = -1.0e9
 SCALE = 1.0 / math.sqrt(P)
-E_PAIRS = 3
-PAIRS_PER_TILE = HEADS // 2
-PAIRS = Q_TILES * PAIRS_PER_TILE
-ALL_GROUPS = Q_TILES * GROUPS
+SUB = 32
+QUARTERS = P // SUB
+HALF = P // 2
+E_ZEROED = 3
+HEADS_PER_PASS = (4, 2, 1, 1)
+PAIRS_IN_TILE = tuple(HEADS // (2 * n) for n in HEADS_PER_PASS)
+FIRST_PAIR = tuple(sum(PAIRS_IN_TILE[:qt]) for qt in range(Q_TILES))
+PAIRS = sum(PAIRS_IN_TILE)
 WEIGHT_UNITS = N_SLICES * GROUPS
-LAG_E_TRANSPOSE = 2
-LAG_E_QUANTISE = 4
-LAG_ATTEND = 5
-LAG_O_TRANSPOSE = 8
-LAG_O_QUANTISE = 10
+LAG_ATTEND = 2
+LAG_NORMALISE = 3
+LAG_O_QUANTISE = 4
+LAG_PROJECT = 5
 WEIGHT_LAG = 2
-WEIGHT_QUANTISE_LAG = 4
-PROJECT_LAG = 17
-WEIGHTS_READY = 20
-STEPS = (Q_TILES - 1) * PAIRS_PER_TILE + PROJECT_LAG + N_SLICES + 1
+WEIGHT_QUANTISE_LAG = 3
+JOBS_A_STEP = 1
+SCORE_BANKS = 2
+TRANSPOSE_BANKS = 4
+MX_BANKS = 2
+VECTOR_UNITS = 4
+VECTOR_QUERY_TILES = ()
+SCALAR_NORMALISE = ()
+STEPS = PAIRS + LAG_PROJECT + 1
 
 FLOPS = 2 * 2 * HEADS * S * S * P + 2 * S * HID * HID
 
 
-def first_project_step(qt):
-    return max(qt * PAIRS_PER_TILE + PROJECT_LAG, WEIGHTS_READY + qt * N_SLICES)
-
-
 def due(index, count):
     return 0 <= index < count
+
+
+def tile_of_pair(pair):
+    return max(qt for qt in range(Q_TILES) if FIRST_PAIR[qt] <= pair)
+
+
+def heads_of_pass(pair, i):
+    qt = tile_of_pair(pair)
+    n = HEADS_PER_PASS[qt]
+    first = (2 * (pair - FIRST_PAIR[qt]) + i) * n
+    return list(range(first, first + n))
+
+
+def groups_ended(pair):
+    ended = []
+    for i in range(2):
+        for h in heads_of_pass(pair, i):
+            if h % GROUP == GROUP - 1:
+                ended.append((tile_of_pair(pair), h // GROUP))
+    return ended
 
 
 def tile_groupqueryattention_pa_kernel(tc, q, k, v, causal_mask, padding_mask, Wo, bo, out):
@@ -56,7 +80,9 @@ def tile_groupqueryattention_pa_kernel(tc, q, k, v, causal_mask, padding_mask, W
         keep = ctx.enter_context(tc.tile_pool(name="keep", bufs=1))
         work = ctx.enter_context(tc.tile_pool(name="work", bufs=3))
         stats = ctx.enter_context(tc.tile_pool(name="stats", bufs=4))
-        psum_b = ctx.enter_context(tc.psum_pool(name="psum_b", bufs=8))
+        psum_s = ctx.enter_context(tc.psum_pool(name="psum_s", bufs=SCORE_BANKS))
+        psum_t = ctx.enter_context(tc.psum_pool(name="psum_t", bufs=TRANSPOSE_BANKS))
+        psum_x = ctx.enter_context(tc.psum_pool(name="psum_x", bufs=MX_BANKS))
 
         k_raw = keep.tile([P, Q_TILES, P], BF16)
         nc.sync.dma_start(out=k_raw[:], in_=k[0].rearrange("(t p) d -> p t d", p=P))
@@ -68,26 +94,36 @@ def tile_groupqueryattention_pa_kernel(tc, q, k, v, causal_mask, padding_mask, W
         for nt in range(HID // P):
             w_tile = keep.tile([P, HID], BF16, name="wo_raw%d" % nt)
             wo_raw.append(w_tile)
-        nc.sync.dma_start(out=q_raw[0][:], in_=q[0, 0:P, :])
+        for half in range(2):
+            cols = slice(half * HID // 2, (half + 1) * HID // 2)
+            nc.sync.dma_start(out=q_raw[0][:, cols], in_=q[0, 0:P, cols])
         pad_all = keep.tile([P, S], BF16)
         nc.sync.dma_start(out=pad_all[:], in_=padding_mask[0].partition_broadcast(P))
-        causal_raw = []
-        for qt in range(Q_TILES):
-            n_keys = P * (qt + 1)
-            c_tile = keep.tile([P, n_keys], BF16, name="causal_raw%d" % qt)
-            nc.sync.dma_start(out=c_tile[:], in_=causal_mask[0, 0, qt * P : (qt + 1) * P, 0:n_keys])
-            causal_raw.append(c_tile)
-        v_raw = keep.tile([P, 4, P], BF16)
-        nc.sync.dma_start(
-            out=v_raw[:].rearrange("p (u e) d -> p u (e d)", u=2),
-            in_=v[0].rearrange("(u p e) d -> p u (e d)", u=2, e=2),
-        )
+        causal_raw = keep.tile([P, P], BF16)
+        nc.sync.dma_start(out=causal_raw[:], in_=causal_mask[0, 0, 0:P, 0:P])
+        v_raw_of = {}
+        for n in (4, 2, 1):
+            v_raw = keep.tile([P, 4, P], BF16, name="v_raw%d" % n)
+            v_raw_of[n] = v_raw
+
+        def load_v(n):
+            rows = P // n
+            for i in range(n):
+                nc.sync.dma_start(
+                    out=v_raw_of[n][i * rows : (i + 1) * rows].rearrange("p t d -> p (t d)"),
+                    in_=v[0, 0 : 4 * rows].rearrange("(p t) d -> p (t d)", t=4),
+                )
+
+        load_v(4)
+        nc.sync.dma_start(out=q_raw[1][:], in_=q[0, P : 2 * P, :])
+        load_v(2)
+        load_v(1)
         for n_slice in range(N_SLICES):
             for i in range(4):
                 nt = 4 * n_slice + i
                 nc.sync.dma_start(out=wo_raw[nt][:], in_=Wo[nt * P : (nt + 1) * P, :])
-            if n_slice + 1 < Q_TILES:
-                qt = n_slice + 1
+            qt = n_slice + 2
+            if qt < Q_TILES:
                 nc.sync.dma_start(out=q_raw[qt][:], in_=q[0, qt * P : (qt + 1) * P, :])
         bias_all = keep.tile([P, HID], BF16)
         nc.sync.dma_start(out=bias_all[:], in_=bo.partition_broadcast(P))
@@ -96,106 +132,176 @@ def tile_groupqueryattention_pa_kernel(tc, q, k, v, causal_mask, padding_mask, W
         make_identity(nc, ident_bf[:])
         ident_f32 = keep.tile([P, P], F32)
         make_identity(nc, ident_f32[:])
-        e_pairs = []
-        for i in range(E_PAIRS):
-            e_tile = keep.tile([P, 2 * S], BF16, name="e_pair%d" % i)
-            nc.vector.memset(e_tile[:], 0.0)
-            e_pairs.append(e_tile)
+        v_four = keep.tile([P, 4, P, 4], BF16, align_bytes=64)
+        v_two = keep.tile([P, 2, P, 4], BF16, align_bytes=64)
+        v_one = keep.tile([P, 1, P, 4], BF16, align_bytes=64)
+        nc.gpsimd.memset(v_four[:], 0.0)
+        nc.gpsimd.memset(v_two[:], 0.0)
+        e_zeroed = []
+        for i in range(E_ZEROED):
+            e_tile = keep.tile([P, 2 * S], BF16, name="e_zeroed%d" % i)
+            nc.gpsimd.memset(e_tile[:], 0.0)
+            e_zeroed.append(e_tile)
 
         kT = keep.tile([P, S], BF16)
-        kT_ps = psum_b.tile([P, Q_TILES, P], BF16, tag="bank")
+        kT_ps = psum_t.tile([P, Q_TILES, P], BF16, tag="bank")
         for t in range(Q_TILES):
             nc.tensor.transpose(kT_ps[:, t, :], k_raw[:, t, :], ident_bf[:])
-        nc.scalar.copy(out=kT[:], in_=kT_ps[:].rearrange("p t c -> p (t c)"))
+        for u in range(2):
+            nc.vector.tensor_copy(
+                out=kT[:].rearrange("p (t u w e) -> p t u w e", u=2, w=SUB, e=2)[:, :, u],
+                in_=kT_ps[:].rearrange("p t (w u e) -> p t w u e", u=2, e=2)[:, :, :, u, :],
+            )
 
+        pad_neg = keep.tile([P, S], BF16)
+        for u in range(2):
+            nc.vector.tensor_scalar_mul(
+                pad_neg[:].rearrange("p (t u w e) -> p t u w e", u=2, w=SUB, e=2)[:, :, u],
+                pad_all[:].rearrange("p (t w u e) -> p t w u e", t=Q_TILES, u=2, e=2)[:, :, :, u, :],
+                NEG,
+            )
         mask_neg = []
-        for qt in range(Q_TILES):
-            n_keys = P * (qt + 1)
-            m_tile = keep.tile([P, n_keys], BF16, name="mask_neg%d" % qt)
-            nc.vector.tensor_tensor(out=m_tile[:], in0=causal_raw[qt][:], in1=pad_all[:, 0:n_keys], op=ALU.add)
-            nc.vector.tensor_scalar_mul(m_tile[:], m_tile[:], NEG)
+
+        def make_mask(qt):
+            m_tile = keep.tile([P, P * (qt + 1)], BF16, name="mask_neg%d" % qt)
+            for u in range(2):
+                cols = slice(qt * P + u * HALF, qt * P + (u + 1) * HALF)
+                nc.vector.scalar_tensor_tensor(
+                    out=m_tile[:, cols].rearrange("p (w e) -> p w e", e=2),
+                    in0=causal_raw[:].rearrange("p (w u e) -> p w u e", u=2, e=2)[:, :, u, :],
+                    scalar=NEG,
+                    in1=pad_neg[:, cols].rearrange("p (w e) -> p w e", e=2),
+                    op0=ALU.mult,
+                    op1=ALU.add,
+                )
+            if qt > 0:
+                nc.vector.tensor_copy(out=m_tile[:, 0 : qt * P], in_=pad_neg[:, 0 : qt * P])
             mask_neg.append(m_tile)
 
-        v_grouped = keep.tile([P, 4 * P], BF16, align_bytes=64)
-        nc.vector.tensor_copy(
-            out=v_grouped[:].rearrange("p (d t) -> p d t", t=4), in_=v_raw[:].rearrange("p t d -> p d t")
-        )
-        v_codes = keep.tile([P, P], U32, align_bytes=64)
-        v_scales = keep.tile([P, P], U8, align_bytes=64)
-        nc.vector.quantize_mx(out=v_codes[:].bitcast(FP8X4), scales=v_scales[:], in_=v_grouped[:])
+        make_mask(0)
 
+        v_tile_of = {4: v_four, 2: v_two, 1: v_one}
+        v_codes_of = {}
         o_codes = keep.tile([P, GROUPS * S], U32, align_bytes=64)
         o_scales = keep.tile([P, GROUPS * S], U8, align_bytes=64)
         w_codes = keep.tile([P, GROUPS * HID], U32, align_bytes=64)
         w_scales = keep.tile([P, GROUPS * HID], U8, align_bytes=64)
 
         qT_of = {}
+        qT_ps_of = {}
+        scores_of = {}
+        top_of = {}
+        eT_ps_of = {}
+        oT_ps_of = {}
+        wT_ps_of = {}
         rowsum_of = {}
+        e_pair_of = {}
         e_grouped_of = {}
         e_codes_of = {}
-        o_sb_of = {}
         o_ps_of = {}
+        o_sb_of = {}
         o_grouped_of = {}
         w_grouped_of = {}
+
+        def lay_out_v(n):
+            rows = P // n
+            for i in range(n):
+                part = slice(i * rows, (i + 1) * rows)
+                nc.vector.tensor_copy(
+                    out=v_tile_of[n][part, i], in_=v_raw_of[n][part].rearrange("p t d -> p d t")
+                )
+
+        def quantise_v(n):
+            v_codes = keep.tile([P, n * P], U32, align_bytes=64, name="v_codes%d" % n)
+            v_scales = keep.tile([P, n * P], U8, align_bytes=64, name="v_scales%d" % n)
+            nc.vector.quantize_mx(
+                out=v_codes[:].bitcast(FP8X4),
+                scales=v_scales[:],
+                in_=v_tile_of[n][:].rearrange("p n d t -> p (n d t)"),
+            )
+            v_codes_of[n] = (v_codes, v_scales)
 
         def transpose_queries(qt, half):
             if half == 0:
                 qT_new = work.tile([P, HID], BF16, name="qT", bufs=2)
                 qT_of[qt] = qT_new
-            qT_ps = psum_b.tile([P, 8, P], BF16, tag="bank")
+            qT_ps = psum_t.tile([P, 8, P], BF16, tag="bank")
             for i in range(8):
                 h = 8 * half + i
                 nc.tensor.transpose(qT_ps[:, i, :], q_raw[qt][:, h * P : (h + 1) * P], ident_bf[:])
-            nc.scalar.copy(
-                out=qT_of[qt][:, half * 8 * P : (half + 1) * 8 * P], in_=qT_ps[:].rearrange("p i c -> p (i c)")
+            qT_ps_of[qt] = qT_ps
+
+        def copy_queries(qt, half):
+            copy = nc.vector.tensor_copy if qt in VECTOR_QUERY_TILES else nc.scalar.copy
+            copy(
+                out=qT_of[qt][:, half * 8 * P : (half + 1) * 8 * P], in_=qT_ps_of[qt][:].rearrange("p i c -> p (i c)")
             )
 
-        def exponentials(pair):
-            qt, pair_in_tile = divmod(pair, PAIRS_PER_TILE)
+        def score(pair, i):
+            qt = tile_of_pair(pair)
+            n_heads = HEADS_PER_PASS[qt]
             n_keys = P * (qt + 1)
-            heads_per_bank = min(2, BANK_F32 // n_keys)
-            top = stats.tile([P, 2], F32)
-            shift = stats.tile([P, 2], F32)
-            rowsum = stats.tile([P, 2], F32, bufs=8)
-            rowsum_of[pair] = rowsum
-            scores_of = []
-            for first in range(0, 2, heads_per_bank):
-                scores = psum_b.tile([P, heads_per_bank, n_keys], F32, tag="bank")
-                for i in range(heads_per_bank):
-                    h = 2 * pair_in_tile + first + i
-                    nc.tensor.matmul(
-                        scores[:, i, :],
-                        lhsT=qT_of[qt][:, h * P : (h + 1) * P],
-                        rhs=kT[:, 0:n_keys],
-                        start=True,
-                        stop=False,
-                    )
-                    nc.tensor.matmul(scores[:, i, :], lhsT=ident_bf[:], rhs=mask_neg[qt][:], start=False, stop=True)
-                    scores_of.append(scores[:, i, :])
-                cols = slice(first, first + heads_per_bank)
-                nc.vector.tensor_reduce(out=top[:, cols], in_=scores[:], axis=mybir.AxisListType.X, op=ALU.max)
-                nc.scalar.mul(out=shift[:, cols], in_=top[:, cols], mul=-SCALE)
-            for i in range(2):
+            scores = psum_s.tile([P, n_heads, n_keys], F32, tag="scores")
+            for a, h in enumerate(heads_of_pass(pair, i)):
+                nc.tensor.matmul(
+                    scores[:, a, :],
+                    lhsT=qT_of[qt][:, h * P : (h + 1) * P],
+                    rhs=kT[:, 0:n_keys],
+                    start=True,
+                    stop=False,
+                )
+                nc.tensor.matmul(scores[:, a, :], lhsT=ident_bf[:], rhs=mask_neg[qt][:], start=False, stop=True)
+            scores_of[pair, i] = scores
+
+        def row_maxima(pair, i):
+            n_heads = HEADS_PER_PASS[tile_of_pair(pair)]
+            top = stats.tile([P, n_heads], F32, tag="top%d" % n_heads)
+            nc.vector.tensor_reduce(out=top[:], in_=scores_of[pair, i][:], axis=mybir.AxisListType.X, op=ALU.max)
+            top_of[pair, i] = top
+
+        def exponentials(pair, i):
+            qt = tile_of_pair(pair)
+            blocks = qt + 1
+            n_heads = HEADS_PER_PASS[qt]
+            shift = stats.tile([P, n_heads], F32, tag="shift%d" % n_heads)
+            nc.gpsimd.tensor_scalar(
+                out=shift[:], in0=top_of[pair, i][:], scalar1=-SCALE, scalar2=0.0, op0=ALU.mult, op1=ALU.add
+            )
+            if i == 0:
+                if qt == 2:
+                    e_pair = e_zeroed[pair % E_ZEROED]
+                else:
+                    e_pair = work.tile([P, 2 * S], BF16, name="e_pair", bufs=4)
+                e_pair_of[pair] = e_pair
+            e_view = e_pair_of[pair][:].rearrange("p (i u j c) -> p i j u c", i=2, u=2, j=QUARTERS)
+            for a, h in enumerate(heads_of_pass(pair, i)):
+                group = (qt, h // GROUP)
+                if group not in rowsum_of:
+                    rowsum = stats.tile([P, GROUP], F32, bufs=9)
+                    rowsum_of[group] = rowsum
                 nc.scalar.activation(
-                    out=e_pairs[pair % E_PAIRS][:, i * S : i * S + n_keys],
-                    in_=scores_of[i],
+                    out=e_view[:, i, a * blocks : (a + 1) * blocks],
+                    in_=scores_of[pair, i][:, a, :].rearrange("p (j u c) -> p j u c", u=2, c=HALF),
                     func=ACT.Exp,
-                    bias=shift[:, i : i + 1],
+                    bias=shift[:, a : a + 1],
                     scale=SCALE,
-                    accum_out=rowsum[:, i : i + 1],
+                    accum_out=rowsum_of[group][:, h % GROUP : h % GROUP + 1],
                 )
 
         def transpose_e(pair):
-            e_words = e_pairs[pair % E_PAIRS][:].bitcast(F32)
-            eT_ps = psum_b.tile([P, 2, 2, P], F32, tag="bank")
+            e_words = e_pair_of[pair][:].bitcast(F32)
+            eT_ps = psum_t.tile([P, 2, 2, P], F32, tag="bank")
             for i in range(2):
                 for u in range(2):
-                    first_word = i * (S // 2) + u * P
+                    first_word = (2 * i + u) * P
                     nc.tensor.transpose(eT_ps[:, i, u, :], e_words[:, first_word : first_word + P], ident_f32[:])
+            eT_ps_of[pair] = eT_ps
+
+        def copy_e(pair):
             e_grouped = work.tile([P, 2 * P * 4], BF16, align_bytes=64)
             nc.scalar.copy(
                 out=e_grouped[:].bitcast(F32).rearrange("p (i r u) -> p i r u", i=2, u=2),
-                in_=eT_ps[:].rearrange("p i u r -> p i r u"),
+                in_=eT_ps_of[pair][:].rearrange("p i u r -> p i r u"),
             )
             e_grouped_of[pair] = e_grouped
 
@@ -206,15 +312,17 @@ def tile_groupqueryattention_pa_kernel(tc, q, k, v, causal_mask, padding_mask, W
             e_codes_of[pair] = (e_codes, e_scales)
 
         def attend_values(pair):
-            group, second = divmod(pair, 2)
-            if second == 0:
-                o_sb_new = work.tile([P, GROUP * P], BF16, name="o_sb")
-                o_sb_of[group] = o_sb_new
-            o_ps = psum_b.tile([P, 2, P], F32, tag="bank")
+            n_heads = HEADS_PER_PASS[tile_of_pair(pair)]
             e_codes, e_scales = e_codes_of[pair]
+            v_codes, v_scales = v_codes_of[n_heads]
+            per_bank = GROUP if n_heads == GROUP else 2 * n_heads
             for i in range(2):
+                first = (i * n_heads) % per_bank
+                if first == 0:
+                    o_ps = psum_x.tile([P, per_bank, P], F32, tag="mx")
+                    o_ps_of.setdefault(pair, []).append(o_ps)
                 nc.tensor.matmul_mx(
-                    out=o_ps[:, i, :],
+                    out=o_ps[:, first : first + n_heads, :].rearrange("p t d -> p (t d)"),
                     lhsT=e_codes[:, i * P : (i + 1) * P].bitcast(FP8X4),
                     lhsT_scale=e_scales[:, i * P : (i + 1) * P],
                     rhs=v_codes[:].bitcast(FP8X4),
@@ -222,56 +330,79 @@ def tile_groupqueryattention_pa_kernel(tc, q, k, v, causal_mask, padding_mask, W
                     start=True,
                     stop=True,
                 )
-            o_ps_of[pair] = o_ps
 
         def normalise(pair):
-            group, second = divmod(pair, 2)
-            o_ps = o_ps_of[pair]
-            recip = stats.tile([P, 2], F32)
-            nc.vector.reciprocal(recip[:], rowsum_of[pair][:])
-            nc.vector.tensor_tensor(
-                out=o_sb_of[group][:, second * 2 * P : (second + 1) * 2 * P].rearrange("p (t d) -> p t d", t=2),
-                in0=o_ps[:],
-                in1=recip[:].unsqueeze(2).to_broadcast([P, 2, P]),
-                op=ALU.mult,
-            )
+            qt = tile_of_pair(pair)
+            h = heads_of_pass(pair, 0)[0]
+            for o_ps in o_ps_of[pair]:
+                n = o_ps[:].shape[1]
+                group = (qt, h // GROUP)
+                first = h % GROUP
+                if first == 0:
+                    o_sb_new = work.tile([P, GROUP * P], BF16, name="o_sb", bufs=4)
+                    o_sb_of[group] = o_sb_new
+                recip = stats.tile([P, n], F32, tag="recip%d" % n)
+                nc.vector.reciprocal(recip[:], rowsum_of[group][:, first : first + n])
+                if qt in SCALAR_NORMALISE:
+                    for a in range(n):
+                        nc.scalar.activation(
+                            out=o_sb_of[group][:, (first + a) * P : (first + a + 1) * P],
+                            in_=o_ps[:, a, :],
+                            func=ACT.Copy,
+                            scale=recip[:, a : a + 1],
+                        )
+                else:
+                    nc.vector.tensor_tensor(
+                        out=o_sb_of[group][:, first * P : (first + n) * P].rearrange("p (t d) -> p t d", t=n),
+                        in0=o_ps[:],
+                        in1=recip[:].unsqueeze(2).to_broadcast([P, n, P]),
+                        op=ALU.mult,
+                    )
+                h += n
 
         def transpose_o(group):
             o_words = o_sb_of[group][:].bitcast(F32)
-            oT_ps = psum_b.tile([P, 2, P], F32, tag="bank")
+            oT_ps = psum_t.tile([P, 2, P], F32, tag="bank")
             for u in range(2):
                 nc.tensor.transpose(oT_ps[:, u, :], o_words[:, u * P : (u + 1) * P], ident_f32[:])
-            o_grouped = work.tile([P, P * 4], BF16, align_bytes=64)
+            oT_ps_of[group] = oT_ps
+
+        def copy_o(group):
+            o_grouped = work.tile([P, P * 4], BF16, align_bytes=64, bufs=4)
             nc.scalar.copy(
                 out=o_grouped[:].bitcast(F32).rearrange("p (r u) -> p r u", u=2),
-                in_=oT_ps[:].rearrange("p u r -> p r u"),
+                in_=oT_ps_of[group][:].rearrange("p u r -> p r u"),
             )
             o_grouped_of[group] = o_grouped
 
         def quantise_o(group):
-            qt, g = divmod(group, GROUPS)
+            qt, g = group
             cols = slice(g * S + qt * P, g * S + (qt + 1) * P)
             nc.vector.quantize_mx(
                 out=o_codes[:, cols].bitcast(FP8X4), scales=o_scales[:, cols], in_=o_grouped_of[group][:]
             )
 
-        def transpose_weights(unit):
+        def transpose_weights(unit, half):
             n_slice, g = divmod(unit, GROUPS)
-            w_grouped = work.tile([P, BANK_F32 * 4], BF16, align_bytes=64)
-            for half in range(2):
-                wT_ps = psum_b.tile([P, 2, 2, P], F32, tag="bank")
-                for i in range(2):
-                    words = wo_raw[4 * n_slice + 2 * half + i][:].bitcast(F32)
-                    for u in range(2):
-                        first_word = g * 2 * P + u * P
-                        nc.tensor.transpose(wT_ps[:, i, u, :], words[:, first_word : first_word + P], ident_f32[:])
-                nc.scalar.copy(
-                    out=w_grouped[:, half * 1024 : (half + 1) * 1024]
-                    .bitcast(F32)
-                    .rearrange("p (i n u) -> p i n u", i=2, u=2),
-                    in_=wT_ps[:].rearrange("p i u n -> p i n u"),
-                )
-            w_grouped_of[unit] = w_grouped
+            wT_ps = psum_t.tile([P, 2, 2, P], F32, tag="bank")
+            for i in range(2):
+                words = wo_raw[4 * n_slice + 2 * half + i][:].bitcast(F32)
+                for u in range(2):
+                    first_word = g * 2 * P + u * P
+                    nc.tensor.transpose(wT_ps[:, i, u, :], words[:, first_word : first_word + P], ident_f32[:])
+            wT_ps_of[unit, half] = wT_ps
+
+        def copy_weights(unit, half):
+            if half == 0:
+                w_grouped_new = work.tile([P, BANK_F32 * 4], BF16, align_bytes=64, name="w_grouped")
+                w_grouped_of[unit] = w_grouped_new
+            copy = nc.vector.tensor_copy if half == 1 and unit < VECTOR_UNITS else nc.scalar.copy
+            copy(
+                out=w_grouped_of[unit][:, half * 1024 : (half + 1) * 1024]
+                .bitcast(F32)
+                .rearrange("p (i n u) -> p i n u", i=2, u=2),
+                in_=wT_ps_of[unit, half][:].rearrange("p i u n -> p i n u"),
+            )
 
         def quantise_weights(unit):
             n_slice, g = divmod(unit, GROUPS)
@@ -281,7 +412,7 @@ def tile_groupqueryattention_pa_kernel(tc, q, k, v, causal_mask, padding_mask, W
             )
 
         def project(qt, n_slice):
-            y_ps = psum_b.tile([P, BANK_F32], F32, tag="bank")
+            y_ps = psum_x.tile([P, BANK_F32], F32, tag="mx")
             for g in range(GROUPS):
                 o_cols = slice(g * S + qt * P, g * S + (qt + 1) * P)
                 w_cols = slice(g * HID + n_slice * BANK_F32, g * HID + (n_slice + 1) * BANK_F32)
@@ -298,41 +429,73 @@ def tile_groupqueryattention_pa_kernel(tc, q, k, v, causal_mask, padding_mask, W
 
         def add_bias_and_store(qt, n_slice, y_ps):
             n_cols = slice(n_slice * BANK_F32, (n_slice + 1) * BANK_F32)
-            y_sb = work.tile([P, BANK_F32], F32)
+            y_sb = work.tile([P, BANK_F32], F32, bufs=6)
             nc.vector.tensor_tensor(out=y_sb[:], in0=y_ps[:], in1=bias_all[:, n_cols], op=ALU.add)
             nc.sync.dma_start(out=out[0, qt * P : (qt + 1) * P, n_cols], in_=y_sb[:])
 
-        transpose_queries(0, 0)
-        transpose_queries(0, 1)
+        def may_project(qt, n_slice, step):
+            last_pair = FIRST_PAIR[qt] + PAIRS_IN_TILE[qt] - 1
+            last_unit = n_slice * GROUPS + GROUPS - 1
+            return step >= last_pair + LAG_PROJECT and step > last_unit + WEIGHT_QUANTISE_LAG
+
+        to_project = [(qt, n_slice) for qt in range(Q_TILES) for n_slice in range(N_SLICES)]
         y_waiting = []
+        ctx.enter_context(tc.manual_schedule())
+        for half in range(2):
+            transpose_queries(0, half)
+            copy_queries(0, half)
         for step in range(STEPS):
-            if due(step - LAG_ATTEND - 1, PAIRS):
-                normalise(step - LAG_ATTEND - 1)
+            now = due(step, PAIRS)
+            last = due(step - 1, PAIRS)
+            ended = groups_ended(step - LAG_NORMALISE) if due(step - LAG_NORMALISE, PAIRS) else []
+            ended_before = groups_ended(step - LAG_O_QUANTISE) if due(step - LAG_O_QUANTISE, PAIRS) else []
+            unit = step - WEIGHT_LAG
+            if now:
+                score(step, 0)
+                row_maxima(step, 0)
+                exponentials(step, 0)
+            if last:
+                transpose_e(step - 1)
+                copy_e(step - 1)
             for qt, n_slice, y_ps in y_waiting:
                 add_bias_and_store(qt, n_slice, y_ps)
             y_waiting = []
-            if step < PAIRS:
-                exponentials(step)
-            if due(step - LAG_E_TRANSPOSE, PAIRS):
-                transpose_e(step - LAG_E_TRANSPOSE)
-            group, odd = divmod(step - LAG_O_TRANSPOSE, 2)
-            if odd == 0 and due(group, ALL_GROUPS):
+            if due(step - LAG_NORMALISE, PAIRS):
+                normalise(step - LAG_NORMALISE)
+            if due(unit, WEIGHT_UNITS):
+                transpose_weights(unit, 0)
+                copy_weights(unit, 0)
+            if now:
+                score(step, 1)
+                row_maxima(step, 1)
+                exponentials(step, 1)
+            if due(unit, WEIGHT_UNITS):
+                transpose_weights(unit, 1)
+                copy_weights(unit, 1)
+            for group in ended:
                 transpose_o(group)
-            if due(step - WEIGHT_LAG, WEIGHT_UNITS):
-                transpose_weights(step - WEIGHT_LAG)
-            next_qt, steps_into_tile = divmod(step + 2, PAIRS_PER_TILE)
-            if steps_into_tile < 2 and due(next_qt - 1, Q_TILES - 1):
-                transpose_queries(next_qt, steps_into_tile)
+                copy_o(group)
+            for qt in range(1, Q_TILES):
+                half = step - (FIRST_PAIR[qt] - 2)
+                if due(half, 2):
+                    transpose_queries(qt, half)
+                    copy_queries(qt, half)
+            if step < Q_TILES - 1:
+                make_mask(step + 1)
+            if step < 3:
+                lay_out_v((4, 2, 1)[step])
+                quantise_v((4, 2, 1)[step])
+            if last:
+                quantise_e(step - 1)
+            for group in ended_before:
+                quantise_o(group)
+            if due(unit - 1, WEIGHT_UNITS):
+                quantise_weights(unit - 1)
+            ready = [job for job in to_project if may_project(job[0], job[1], step)]
+            for qt, n_slice in ready[0 : 4 if step >= PAIRS + LAG_PROJECT - 1 else JOBS_A_STEP]:
+                to_project.remove((qt, n_slice))
+                y_waiting.append((qt, n_slice, project(qt, n_slice)))
             if due(step - LAG_ATTEND, PAIRS):
                 attend_values(step - LAG_ATTEND)
-            for qt in range(Q_TILES):
-                n_slice = step - first_project_step(qt)
-                if due(n_slice, N_SLICES):
-                    y_waiting.append((qt, n_slice, project(qt, n_slice)))
-            if due(step - LAG_E_QUANTISE, PAIRS):
-                quantise_e(step - LAG_E_QUANTISE)
-            if due(step - WEIGHT_QUANTISE_LAG, WEIGHT_UNITS):
-                quantise_weights(step - WEIGHT_QUANTISE_LAG)
-            group, odd = divmod(step - LAG_O_QUANTISE, 2)
-            if odd == 0 and due(group, ALL_GROUPS):
-                quantise_o(group)
+        for qt, n_slice, y_ps in y_waiting:
+            add_bias_and_store(qt, n_slice, y_ps)

@@ -32,20 +32,21 @@ PAIRS_IN_TILE = tuple(HEADS // (2 * n) for n in HEADS_PER_PASS)
 FIRST_PAIR = tuple(sum(PAIRS_IN_TILE[:qt]) for qt in range(Q_TILES))
 PAIRS = sum(PAIRS_IN_TILE)
 WEIGHT_UNITS = N_SLICES * GROUPS
-LAG_ATTEND = 2
-LAG_NORMALISE = 3
-LAG_O_QUANTISE = 4
-LAG_PROJECT = 5
-WEIGHT_LAG = 2
-WEIGHT_QUANTISE_LAG = 3
+EXP_LAG = 1
+LAG_E = 2
+LAG_ATTEND = 3
+LAG_NORMALISE = 4
+LAG_O = 4
+LAG_PROJECT = 6
+WEIGHT_START = 4
+FAST_START = 99
+FAST_HALVES = 2
 JOBS_A_STEP = 1
-SCORE_BANKS = 2
-TRANSPOSE_BANKS = 4
-MX_BANKS = 2
+SCORE_BANKS = 3
 VECTOR_UNITS = 4
 VECTOR_QUERY_TILES = ()
 SCALAR_NORMALISE = ()
-STEPS = PAIRS + LAG_PROJECT + 1
+STEPS = PAIRS + LAG_O + 2
 
 FLOPS = 2 * 2 * HEADS * S * S * P + 2 * S * HID * HID
 
@@ -67,6 +68,8 @@ def heads_of_pass(pair, i):
 
 def groups_ended(pair):
     ended = []
+    if not due(pair, PAIRS):
+        return ended
     for i in range(2):
         for h in heads_of_pass(pair, i):
             if h % GROUP == GROUP - 1:
@@ -81,8 +84,7 @@ def tile_groupqueryattention_pa_kernel(tc, q, k, v, causal_mask, padding_mask, W
         work = ctx.enter_context(tc.tile_pool(name="work", bufs=3))
         stats = ctx.enter_context(tc.tile_pool(name="stats", bufs=4))
         psum_s = ctx.enter_context(tc.psum_pool(name="psum_s", bufs=SCORE_BANKS))
-        psum_t = ctx.enter_context(tc.psum_pool(name="psum_t", bufs=TRANSPOSE_BANKS))
-        psum_x = ctx.enter_context(tc.psum_pool(name="psum_x", bufs=MX_BANKS))
+        psum_b = ctx.enter_context(tc.psum_pool(name="psum_b", bufs=8 - SCORE_BANKS))
 
         k_raw = keep.tile([P, Q_TILES, P], BF16)
         nc.sync.dma_start(out=k_raw[:], in_=k[0].rearrange("(t p) d -> p t d", p=P))
@@ -144,7 +146,7 @@ def tile_groupqueryattention_pa_kernel(tc, q, k, v, causal_mask, padding_mask, W
             e_zeroed.append(e_tile)
 
         kT = keep.tile([P, S], BF16)
-        kT_ps = psum_t.tile([P, Q_TILES, P], BF16, tag="bank")
+        kT_ps = psum_b.tile([P, Q_TILES, P], BF16, tag="bank")
         for t in range(Q_TILES):
             nc.tensor.transpose(kT_ps[:, t, :], k_raw[:, t, :], ident_bf[:])
         for u in range(2):
@@ -191,6 +193,8 @@ def tile_groupqueryattention_pa_kernel(tc, q, k, v, causal_mask, padding_mask, W
         qT_ps_of = {}
         scores_of = {}
         top_of = {}
+        shift_of = {}
+        recip_of = {}
         eT_ps_of = {}
         oT_ps_of = {}
         wT_ps_of = {}
@@ -225,7 +229,7 @@ def tile_groupqueryattention_pa_kernel(tc, q, k, v, causal_mask, padding_mask, W
             if half == 0:
                 qT_new = work.tile([P, HID], BF16, name="qT", bufs=2)
                 qT_of[qt] = qT_new
-            qT_ps = psum_t.tile([P, 8, P], BF16, tag="bank")
+            qT_ps = psum_b.tile([P, 8, P], BF16, tag="bank")
             for i in range(8):
                 h = 8 * half + i
                 nc.tensor.transpose(qT_ps[:, i, :], q_raw[qt][:, h * P : (h + 1) * P], ident_bf[:])
@@ -259,14 +263,18 @@ def tile_groupqueryattention_pa_kernel(tc, q, k, v, causal_mask, padding_mask, W
             nc.vector.tensor_reduce(out=top[:], in_=scores_of[pair, i][:], axis=mybir.AxisListType.X, op=ALU.max)
             top_of[pair, i] = top
 
-        def exponentials(pair, i):
-            qt = tile_of_pair(pair)
-            blocks = qt + 1
-            n_heads = HEADS_PER_PASS[qt]
+        def scale_maxima(pair, i):
+            n_heads = HEADS_PER_PASS[tile_of_pair(pair)]
             shift = stats.tile([P, n_heads], F32, tag="shift%d" % n_heads)
             nc.gpsimd.tensor_scalar(
                 out=shift[:], in0=top_of[pair, i][:], scalar1=-SCALE, scalar2=0.0, op0=ALU.mult, op1=ALU.add
             )
+            shift_of[pair, i] = shift
+
+        def exponentials(pair, i):
+            qt = tile_of_pair(pair)
+            blocks = qt + 1
+            n_heads = HEADS_PER_PASS[qt]
             if i == 0:
                 if qt == 2:
                     e_pair = e_zeroed[pair % E_ZEROED]
@@ -283,14 +291,14 @@ def tile_groupqueryattention_pa_kernel(tc, q, k, v, causal_mask, padding_mask, W
                     out=e_view[:, i, a * blocks : (a + 1) * blocks],
                     in_=scores_of[pair, i][:, a, :].rearrange("p (j u c) -> p j u c", u=2, c=HALF),
                     func=ACT.Exp,
-                    bias=shift[:, a : a + 1],
+                    bias=shift_of[pair, i][:, a : a + 1],
                     scale=SCALE,
                     accum_out=rowsum_of[group][:, h % GROUP : h % GROUP + 1],
                 )
 
         def transpose_e(pair):
             e_words = e_pair_of[pair][:].bitcast(F32)
-            eT_ps = psum_t.tile([P, 2, 2, P], F32, tag="bank")
+            eT_ps = psum_b.tile([P, 2, 2, P], F32, tag="bank")
             for i in range(2):
                 for u in range(2):
                     first_word = (2 * i + u) * P
@@ -319,7 +327,7 @@ def tile_groupqueryattention_pa_kernel(tc, q, k, v, causal_mask, padding_mask, W
             for i in range(2):
                 first = (i * n_heads) % per_bank
                 if first == 0:
-                    o_ps = psum_x.tile([P, per_bank, P], F32, tag="mx")
+                    o_ps = psum_b.tile([P, per_bank, P], F32, tag="bank")
                     o_ps_of.setdefault(pair, []).append(o_ps)
                 nc.tensor.matmul_mx(
                     out=o_ps[:, first : first + n_heads, :].rearrange("p t d -> p (t d)"),
@@ -331,38 +339,40 @@ def tile_groupqueryattention_pa_kernel(tc, q, k, v, causal_mask, padding_mask, W
                     stop=True,
                 )
 
+        def invert_row_sums(pair):
+            qt = tile_of_pair(pair)
+            h = heads_of_pass(pair, 0)[0]
+            n_heads = 2 * HEADS_PER_PASS[qt]
+            recips = []
+            for first in range(0, n_heads, GROUP):
+                n = min(GROUP, n_heads)
+                col = (h + first) % GROUP
+                recip = stats.tile([P, n], F32, tag="recip%d" % n, bufs=6)
+                nc.vector.reciprocal(recip[:], rowsum_of[qt, (h + first) // GROUP][:, col : col + n])
+                recips.append(recip)
+            recip_of[pair] = recips
+
         def normalise(pair):
             qt = tile_of_pair(pair)
             h = heads_of_pass(pair, 0)[0]
-            for o_ps in o_ps_of[pair]:
+            for o_ps, recip in zip(o_ps_of[pair], recip_of[pair]):
                 n = o_ps[:].shape[1]
                 group = (qt, h // GROUP)
                 first = h % GROUP
                 if first == 0:
                     o_sb_new = work.tile([P, GROUP * P], BF16, name="o_sb", bufs=4)
                     o_sb_of[group] = o_sb_new
-                recip = stats.tile([P, n], F32, tag="recip%d" % n)
-                nc.vector.reciprocal(recip[:], rowsum_of[group][:, first : first + n])
-                if qt in SCALAR_NORMALISE:
-                    for a in range(n):
-                        nc.scalar.activation(
-                            out=o_sb_of[group][:, (first + a) * P : (first + a + 1) * P],
-                            in_=o_ps[:, a, :],
-                            func=ACT.Copy,
-                            scale=recip[:, a : a + 1],
-                        )
-                else:
-                    nc.vector.tensor_tensor(
-                        out=o_sb_of[group][:, first * P : (first + n) * P].rearrange("p (t d) -> p t d", t=n),
-                        in0=o_ps[:],
-                        in1=recip[:].unsqueeze(2).to_broadcast([P, n, P]),
-                        op=ALU.mult,
-                    )
+                nc.vector.tensor_tensor(
+                    out=o_sb_of[group][:, first * P : (first + n) * P].rearrange("p (t d) -> p t d", t=n),
+                    in0=o_ps[:],
+                    in1=recip[:].unsqueeze(2).to_broadcast([P, n, P]),
+                    op=ALU.mult,
+                )
                 h += n
 
         def transpose_o(group):
             o_words = o_sb_of[group][:].bitcast(F32)
-            oT_ps = psum_t.tile([P, 2, P], F32, tag="bank")
+            oT_ps = psum_b.tile([P, 2, P], F32, tag="bank")
             for u in range(2):
                 nc.tensor.transpose(oT_ps[:, u, :], o_words[:, u * P : (u + 1) * P], ident_f32[:])
             oT_ps_of[group] = oT_ps
@@ -384,7 +394,7 @@ def tile_groupqueryattention_pa_kernel(tc, q, k, v, causal_mask, padding_mask, W
 
         def transpose_weights(unit, half):
             n_slice, g = divmod(unit, GROUPS)
-            wT_ps = psum_t.tile([P, 2, 2, P], F32, tag="bank")
+            wT_ps = psum_b.tile([P, 2, 2, P], F32, tag="bank")
             for i in range(2):
                 words = wo_raw[4 * n_slice + 2 * half + i][:].bitcast(F32)
                 for u in range(2):
@@ -394,7 +404,7 @@ def tile_groupqueryattention_pa_kernel(tc, q, k, v, causal_mask, padding_mask, W
 
         def copy_weights(unit, half):
             if half == 0:
-                w_grouped_new = work.tile([P, BANK_F32 * 4], BF16, align_bytes=64, name="w_grouped")
+                w_grouped_new = work.tile([P, BANK_F32 * 4], BF16, align_bytes=64, name="w_grouped", bufs=4)
                 w_grouped_of[unit] = w_grouped_new
             copy = nc.vector.tensor_copy if half == 1 and unit < VECTOR_UNITS else nc.scalar.copy
             copy(
@@ -411,21 +421,18 @@ def tile_groupqueryattention_pa_kernel(tc, q, k, v, causal_mask, padding_mask, W
                 out=w_codes[:, cols].bitcast(FP8X4), scales=w_scales[:, cols], in_=w_grouped_of[unit][:]
             )
 
-        def project(qt, n_slice):
-            y_ps = psum_x.tile([P, BANK_F32], F32, tag="mx")
-            for g in range(GROUPS):
-                o_cols = slice(g * S + qt * P, g * S + (qt + 1) * P)
-                w_cols = slice(g * HID + n_slice * BANK_F32, g * HID + (n_slice + 1) * BANK_F32)
-                nc.tensor.matmul_mx(
-                    out=y_ps[:],
-                    lhsT=o_codes[:, o_cols].bitcast(FP8X4),
-                    lhsT_scale=o_scales[:, o_cols],
-                    rhs=w_codes[:, w_cols].bitcast(FP8X4),
-                    rhs_scale=w_scales[:, w_cols],
-                    start=(g == 0),
-                    stop=(g == GROUPS - 1),
-                )
-            return y_ps
+        def project(qt, n_slice, g, y_ps):
+            o_cols = slice(g * S + qt * P, g * S + (qt + 1) * P)
+            w_cols = slice(g * HID + n_slice * BANK_F32, g * HID + (n_slice + 1) * BANK_F32)
+            nc.tensor.matmul_mx(
+                out=y_ps[:],
+                lhsT=o_codes[:, o_cols].bitcast(FP8X4),
+                lhsT_scale=o_scales[:, o_cols],
+                rhs=w_codes[:, w_cols].bitcast(FP8X4),
+                rhs_scale=w_scales[:, w_cols],
+                start=(g == 0),
+                stop=(g == GROUPS - 1),
+            )
 
         def add_bias_and_store(qt, n_slice, y_ps):
             n_cols = slice(n_slice * BANK_F32, (n_slice + 1) * BANK_F32)
@@ -433,69 +440,97 @@ def tile_groupqueryattention_pa_kernel(tc, q, k, v, causal_mask, padding_mask, W
             nc.vector.tensor_tensor(out=y_sb[:], in0=y_ps[:], in1=bias_all[:, n_cols], op=ALU.add)
             nc.sync.dma_start(out=out[0, qt * P : (qt + 1) * P, n_cols], in_=y_sb[:])
 
+        units_waiting = []
+        units_quantised = []
+
         def may_project(qt, n_slice, step):
             last_pair = FIRST_PAIR[qt] + PAIRS_IN_TILE[qt] - 1
-            last_unit = n_slice * GROUPS + GROUPS - 1
-            return step >= last_pair + LAG_PROJECT and step > last_unit + WEIGHT_QUANTISE_LAG
+            return step >= last_pair + LAG_PROJECT and n_slice * GROUPS + GROUPS - 1 in units_quantised
 
-        to_project = [(qt, n_slice) for qt in range(Q_TILES) for n_slice in range(N_SLICES)]
+        to_project = [(qt, n_slice) for qt in range(Q_TILES - 1) for n_slice in range(N_SLICES)]
         y_waiting = []
         ctx.enter_context(tc.manual_schedule())
         for half in range(2):
             transpose_queries(0, half)
             copy_queries(0, half)
-        for step in range(STEPS):
-            now = due(step, PAIRS)
-            last = due(step - 1, PAIRS)
-            ended = groups_ended(step - LAG_NORMALISE) if due(step - LAG_NORMALISE, PAIRS) else []
-            ended_before = groups_ended(step - LAG_O_QUANTISE) if due(step - LAG_O_QUANTISE, PAIRS) else []
-            unit = step - WEIGHT_LAG
-            if now:
-                score(step, 0)
-                row_maxima(step, 0)
-                exponentials(step, 0)
-            if last:
-                transpose_e(step - 1)
-                copy_e(step - 1)
-            for qt, n_slice, y_ps in y_waiting:
-                add_bias_and_store(qt, n_slice, y_ps)
-            y_waiting = []
-            if due(step - LAG_NORMALISE, PAIRS):
-                normalise(step - LAG_NORMALISE)
-            if due(unit, WEIGHT_UNITS):
-                transpose_weights(unit, 0)
-                copy_weights(unit, 0)
-            if now:
-                score(step, 1)
-                row_maxima(step, 1)
-                exponentials(step, 1)
-            if due(unit, WEIGHT_UNITS):
-                transpose_weights(unit, 1)
-                copy_weights(unit, 1)
-            for group in ended:
-                transpose_o(group)
-                copy_o(group)
-            for qt in range(1, Q_TILES):
-                half = step - (FIRST_PAIR[qt] - 2)
-                if due(half, 2):
-                    transpose_queries(qt, half)
-                    copy_queries(qt, half)
-            if step < Q_TILES - 1:
-                make_mask(step + 1)
-            if step < 3:
-                lay_out_v((4, 2, 1)[step])
-                quantise_v((4, 2, 1)[step])
-            if last:
-                quantise_e(step - 1)
-            for group in ended_before:
-                quantise_o(group)
-            if due(unit - 1, WEIGHT_UNITS):
-                quantise_weights(unit - 1)
-            ready = [job for job in to_project if may_project(job[0], job[1], step)]
-            for qt, n_slice in ready[0 : 4 if step >= PAIRS + LAG_PROJECT - 1 else JOBS_A_STEP]:
-                to_project.remove((qt, n_slice))
-                y_waiting.append((qt, n_slice, project(qt, n_slice)))
-            if due(step - LAG_ATTEND, PAIRS):
-                attend_values(step - LAG_ATTEND)
-        for qt, n_slice, y_ps in y_waiting:
-            add_bias_and_store(qt, n_slice, y_ps)
+        def staged(stage, pair):
+            if due(pair, PAIRS):
+                stage(pair)
+
+        last_tile = Q_TILES - 1
+        last_y = []
+        halves_done = 0
+        for tick in range(2 * STEPS):
+            step, i = divmod(tick, 2)
+            if step < PAIRS:
+                score(step, i)
+                row_maxima(step, i)
+            before = tick - EXP_LAG
+            if due(before // 2, PAIRS):
+                exponentials(before // 2, before % 2)
+            if i == 0:
+                staged(transpose_e, step - LAG_E)
+                staged(copy_e, step - LAG_E)
+            halves = 0 if tick < WEIGHT_START else (1 if tick < FAST_START else FAST_HALVES)
+            units_ended = []
+            for half_unit in range(halves_done, min(halves_done + halves, 2 * WEIGHT_UNITS)):
+                unit, half = divmod(half_unit, 2)
+                transpose_weights(unit, half)
+                copy_weights(unit, half)
+                halves_done += 1
+                if half == 1:
+                    units_ended.append(unit)
+            if i == 0:
+                for qt, n_slice, y_ps in y_waiting:
+                    add_bias_and_store(qt, n_slice, y_ps)
+                y_waiting = []
+                staged(normalise, step - LAG_NORMALISE)
+            else:
+                for group in groups_ended(step - LAG_O):
+                    transpose_o(group)
+                    copy_o(group)
+                for qt in range(1, Q_TILES):
+                    half = step - (FIRST_PAIR[qt] - 2)
+                    if due(half, 2):
+                        transpose_queries(qt, half)
+                        copy_queries(qt, half)
+                if step < Q_TILES - 1:
+                    make_mask(step + 1)
+                if step < 3:
+                    lay_out_v((4, 2, 1)[step])
+                    quantise_v((4, 2, 1)[step])
+                staged(quantise_e, step - LAG_E)
+                staged(invert_row_sums, step - LAG_E)
+            for unit in units_waiting:
+                quantise_weights(unit)
+                units_quantised.append(unit)
+            units_waiting = units_ended
+            if i == 0:
+                for group in groups_ended(step - LAG_O - 1):
+                    quantise_o(group)
+            else:
+                staged(attend_values, step - LAG_ATTEND)
+                jobs = [job for job in to_project if may_project(job[0], job[1], step)]
+                for qt, n_slice in jobs[0:JOBS_A_STEP]:
+                    to_project.remove((qt, n_slice))
+                    y_ps = psum_b.tile([P, BANK_F32], F32, tag="bank")
+                    for g in range(GROUPS):
+                        project(qt, n_slice, g, y_ps)
+                    y_waiting.append((qt, n_slice, y_ps))
+            if step < PAIRS:
+                scale_maxima(step, i)
+            if step == PAIRS and i == 1:
+                for n_slice in range(N_SLICES):
+                    if n_slice < SCORE_BANKS:
+                        y_ps = psum_s.tile([P, BANK_F32], F32, name="last_y", tag="scores")
+                    else:
+                        y_ps = psum_b.tile([P, BANK_F32], F32, name="last_y", tag="bank")
+                    last_y.append(y_ps)
+            g = step - PAIRS
+            if i == 1 and due(g, GROUPS - 1):
+                for n_slice in range(N_SLICES):
+                    project(last_tile, n_slice, g, last_y[n_slice])
+        for n_slice in range(N_SLICES):
+            project(last_tile, n_slice, GROUPS - 1, last_y[n_slice])
+        for n_slice in range(N_SLICES):
+            add_bias_and_store(last_tile, n_slice, last_y[n_slice])

@@ -32,6 +32,7 @@ PAIRS_IN_TILE = tuple(HEADS // (2 * n) for n in HEADS_PER_PASS)
 FIRST_PAIR = tuple(sum(PAIRS_IN_TILE[:qt]) for qt in range(Q_TILES))
 PAIRS = sum(PAIRS_IN_TILE)
 WEIGHT_UNITS = N_SLICES * GROUPS
+PREPARE_A_TICK = 2
 EXP_LAG = 1
 LAG_E = 2
 LAG_ATTEND = 3
@@ -207,13 +208,9 @@ def tile_groupqueryattention_pa_kernel(tc, q, k, v, causal_mask, padding_mask, W
         o_grouped_of = {}
         w_grouped_of = {}
 
-        def lay_out_v(n):
-            rows = P // n
-            for i in range(n):
-                part = slice(i * rows, (i + 1) * rows)
-                nc.vector.tensor_copy(
-                    out=v_tile_of[n][part, i], in_=v_raw_of[n][part].rearrange("p t d -> p d t")
-                )
+        def lay_out_v(n, head):
+            part = slice(head * P // n, (head + 1) * P // n)
+            nc.vector.tensor_copy(out=v_tile_of[n][part, head], in_=v_raw_of[n][part].rearrange("p t d -> p d t"))
 
         def quantise_v(n):
             v_codes = keep.tile([P, n * P], U32, align_bytes=64, name="v_codes%d" % n)
@@ -457,11 +454,20 @@ def tile_groupqueryattention_pa_kernel(tc, q, k, v, causal_mask, padding_mask, W
             if due(pair, PAIRS):
                 stage(pair)
 
+        preparations = [(make_mask, (1,))]
+        for qt, n in enumerate((4, 2, 1)):
+            preparations += [(lay_out_v, (n, head)) for head in range(n)] + [(quantise_v, (n,))]
+            if qt > 0:
+                preparations.append((make_mask, (qt + 1,)))
         last_tile = Q_TILES - 1
         last_y = []
         halves_done = 0
         for tick in range(2 * STEPS):
             step, i = divmod(tick, 2)
+            for prepare, argument in preparations[tick * PREPARE_A_TICK : (tick + 1) * PREPARE_A_TICK]:
+                prepare(*argument)
+            if i == 0:
+                staged(normalise, step - LAG_NORMALISE)
             if step < PAIRS:
                 score(step, i)
                 row_maxima(step, i)
@@ -484,7 +490,6 @@ def tile_groupqueryattention_pa_kernel(tc, q, k, v, causal_mask, padding_mask, W
                 for qt, n_slice, y_ps in y_waiting:
                     add_bias_and_store(qt, n_slice, y_ps)
                 y_waiting = []
-                staged(normalise, step - LAG_NORMALISE)
             else:
                 for group in groups_ended(step - LAG_O):
                     transpose_o(group)
@@ -494,11 +499,6 @@ def tile_groupqueryattention_pa_kernel(tc, q, k, v, causal_mask, padding_mask, W
                     if due(half, 2):
                         transpose_queries(qt, half)
                         copy_queries(qt, half)
-                if step < Q_TILES - 1:
-                    make_mask(step + 1)
-                if step < 3:
-                    lay_out_v((4, 2, 1)[step])
-                    quantise_v((4, 2, 1)[step])
                 staged(quantise_e, step - LAG_E)
                 staged(invert_row_sums, step - LAG_E)
             for unit in units_waiting:

@@ -40,14 +40,12 @@ LAG_NORMALISE = 4
 LAG_O = 4
 LAG_PROJECT = 6
 WEIGHT_START = 4
-FAST_START = 99
-FAST_HALVES = 2
+TAIL_EARLY = 1
 JOBS_A_STEP = 1
 SCORE_BANKS = 3
 VECTOR_UNITS = 4
 VECTOR_QUERY_TILES = ()
 SCALAR_NORMALISE = ()
-STEPS = PAIRS + LAG_O + 2
 
 FLOPS = 2 * 2 * HEADS * S * S * P + 2 * S * HID * HID
 
@@ -65,6 +63,15 @@ def heads_of_pass(pair, i):
     n = HEADS_PER_PASS[qt]
     first = (2 * (pair - FIRST_PAIR[qt]) + i) * n
     return list(range(first, first + n))
+
+
+def heads_of_bank(pair, i):
+    n = HEADS_PER_PASS[tile_of_pair(pair)]
+    first = heads_of_pass(pair, 0)[0]
+    if n == 1:
+        return [(first + i, i, 0)]
+    slots = range(i * n // 2, (i + 1) * n // 2)
+    return [(first + turn * n + slot, turn, slot) for slot in slots for turn in range(2)]
 
 
 def groups_ended(pair):
@@ -240,10 +247,10 @@ def tile_groupqueryattention_pa_kernel(tc, q, k, v, causal_mask, padding_mask, W
 
         def score(pair, i):
             qt = tile_of_pair(pair)
-            n_heads = HEADS_PER_PASS[qt]
             n_keys = P * (qt + 1)
-            scores = psum_s.tile([P, n_heads, n_keys], F32, tag="scores")
-            for a, h in enumerate(heads_of_pass(pair, i)):
+            heads = heads_of_bank(pair, i)
+            scores = psum_s.tile([P, len(heads), n_keys], F32, tag="scores")
+            for a, (h, turn, slot) in enumerate(heads):
                 nc.tensor.matmul(
                     scores[:, a, :],
                     lhsT=qT_of[qt][:, h * P : (h + 1) * P],
@@ -255,14 +262,14 @@ def tile_groupqueryattention_pa_kernel(tc, q, k, v, causal_mask, padding_mask, W
             scores_of[pair, i] = scores
 
         def row_maxima(pair, i):
-            n_heads = HEADS_PER_PASS[tile_of_pair(pair)]
-            top = stats.tile([P, n_heads], F32, tag="top%d" % n_heads)
+            n = len(heads_of_bank(pair, i))
+            top = stats.tile([P, n], F32, tag="top%d" % n)
             nc.vector.tensor_reduce(out=top[:], in_=scores_of[pair, i][:], axis=mybir.AxisListType.X, op=ALU.max)
             top_of[pair, i] = top
 
         def scale_maxima(pair, i):
-            n_heads = HEADS_PER_PASS[tile_of_pair(pair)]
-            shift = stats.tile([P, n_heads], F32, tag="shift%d" % n_heads)
+            n = len(heads_of_bank(pair, i))
+            shift = stats.tile([P, n], F32, tag="shift%d" % n)
             nc.gpsimd.tensor_scalar(
                 out=shift[:], in0=top_of[pair, i][:], scalar1=-SCALE, scalar2=0.0, op0=ALU.mult, op1=ALU.add
             )
@@ -271,7 +278,6 @@ def tile_groupqueryattention_pa_kernel(tc, q, k, v, causal_mask, padding_mask, W
         def exponentials(pair, i):
             qt = tile_of_pair(pair)
             blocks = qt + 1
-            n_heads = HEADS_PER_PASS[qt]
             if i == 0:
                 if qt == 2:
                     e_pair = e_zeroed[pair % E_ZEROED]
@@ -279,13 +285,13 @@ def tile_groupqueryattention_pa_kernel(tc, q, k, v, causal_mask, padding_mask, W
                     e_pair = work.tile([P, 2 * S], BF16, name="e_pair", bufs=4)
                 e_pair_of[pair] = e_pair
             e_view = e_pair_of[pair][:].rearrange("p (i u j c) -> p i j u c", i=2, u=2, j=QUARTERS)
-            for a, h in enumerate(heads_of_pass(pair, i)):
+            for a, (h, turn, slot) in enumerate(heads_of_bank(pair, i)):
                 group = (qt, h // GROUP)
                 if group not in rowsum_of:
                     rowsum = stats.tile([P, GROUP], F32, bufs=9)
                     rowsum_of[group] = rowsum
                 nc.scalar.activation(
-                    out=e_view[:, i, a * blocks : (a + 1) * blocks],
+                    out=e_view[:, turn, slot * blocks : (slot + 1) * blocks],
                     in_=scores_of[pair, i][:, a, :].rearrange("p (j u c) -> p j u c", u=2, c=HALF),
                     func=ACT.Exp,
                     bias=shift_of[pair, i][:, a : a + 1],
@@ -431,6 +437,12 @@ def tile_groupqueryattention_pa_kernel(tc, q, k, v, causal_mask, padding_mask, W
                 stop=(g == GROUPS - 1),
             )
 
+        def project_slice(qt, n_slice):
+            y_ps = psum_b.tile([P, BANK_F32], F32, tag="bank")
+            for g in range(GROUPS):
+                project(qt, n_slice, g, y_ps)
+            return y_ps
+
         def add_bias_and_store(qt, n_slice, y_ps):
             n_cols = slice(n_slice * BANK_F32, (n_slice + 1) * BANK_F32)
             y_sb = work.tile([P, BANK_F32], F32, bufs=6)
@@ -459,25 +471,22 @@ def tile_groupqueryattention_pa_kernel(tc, q, k, v, causal_mask, padding_mask, W
             preparations += [(lay_out_v, (n, head)) for head in range(n)] + [(quantise_v, (n,))]
             if qt > 0:
                 preparations.append((make_mask, (qt + 1,)))
-        last_tile = Q_TILES - 1
-        last_y = []
         halves_done = 0
-        for tick in range(2 * STEPS):
+        for tick in range(2 * PAIRS):
             step, i = divmod(tick, 2)
             for prepare, argument in preparations[tick * PREPARE_A_TICK : (tick + 1) * PREPARE_A_TICK]:
                 prepare(*argument)
             if i == 0:
                 staged(normalise, step - LAG_NORMALISE)
-            if step < PAIRS:
-                score(step, i)
-                row_maxima(step, i)
+            score(step, i)
+            row_maxima(step, i)
             before = tick - EXP_LAG
-            if due(before // 2, PAIRS):
+            if before >= 0:
                 exponentials(before // 2, before % 2)
             if i == 0:
                 staged(transpose_e, step - LAG_E)
                 staged(copy_e, step - LAG_E)
-            halves = 0 if tick < WEIGHT_START else (1 if tick < FAST_START else FAST_HALVES)
+            halves = 0 if tick < WEIGHT_START else 1
             units_ended = []
             for half_unit in range(halves_done, min(halves_done + halves, 2 * WEIGHT_UNITS)):
                 unit, half = divmod(half_unit, 2)
@@ -513,24 +522,59 @@ def tile_groupqueryattention_pa_kernel(tc, q, k, v, causal_mask, padding_mask, W
                 jobs = [job for job in to_project if may_project(job[0], job[1], step)]
                 for qt, n_slice in jobs[0:JOBS_A_STEP]:
                     to_project.remove((qt, n_slice))
-                    y_ps = psum_b.tile([P, BANK_F32], F32, tag="bank")
-                    for g in range(GROUPS):
-                        project(qt, n_slice, g, y_ps)
-                    y_waiting.append((qt, n_slice, y_ps))
-            if step < PAIRS:
-                scale_maxima(step, i)
-            if step == PAIRS and i == 1:
-                for n_slice in range(N_SLICES):
-                    if n_slice < SCORE_BANKS:
-                        y_ps = psum_s.tile([P, BANK_F32], F32, name="last_y", tag="scores")
-                    else:
-                        y_ps = psum_b.tile([P, BANK_F32], F32, name="last_y", tag="bank")
-                    last_y.append(y_ps)
-            g = step - PAIRS
-            if i == 1 and due(g, GROUPS - 1):
-                for n_slice in range(N_SLICES):
-                    project(last_tile, n_slice, g, last_y[n_slice])
+                    y_waiting.append((qt, n_slice, project_slice(qt, n_slice)))
+            scale_maxima(step, i)
+
+        last = PAIRS - 1
+        last_tile = Q_TILES - 1
+        normalise(last - 3)
+        exponentials(last, 1)
+        transpose_e(last - 1)
+        copy_e(last - 1)
+        attend_values(last - 2)
+        for qt, n_slice, y_ps in y_waiting:
+            add_bias_and_store(qt, n_slice, y_ps)
+        y_waiting = []
+        quantise_e(last - 1)
+        invert_row_sums(last - 1)
+        for group in groups_ended(last - 4):
+            quantise_o(group)
+        for qt, n_slice in to_project[0:1]:
+            y_waiting.append((qt, n_slice, project_slice(qt, n_slice)))
+        transpose_e(last)
+        copy_e(last)
+        normalise(last - 2)
+        quantise_e(last)
+        invert_row_sums(last)
+        attend_values(last - 1)
+        for group in groups_ended(last - 2):
+            transpose_o(group)
+            copy_o(group)
+        for qt, n_slice in to_project[1:]:
+            y_waiting.append((qt, n_slice, project_slice(qt, n_slice)))
+        attend_values(last)
+        for group in groups_ended(last - 2):
+            quantise_o(group)
+        normalise(last - 1)
+        normalise(last)
+        for qt, n_slice, y_ps in y_waiting:
+            add_bias_and_store(qt, n_slice, y_ps)
+        last_y = []
         for n_slice in range(N_SLICES):
-            project(last_tile, n_slice, GROUPS - 1, last_y[n_slice])
+            if n_slice < SCORE_BANKS:
+                y_ps = psum_s.tile([P, BANK_F32], F32, name="last_y", tag="scores")
+            else:
+                y_ps = psum_b.tile([P, BANK_F32], F32, name="last_y", tag="bank")
+            last_y.append(y_ps)
+        for g in range(TAIL_EARLY):
+            for n_slice in range(N_SLICES):
+                project(last_tile, n_slice, g, last_y[n_slice])
+        for group in groups_ended(last):
+            transpose_o(group)
+            copy_o(group)
+            quantise_o(group)
+        for g in range(TAIL_EARLY, GROUPS):
+            for n_slice in range(N_SLICES):
+                project(last_tile, n_slice, g, last_y[n_slice])
         for n_slice in range(N_SLICES):
             add_bias_and_store(last_tile, n_slice, last_y[n_slice])

@@ -95,7 +95,7 @@ def tile_groupqueryattention_pa_kernel(tc, q, k, v, causal_mask, padding_mask, W
         psum_b = ctx.enter_context(tc.psum_pool(name="psum_b", bufs=8 - SCORE_BANKS))
 
         k_raw = keep.tile([P, Q_TILES, P], BF16)
-        nc.sync.dma_start(out=k_raw[:], in_=k[0].rearrange("(t p) d -> p t d", p=P))
+        nc.sync.dma_start(out=k_raw[:, 0, :], in_=k[0, 0:P, :])
         q_raw = []
         for qt in range(Q_TILES):
             q_tile = keep.tile([P, HID], BF16, name="q_raw%d" % qt)
@@ -104,13 +104,13 @@ def tile_groupqueryattention_pa_kernel(tc, q, k, v, causal_mask, padding_mask, W
         for nt in range(HID // P):
             w_tile = keep.tile([P, HID], BF16, name="wo_raw%d" % nt)
             wo_raw.append(w_tile)
-        for half in range(2):
-            cols = slice(half * HID // 2, (half + 1) * HID // 2)
-            nc.sync.dma_start(out=q_raw[0][:, cols], in_=q[0, 0:P, cols])
+        nc.sync.dma_start(out=q_raw[0][:, 0 : HID // 2], in_=q[0, 0:P, 0 : HID // 2])
         pad_all = keep.tile([P, S], BF16)
         nc.sync.dma_start(out=pad_all[:], in_=padding_mask[0].partition_broadcast(P))
         causal_raw = keep.tile([P, P], BF16)
         nc.sync.dma_start(out=causal_raw[:], in_=causal_mask[0, 0, 0:P, 0:P])
+        nc.sync.dma_start(out=k_raw[:, 1:, :], in_=k[0, P:, :].rearrange("(t p) d -> p t d", p=P))
+        nc.sync.dma_start(out=q_raw[0][:, HID // 2 :], in_=q[0, 0:P, HID // 2 :])
         v_raw_of = {}
         for n in (4, 2, 1):
             v_raw = keep.tile([P, 4, P], BF16, name="v_raw%d" % n)
@@ -142,56 +142,58 @@ def tile_groupqueryattention_pa_kernel(tc, q, k, v, causal_mask, padding_mask, W
         make_identity(nc, ident_bf[:])
         ident_f32 = keep.tile([P, P], F32)
         make_identity(nc, ident_f32[:])
-        v_four = keep.tile([P, 4, P, 4], BF16, align_bytes=64)
-        v_two = keep.tile([P, 2, P, 4], BF16, align_bytes=64)
-        v_one = keep.tile([P, 1, P, 4], BF16, align_bytes=64)
-        nc.gpsimd.memset(v_four[:], 0.0)
-        nc.gpsimd.memset(v_two[:], 0.0)
+        v_codes_of = {}
+        for n in (4, 2, 1):
+            v_codes = keep.tile([P, n * P], U32, align_bytes=64, name="v_codes%d" % n)
+            if n > 1:
+                nc.vector.memset(v_codes[:], 0)
+            v_codes_of[n] = v_codes
         e_zeroed = []
         for i in range(E_ZEROED):
             e_tile = keep.tile([P, 2 * S], BF16, name="e_zeroed%d" % i)
-            nc.gpsimd.memset(e_tile[:], 0.0)
+            nc.vector.memset(e_tile[:].bitcast(F32), 0.0)
             e_zeroed.append(e_tile)
 
         kT = keep.tile([P, S], BF16)
-        kT_ps = psum_b.tile([P, Q_TILES, P], BF16, tag="bank")
-        for t in range(Q_TILES):
-            nc.tensor.transpose(kT_ps[:, t, :], k_raw[:, t, :], ident_bf[:])
-        for u in range(2):
-            nc.vector.tensor_copy(
-                out=kT[:].rearrange("p (t u w e) -> p t u w e", u=2, w=SUB, e=2)[:, :, u],
-                in_=kT_ps[:].rearrange("p t (w u e) -> p t w u e", u=2, e=2)[:, :, :, u, :],
-            )
 
-        pad_neg = keep.tile([P, S], BF16)
-        for u in range(2):
-            nc.vector.tensor_scalar_mul(
-                pad_neg[:].rearrange("p (t u w e) -> p t u w e", u=2, w=SUB, e=2)[:, :, u],
-                pad_all[:].rearrange("p (t w u e) -> p t w u e", t=Q_TILES, u=2, e=2)[:, :, :, u, :],
-                NEG,
-            )
-        mask_neg = []
+        def half_block(ap, first, end, u):
+            return ap.rearrange("p (t u w e) -> p t u w e", u=2, w=SUB, e=2)[:, first:end, u]
 
-        def make_mask(qt):
-            m_tile = keep.tile([P, P * (qt + 1)], BF16, name="mask_neg%d" % qt)
+        def half_read(ap, first, end, u):
+            return ap.rearrange("p (t w u e) -> p t w u e", w=SUB, u=2, e=2)[:, first:end, :, u, :]
+
+        def transpose_keys(first, end):
+            kT_ps = psum_b.tile([P, Q_TILES, P], BF16, tag="bank")
+            for t in range(first, end):
+                nc.tensor.transpose(kT_ps[:, t, :], k_raw[:, t, :], ident_bf[:])
+            kT_cols = kT_ps[:].rearrange("p t c -> p (t c)")
             for u in range(2):
-                cols = slice(qt * P + u * HALF, qt * P + (u + 1) * HALF)
-                nc.vector.scalar_tensor_tensor(
-                    out=m_tile[:, cols].rearrange("p (w e) -> p w e", e=2),
-                    in0=causal_raw[:].rearrange("p (w u e) -> p w u e", u=2, e=2)[:, :, u, :],
-                    scalar=NEG,
-                    in1=pad_neg[:, cols].rearrange("p (w e) -> p w e", e=2),
-                    op0=ALU.mult,
-                    op1=ALU.add,
+                nc.vector.tensor_copy(
+                    out=half_block(kT[:], first, end, u), in_=half_read(kT_cols, first, end, u)
                 )
-            if qt > 0:
-                nc.vector.tensor_copy(out=m_tile[:, 0 : qt * P], in_=pad_neg[:, 0 : qt * P])
-            mask_neg.append(m_tile)
 
-        make_mask(0)
+        diagonal_neg = keep.tile([P, S], BF16)
+        pad_neg = keep.tile([P, S], BF16)
 
-        v_tile_of = {4: v_four, 2: v_two, 1: v_one}
-        v_codes_of = {}
+        def make_diagonal_masks():
+            for u in range(2):
+                nc.vector.tensor_tensor(
+                    out=half_block(diagonal_neg[:], 0, Q_TILES, u),
+                    in0=half_read(causal_raw[:], 0, 1, u).to_broadcast([P, Q_TILES, SUB, 2]),
+                    in1=half_read(pad_all[:], 0, Q_TILES, u),
+                    op=ALU.add,
+                )
+            nc.vector.tensor_scalar_mul(diagonal_neg[:], diagonal_neg[:], NEG)
+
+        def make_padding_mask():
+            for u in range(2):
+                nc.vector.tensor_scalar_mul(
+                    half_block(pad_neg[:], 0, Q_TILES, u), half_read(pad_all[:], 0, Q_TILES, u), NEG
+                )
+
+        v_scales_of = {}
+        v_grouped_of = {}
+        v_dense_of = {}
         o_codes = keep.tile([P, GROUPS * S], U32, align_bytes=64)
         o_scales = keep.tile([P, GROUPS * S], U8, align_bytes=64)
         w_codes = keep.tile([P, GROUPS * HID], U32, align_bytes=64)
@@ -215,19 +217,28 @@ def tile_groupqueryattention_pa_kernel(tc, q, k, v, causal_mask, padding_mask, W
         o_grouped_of = {}
         w_grouped_of = {}
 
-        def lay_out_v(n, head):
-            part = slice(head * P // n, (head + 1) * P // n)
-            nc.vector.tensor_copy(out=v_tile_of[n][part, head], in_=v_raw_of[n][part].rearrange("p t d -> p d t"))
+        def group_v(n):
+            v_grouped = work.tile([P, P * 4], BF16, align_bytes=64, bufs=2)
+            nc.vector.tensor_copy(
+                out=v_grouped[:].rearrange("p (d t) -> p d t", t=4), in_=v_raw_of[n][:].rearrange("p t d -> p d t")
+            )
+            v_grouped_of[n] = v_grouped
 
         def quantise_v(n):
-            v_codes = keep.tile([P, n * P], U32, align_bytes=64, name="v_codes%d" % n)
-            v_scales = keep.tile([P, n * P], U8, align_bytes=64, name="v_scales%d" % n)
-            nc.vector.quantize_mx(
-                out=v_codes[:].bitcast(FP8X4),
-                scales=v_scales[:],
-                in_=v_tile_of[n][:].rearrange("p n d t -> p (n d t)"),
-            )
-            v_codes_of[n] = (v_codes, v_scales)
+            v_scales = keep.tile([P, P], U8, align_bytes=64, name="v_scales%d" % n)
+            v_dense = v_codes_of[1]
+            if n > 1:
+                v_dense = keep.tile([P, P], U32, align_bytes=64, name="v_dense%d" % n)
+            nc.vector.quantize_mx(out=v_dense[:].bitcast(FP8X4), scales=v_scales[:], in_=v_grouped_of[n][:])
+            v_scales_of[n] = v_scales
+            v_dense_of[n] = v_dense
+
+        def spread_v(n):
+            for head in range(n):
+                part = slice(head * P // n, (head + 1) * P // n)
+                nc.vector.tensor_copy(
+                    out=v_codes_of[n][part, head * P : (head + 1) * P], in_=v_dense_of[n][part]
+                )
 
         def transpose_queries(qt, half):
             if half == 0:
@@ -258,7 +269,18 @@ def tile_groupqueryattention_pa_kernel(tc, q, k, v, causal_mask, padding_mask, W
                     start=True,
                     stop=False,
                 )
-                nc.tensor.matmul(scores[:, a, :], lhsT=ident_bf[:], rhs=mask_neg[qt][:], start=False, stop=True)
+                if qt > 0:
+                    left = qt * P
+                    nc.tensor.matmul(
+                        scores[:, a, 0:left], lhsT=ident_bf[:], rhs=pad_neg[:, 0:left], start=False, stop=False
+                    )
+                nc.tensor.matmul(
+                    scores[:, a, qt * P :],
+                    lhsT=ident_bf[:],
+                    rhs=diagonal_neg[:, qt * P : (qt + 1) * P],
+                    start=False,
+                    stop=True,
+                )
             scores_of[pair, i] = scores
 
         def row_maxima(pair, i):
@@ -325,22 +347,23 @@ def tile_groupqueryattention_pa_kernel(tc, q, k, v, causal_mask, padding_mask, W
         def attend_values(pair):
             n_heads = HEADS_PER_PASS[tile_of_pair(pair)]
             e_codes, e_scales = e_codes_of[pair]
-            v_codes, v_scales = v_codes_of[n_heads]
+            v_codes, v_scales = v_codes_of[n_heads], v_scales_of[n_heads]
             per_bank = GROUP if n_heads == GROUP else 2 * n_heads
             for i in range(2):
                 first = (i * n_heads) % per_bank
                 if first == 0:
                     o_ps = psum_b.tile([P, per_bank, P], F32, tag="bank")
                     o_ps_of.setdefault(pair, []).append(o_ps)
-                nc.tensor.matmul_mx(
-                    out=o_ps[:, first : first + n_heads, :].rearrange("p t d -> p (t d)"),
-                    lhsT=e_codes[:, i * P : (i + 1) * P].bitcast(FP8X4),
-                    lhsT_scale=e_scales[:, i * P : (i + 1) * P],
-                    rhs=v_codes[:].bitcast(FP8X4),
-                    rhs_scale=v_scales[:],
-                    start=True,
-                    stop=True,
-                )
+                for a in range(n_heads):
+                    nc.tensor.matmul_mx(
+                        out=o_ps[:, first + a, :],
+                        lhsT=e_codes[:, i * P : (i + 1) * P].bitcast(FP8X4),
+                        lhsT_scale=e_scales[:, i * P : (i + 1) * P],
+                        rhs=v_codes[:, a * P : (a + 1) * P].bitcast(FP8X4),
+                        rhs_scale=v_scales[:],
+                        start=True,
+                        stop=True,
+                    )
 
         def invert_row_sums(pair):
             qt = tile_of_pair(pair)
@@ -459,18 +482,21 @@ def tile_groupqueryattention_pa_kernel(tc, q, k, v, causal_mask, padding_mask, W
         to_project = [(qt, n_slice) for qt in range(Q_TILES - 1) for n_slice in range(N_SLICES)]
         y_waiting = []
         ctx.enter_context(tc.manual_schedule())
-        for half in range(2):
-            transpose_queries(0, half)
-            copy_queries(0, half)
+        transpose_keys(0, 1)
+        transpose_queries(0, 0)
+        copy_queries(0, 0)
+        transpose_queries(0, 1)
+        copy_queries(0, 1)
+        make_diagonal_masks()
         def staged(stage, pair):
             if due(pair, PAIRS):
                 stage(pair)
 
-        preparations = [(make_mask, (1,))]
-        for qt, n in enumerate((4, 2, 1)):
-            preparations += [(lay_out_v, (n, head)) for head in range(n)] + [(quantise_v, (n,))]
-            if qt > 0:
-                preparations.append((make_mask, (qt + 1,)))
+        preparations = [(transpose_keys, (1, Q_TILES)), (make_padding_mask, ())]
+        for n in (4, 2, 1):
+            preparations += [(group_v, (n,)), (quantise_v, (n,))]
+            if n > 1:
+                preparations.append((spread_v, (n,)))
         halves_done = 0
         for tick in range(2 * PAIRS):
             step, i = divmod(tick, 2)

@@ -31,7 +31,7 @@ HEADS_PER_PASS = (4, 2, 1, 1)
 PAIRS_IN_TILE = tuple(HEADS // (2 * n) for n in HEADS_PER_PASS)
 FIRST_PAIR = tuple(sum(PAIRS_IN_TILE[:qt]) for qt in range(Q_TILES))
 PAIRS = sum(PAIRS_IN_TILE)
-WEIGHT_UNITS = N_SLICES * GROUPS
+WEIGHT_UNITS = HID // (2 * P) * GROUPS
 PREPARE_A_TICK = 2
 EXP_LAG = 1
 LAG_E = 2
@@ -40,10 +40,11 @@ LAG_NORMALISE = 4
 LAG_O = 4
 LAG_PROJECT = 6
 WEIGHT_START = 4
+WEIGHT_QUANTISE_LAG = 1
 TAIL_EARLY = 1
 JOBS_A_STEP = 1
 SCORE_BANKS = 3
-VECTOR_UNITS = 4
+VECTOR_UNITS = 8
 VECTOR_QUERY_TILES = ()
 SCALAR_NORMALISE = ()
 
@@ -128,15 +129,16 @@ def tile_groupqueryattention_pa_kernel(tc, q, k, v, causal_mask, padding_mask, W
         nc.sync.dma_start(out=q_raw[1][:], in_=q[0, P : 2 * P, :])
         load_v(2)
         load_v(1)
+        bias_all = keep.tile([P, HID], BF16)
         for n_slice in range(N_SLICES):
             for i in range(4):
                 nt = 4 * n_slice + i
                 nc.sync.dma_start(out=wo_raw[nt][:], in_=Wo[nt * P : (nt + 1) * P, :])
+            if n_slice == 0:
+                nc.sync.dma_start(out=bias_all[:], in_=bo.partition_broadcast(P))
             qt = n_slice + 2
             if qt < Q_TILES:
                 nc.sync.dma_start(out=q_raw[qt][:], in_=q[0, qt * P : (qt + 1) * P, :])
-        bias_all = keep.tile([P, HID], BF16)
-        nc.sync.dma_start(out=bias_all[:], in_=bo.partition_broadcast(P))
 
         ident_bf = keep.tile([P, P], BF16)
         make_identity(nc, ident_bf[:])
@@ -418,33 +420,32 @@ def tile_groupqueryattention_pa_kernel(tc, q, k, v, causal_mask, padding_mask, W
                 out=o_codes[:, cols].bitcast(FP8X4), scales=o_scales[:, cols], in_=o_grouped_of[group][:]
             )
 
-        def transpose_weights(unit, half):
-            n_slice, g = divmod(unit, GROUPS)
+        def transpose_weights(unit):
+            row_pair, g = divmod(unit, GROUPS)
             wT_ps = psum_b.tile([P, 2, 2, P], F32, tag="bank")
             for i in range(2):
-                words = wo_raw[4 * n_slice + 2 * half + i][:].bitcast(F32)
+                words = wo_raw[2 * row_pair + i][:].bitcast(F32)
                 for u in range(2):
                     first_word = g * 2 * P + u * P
                     nc.tensor.transpose(wT_ps[:, i, u, :], words[:, first_word : first_word + P], ident_f32[:])
-            wT_ps_of[unit, half] = wT_ps
+            wT_ps_of[unit] = wT_ps
 
-        def copy_weights(unit, half):
-            if half == 0:
-                w_grouped_new = work.tile([P, BANK_F32 * 4], BF16, align_bytes=64, name="w_grouped", bufs=4)
-                w_grouped_of[unit] = w_grouped_new
-            copy = nc.vector.tensor_copy if half == 1 and unit < VECTOR_UNITS else nc.scalar.copy
+        def copy_weights(unit):
+            w_grouped = work.tile([P, 2 * P * 4], BF16, align_bytes=64)
+            copy = nc.vector.tensor_copy if unit % 2 == 1 and unit < VECTOR_UNITS else nc.scalar.copy
             copy(
-                out=w_grouped_of[unit][:, half * 1024 : (half + 1) * 1024]
-                .bitcast(F32)
-                .rearrange("p (i n u) -> p i n u", i=2, u=2),
-                in_=wT_ps_of[unit, half][:].rearrange("p i u n -> p i n u"),
+                out=w_grouped[:].bitcast(F32).rearrange("p (i n u) -> p i n u", i=2, u=2),
+                in_=wT_ps_of[unit][:].rearrange("p i u n -> p i n u"),
             )
+            w_grouped_of[unit] = w_grouped
 
         def quantise_weights(unit):
-            n_slice, g = divmod(unit, GROUPS)
-            cols = slice(g * HID + n_slice * BANK_F32, g * HID + (n_slice + 1) * BANK_F32)
+            row_pair, g = divmod(unit, GROUPS)
+            first = g * HID + row_pair * 2 * P
             nc.vector.quantize_mx(
-                out=w_codes[:, cols].bitcast(FP8X4), scales=w_scales[:, cols], in_=w_grouped_of[unit][:]
+                out=w_codes[:, first : first + 2 * P].bitcast(FP8X4),
+                scales=w_scales[:, first : first + 2 * P],
+                in_=w_grouped_of[unit][:],
             )
 
         def project(qt, n_slice, g, y_ps):
@@ -472,12 +473,10 @@ def tile_groupqueryattention_pa_kernel(tc, q, k, v, causal_mask, padding_mask, W
             nc.vector.tensor_tensor(out=y_sb[:], in0=y_ps[:], in1=bias_all[:, n_cols], op=ALU.add)
             nc.sync.dma_start(out=out[0, qt * P : (qt + 1) * P, n_cols], in_=y_sb[:])
 
-        units_waiting = []
-        units_quantised = []
-
-        def may_project(qt, n_slice, step):
+        def may_project(qt, n_slice, tick):
             last_pair = FIRST_PAIR[qt] + PAIRS_IN_TILE[qt] - 1
-            return step >= last_pair + LAG_PROJECT and n_slice * GROUPS + GROUPS - 1 in units_quantised
+            units = (n_slice + 1) * WEIGHT_UNITS // N_SLICES
+            return tick // 2 >= last_pair + LAG_PROJECT and tick - WEIGHT_START - WEIGHT_QUANTISE_LAG >= units - 1
 
         to_project = [(qt, n_slice) for qt in range(Q_TILES - 1) for n_slice in range(N_SLICES)]
         y_waiting = []
@@ -497,7 +496,6 @@ def tile_groupqueryattention_pa_kernel(tc, q, k, v, causal_mask, padding_mask, W
             preparations += [(group_v, (n,)), (quantise_v, (n,))]
             if n > 1:
                 preparations.append((spread_v, (n,)))
-        halves_done = 0
         for tick in range(2 * PAIRS):
             step, i = divmod(tick, 2)
             for prepare, argument in preparations[tick * PREPARE_A_TICK : (tick + 1) * PREPARE_A_TICK]:
@@ -512,15 +510,10 @@ def tile_groupqueryattention_pa_kernel(tc, q, k, v, causal_mask, padding_mask, W
             if i == 0:
                 staged(transpose_e, step - LAG_E)
                 staged(copy_e, step - LAG_E)
-            halves = 0 if tick < WEIGHT_START else 1
-            units_ended = []
-            for half_unit in range(halves_done, min(halves_done + halves, 2 * WEIGHT_UNITS)):
-                unit, half = divmod(half_unit, 2)
-                transpose_weights(unit, half)
-                copy_weights(unit, half)
-                halves_done += 1
-                if half == 1:
-                    units_ended.append(unit)
+            unit = tick - WEIGHT_START
+            if due(unit, WEIGHT_UNITS):
+                transpose_weights(unit)
+                copy_weights(unit)
             if i == 0:
                 for qt, n_slice, y_ps in y_waiting:
                     add_bias_and_store(qt, n_slice, y_ps)
@@ -536,16 +529,14 @@ def tile_groupqueryattention_pa_kernel(tc, q, k, v, causal_mask, padding_mask, W
                         copy_queries(qt, half)
                 staged(quantise_e, step - LAG_E)
                 staged(invert_row_sums, step - LAG_E)
-            for unit in units_waiting:
-                quantise_weights(unit)
-                units_quantised.append(unit)
-            units_waiting = units_ended
+            if due(unit - WEIGHT_QUANTISE_LAG, WEIGHT_UNITS):
+                quantise_weights(unit - WEIGHT_QUANTISE_LAG)
             if i == 0:
                 for group in groups_ended(step - LAG_O - 1):
                     quantise_o(group)
             else:
                 staged(attend_values, step - LAG_ATTEND)
-                jobs = [job for job in to_project if may_project(job[0], job[1], step)]
+                jobs = [job for job in to_project if may_project(job[0], job[1], tick)]
                 for qt, n_slice in jobs[0:JOBS_A_STEP]:
                     to_project.remove((qt, n_slice))
                     y_waiting.append((qt, n_slice, project_slice(qt, n_slice)))
@@ -599,8 +590,17 @@ def tile_groupqueryattention_pa_kernel(tc, q, k, v, causal_mask, padding_mask, W
             transpose_o(group)
             copy_o(group)
             quantise_o(group)
-        for g in range(TAIL_EARLY, GROUPS):
-            for n_slice in range(N_SLICES):
+        half = N_SLICES // 2
+        for slices, groups in (
+            (range(N_SLICES), range(TAIL_EARLY, GROUPS - 2)),
+            (range(half), range(GROUPS - 2, GROUPS - 1)),
+            (range(half), range(GROUPS - 1, GROUPS)),
+        ):
+            for g in groups:
+                for n_slice in slices:
+                    project(last_tile, n_slice, g, last_y[n_slice])
+        for n_slice in range(half, N_SLICES):
+            for g in range(GROUPS - 2, GROUPS):
                 project(last_tile, n_slice, g, last_y[n_slice])
         for n_slice in range(N_SLICES):
             add_bias_and_store(last_tile, n_slice, last_y[n_slice])

@@ -32,6 +32,8 @@ PAIRS_IN_TILE = tuple(HEADS // (2 * n) for n in HEADS_PER_PASS)
 FIRST_PAIR = tuple(sum(PAIRS_IN_TILE[:qt]) for qt in range(Q_TILES))
 PAIRS = sum(PAIRS_IN_TILE)
 WEIGHT_UNITS = HID // (2 * P) * GROUPS
+KEYS_TICK = 1
+V_TICK = 2
 PREPARE_A_TICK = 2
 EXP_LAG = 1
 LAG_E = 2
@@ -125,10 +127,9 @@ def tile_groupqueryattention_pa_kernel(tc, q, k, v, causal_mask, padding_mask, W
                     in_=v[0, 0 : 4 * rows].rearrange("(p t) d -> p (t d)", t=4),
                 )
 
-        load_v(4)
         nc.sync.dma_start(out=q_raw[1][:], in_=q[0, P : 2 * P, :])
-        load_v(2)
-        load_v(1)
+        for n in (4, 2, 1):
+            load_v(n)
         bias_all = keep.tile([P, HID], BF16)
         for n_slice in range(N_SLICES):
             for i in range(4):
@@ -169,8 +170,9 @@ def tile_groupqueryattention_pa_kernel(tc, q, k, v, causal_mask, padding_mask, W
             for t in range(first, end):
                 nc.tensor.transpose(kT_ps[:, t, :], k_raw[:, t, :], ident_bf[:])
             kT_cols = kT_ps[:].rearrange("p t c -> p (t c)")
+            copy = nc.vector.tensor_copy if first == 0 else nc.scalar.copy
             for u in range(2):
-                nc.vector.tensor_copy(
+                copy(
                     out=half_block(kT[:], first, end, u), in_=half_read(kT_cols, first, end, u)
                 )
 
@@ -262,7 +264,10 @@ def tile_groupqueryattention_pa_kernel(tc, q, k, v, causal_mask, padding_mask, W
             qt = tile_of_pair(pair)
             n_keys = P * (qt + 1)
             heads = heads_of_bank(pair, i)
-            scores = psum_s.tile([P, len(heads), n_keys], F32, tag="scores")
+            if pair == 0:
+                scores = psum_b.tile([P, len(heads), n_keys], F32, tag="bank")
+            else:
+                scores = psum_s.tile([P, len(heads), n_keys], F32, tag="scores")
             for a, (h, turn, slot) in enumerate(heads):
                 nc.tensor.matmul(
                     scores[:, a, :],
@@ -491,19 +496,28 @@ def tile_groupqueryattention_pa_kernel(tc, q, k, v, causal_mask, padding_mask, W
             if due(pair, PAIRS):
                 stage(pair)
 
-        preparations = [(transpose_keys, (1, Q_TILES)), (make_padding_mask, ())]
+        preparations = []
         for n in (4, 2, 1):
             preparations += [(group_v, (n,)), (quantise_v, (n,))]
             if n > 1:
                 preparations.append((spread_v, (n,)))
         for tick in range(2 * PAIRS):
             step, i = divmod(tick, 2)
-            for prepare, argument in preparations[tick * PREPARE_A_TICK : (tick + 1) * PREPARE_A_TICK]:
-                prepare(*argument)
+            if tick == KEYS_TICK:
+                transpose_keys(1, Q_TILES)
+                make_padding_mask()
+            if tick >= V_TICK:
+                first = (tick - V_TICK) * PREPARE_A_TICK
+                for prepare, argument in preparations[first : first + PREPARE_A_TICK]:
+                    prepare(*argument)
             if i == 0:
                 staged(normalise, step - LAG_NORMALISE)
             score(step, i)
             row_maxima(step, i)
+            if tick == 1:
+                for half in range(2):
+                    transpose_queries(1, half)
+                    copy_queries(1, half)
             before = tick - EXP_LAG
             if before >= 0:
                 exponentials(before // 2, before % 2)
@@ -522,7 +536,7 @@ def tile_groupqueryattention_pa_kernel(tc, q, k, v, causal_mask, padding_mask, W
                 for group in groups_ended(step - LAG_O):
                     transpose_o(group)
                     copy_o(group)
-                for qt in range(1, Q_TILES):
+                for qt in range(2, Q_TILES):
                     half = step - (FIRST_PAIR[qt] - 2)
                     if due(half, 2):
                         transpose_queries(qt, half)
@@ -545,7 +559,8 @@ def tile_groupqueryattention_pa_kernel(tc, q, k, v, causal_mask, padding_mask, W
         last = PAIRS - 1
         last_tile = Q_TILES - 1
         normalise(last - 3)
-        exponentials(last, 1)
+        for late in range(2 * PAIRS - EXP_LAG, 2 * PAIRS):
+            exponentials(late // 2, late % 2)
         transpose_e(last - 1)
         copy_e(last - 1)
         attend_values(last - 2)

@@ -35,7 +35,7 @@ WEIGHT_UNITS = HID // (2 * P) * GROUPS
 KEYS_TICK = 1
 V_TICK = 2
 PREPARE_A_TICK = 2
-EXP_LAG = 1
+EXP_LAG = 2
 LAG_E = 2
 LAG_ATTEND = 3
 LAG_NORMALISE = 4
@@ -45,8 +45,7 @@ WEIGHT_START = 4
 WEIGHT_QUANTISE_LAG = 1
 TAIL_EARLY = 1
 JOBS_A_STEP = 1
-SCORE_BANKS = 3
-VECTOR_UNITS = 8
+VECTOR_UNITS = 6
 VECTOR_QUERY_TILES = ()
 SCALAR_NORMALISE = ()
 
@@ -94,8 +93,7 @@ def tile_groupqueryattention_pa_kernel(tc, q, k, v, causal_mask, padding_mask, W
         keep = ctx.enter_context(tc.tile_pool(name="keep", bufs=1))
         work = ctx.enter_context(tc.tile_pool(name="work", bufs=3))
         stats = ctx.enter_context(tc.tile_pool(name="stats", bufs=4))
-        psum_s = ctx.enter_context(tc.psum_pool(name="psum_s", bufs=SCORE_BANKS))
-        psum_b = ctx.enter_context(tc.psum_pool(name="psum_b", bufs=8 - SCORE_BANKS))
+        psum_b = ctx.enter_context(tc.psum_pool(name="psum_b", bufs=8))
 
         k_raw = keep.tile([P, Q_TILES, P], BF16)
         nc.sync.dma_start(out=k_raw[:, 0, :], in_=k[0, 0:P, :])
@@ -264,10 +262,7 @@ def tile_groupqueryattention_pa_kernel(tc, q, k, v, causal_mask, padding_mask, W
             qt = tile_of_pair(pair)
             n_keys = P * (qt + 1)
             heads = heads_of_bank(pair, i)
-            if pair == 0:
-                scores = psum_b.tile([P, len(heads), n_keys], F32, tag="bank")
-            else:
-                scores = psum_s.tile([P, len(heads), n_keys], F32, tag="scores")
+            scores = psum_b.tile([P, len(heads), n_keys], F32, tag="bank")
             for a, (h, turn, slot) in enumerate(heads):
                 nc.tensor.matmul(
                     scores[:, a, :],
@@ -593,10 +588,7 @@ def tile_groupqueryattention_pa_kernel(tc, q, k, v, causal_mask, padding_mask, W
             add_bias_and_store(qt, n_slice, y_ps)
         last_y = []
         for n_slice in range(N_SLICES):
-            if n_slice < SCORE_BANKS:
-                y_ps = psum_s.tile([P, BANK_F32], F32, name="last_y", tag="scores")
-            else:
-                y_ps = psum_b.tile([P, BANK_F32], F32, name="last_y", tag="bank")
+            y_ps = psum_b.tile([P, BANK_F32], F32, name="last_y", tag="bank")
             last_y.append(y_ps)
         for g in range(TAIL_EARLY):
             for n_slice in range(N_SLICES):

@@ -40,12 +40,12 @@ LAG_E = 2
 LAG_ATTEND = 3
 LAG_NORMALISE = 4
 LAG_O = 4
-LAG_PROJECT = 6
-WEIGHT_START = 4
-WEIGHT_QUANTISE_LAG = 1
+LAG_PROJECT = 5
+WEIGHT_START = 5
+WEIGHT_QUANTISE_LAG = 2
 TAIL_EARLY = 1
 JOBS_A_STEP = 1
-VECTOR_UNITS = 6
+VECTOR_UNITS = 4
 VECTOR_QUERY_TILES = ()
 SCALAR_NORMALISE = ()
 
@@ -507,6 +507,8 @@ def tile_groupqueryattention_pa_kernel(tc, q, k, v, causal_mask, padding_mask, W
                     prepare(*argument)
             if i == 0:
                 staged(normalise, step - LAG_NORMALISE)
+            if due(tick - WEIGHT_START - WEIGHT_QUANTISE_LAG, WEIGHT_UNITS):
+                quantise_weights(tick - WEIGHT_START - WEIGHT_QUANTISE_LAG)
             score(step, i)
             row_maxima(step, i)
             if tick == 1:
@@ -516,13 +518,14 @@ def tile_groupqueryattention_pa_kernel(tc, q, k, v, causal_mask, padding_mask, W
             before = tick - EXP_LAG
             if before >= 0:
                 exponentials(before // 2, before % 2)
+            unit = tick - WEIGHT_START
+            if due(unit - 1, WEIGHT_UNITS):
+                copy_weights(unit - 1)
             if i == 0:
                 staged(transpose_e, step - LAG_E)
                 staged(copy_e, step - LAG_E)
-            unit = tick - WEIGHT_START
-            if due(unit, WEIGHT_UNITS):
+            if i == 0 and due(unit, WEIGHT_UNITS):
                 transpose_weights(unit)
-                copy_weights(unit)
             if i == 0:
                 for qt, n_slice, y_ps in y_waiting:
                     add_bias_and_store(qt, n_slice, y_ps)
@@ -538,8 +541,6 @@ def tile_groupqueryattention_pa_kernel(tc, q, k, v, causal_mask, padding_mask, W
                         copy_queries(qt, half)
                 staged(quantise_e, step - LAG_E)
                 staged(invert_row_sums, step - LAG_E)
-            if due(unit - WEIGHT_QUANTISE_LAG, WEIGHT_UNITS):
-                quantise_weights(unit - WEIGHT_QUANTISE_LAG)
             if i == 0:
                 for group in groups_ended(step - LAG_O - 1):
                     quantise_o(group)
@@ -549,6 +550,8 @@ def tile_groupqueryattention_pa_kernel(tc, q, k, v, causal_mask, padding_mask, W
                 for qt, n_slice in jobs[0:JOBS_A_STEP]:
                     to_project.remove((qt, n_slice))
                     y_waiting.append((qt, n_slice, project_slice(qt, n_slice)))
+            if i == 1 and due(unit, WEIGHT_UNITS):
+                transpose_weights(unit)
             scale_maxima(step, i)
 
         last = PAIRS - 1

@@ -287,12 +287,28 @@ def tile_groupqueryattention_pa_kernel(tc, q, k, v, causal_mask, padding_mask, W
 
         def row_maxima(pair, i):
             n = len(heads_of_bank(pair, i))
+            if n == 1:
+                shift = stats.tile([P, 1], F32, tag="shift1")
+                scaled = work.tile([P, BANK_F32], BF16, bufs=2)
+                nc.vector.tensor_scalar(
+                    out=scaled[:, 0 : scores_of[pair, i][:].shape[2]],
+                    in0=scores_of[pair, i][:, 0, :],
+                    scalar1=-SCALE,
+                    scalar2=None,
+                    op0=ALU.mult,
+                    op1=ALU.min,
+                    accum_out=shift[:],
+                )
+                shift_of[pair, i] = shift
+                return
             top = stats.tile([P, n], F32, tag="top%d" % n)
             nc.vector.tensor_reduce(out=top[:], in_=scores_of[pair, i][:], axis=mybir.AxisListType.X, op=ALU.max)
             top_of[pair, i] = top
 
         def scale_maxima(pair, i):
             n = len(heads_of_bank(pair, i))
+            if n == 1:
+                return
             shift = stats.tile([P, n], F32, tag="shift%d" % n)
             nc.gpsimd.tensor_scalar(
                 out=shift[:], in0=top_of[pair, i][:], scalar1=-SCALE, scalar2=0.0, op0=ALU.mult, op1=ALU.add

@@ -26,7 +26,8 @@ SCALE = 1.0 / math.sqrt(P)
 SUB = 32
 QUARTERS = P // SUB
 HALF = P // 2
-E_ZEROED = 3
+SUB_BLOCKS = S // HALF
+E_TILES = 3
 HEADS_PER_PASS = (4, 2, 1, 1)
 PAIRS_IN_TILE = tuple(HEADS // (2 * n) for n in HEADS_PER_PASS)
 FIRST_PAIR = tuple(sum(PAIRS_IN_TILE[:qt]) for qt in range(Q_TILES))
@@ -37,12 +38,16 @@ V_TICK = 2
 PREPARE_A_TICK = 2
 EXP_LAG = 2
 LAG_E = 2
+LAG_INVERT = 3
 LAG_ATTEND = 3
 LAG_NORMALISE = 4
 LAG_O = 4
 LAG_PROJECT = 5
 WEIGHT_START = 5
-WEIGHT_QUANTISE_LAG = 2
+W_COPY_LAG = 1
+W_QUANT_LAG = 2
+Q_EARLY = 2
+W_DOUBLE = 0
 TAIL_EARLY = 1
 JOBS_A_STEP = 1
 VECTOR_UNITS = 4
@@ -50,6 +55,19 @@ VECTOR_QUERY_TILES = ()
 SCALAR_NORMALISE = ()
 
 FLOPS = 2 * 2 * HEADS * S * S * P + 2 * S * HID * HID
+
+
+def units_of(tick):
+    n = tick - WEIGHT_START
+    if n < 0:
+        return []
+    first = 2 * min(n, W_DOUBLE) + max(0, n - W_DOUBLE)
+    return [u for u in range(first, first + (2 if n < W_DOUBLE else 1)) if u < WEIGHT_UNITS]
+
+
+def last_unit_by(tick):
+    n = tick - WEIGHT_START
+    return 2 * min(n, W_DOUBLE - 1) + 1 + max(0, n - W_DOUBLE + 1) if n < W_DOUBLE else 2 * W_DOUBLE + n - W_DOUBLE
 
 
 def due(index, count):
@@ -60,31 +78,29 @@ def tile_of_pair(pair):
     return max(qt for qt in range(Q_TILES) if FIRST_PAIR[qt] <= pair)
 
 
-def heads_of_pass(pair, i):
+def couples_of_pair(pair):
     qt = tile_of_pair(pair)
     n = HEADS_PER_PASS[qt]
-    first = (2 * (pair - FIRST_PAIR[qt]) + i) * n
+    first = (pair - FIRST_PAIR[qt]) * n
     return list(range(first, first + n))
 
 
-def heads_of_bank(pair, i):
-    n = HEADS_PER_PASS[tile_of_pair(pair)]
-    first = heads_of_pass(pair, 0)[0]
-    if n == 1:
-        return [(first + i, i, 0)]
-    slots = range(i * n // 2, (i + 1) * n // 2)
-    return [(first + turn * n + slot, turn, slot) for slot in slots for turn in range(2)]
+def head_of(couple, cls):
+    return couple // 2 * GROUP + couple % 2 + 2 * cls
 
 
 def groups_ended(pair):
-    ended = []
     if not due(pair, PAIRS):
-        return ended
-    for i in range(2):
-        for h in heads_of_pass(pair, i):
-            if h % GROUP == GROUP - 1:
-                ended.append((tile_of_pair(pair), h // GROUP))
-    return ended
+        return []
+    return [(tile_of_pair(pair), couple // 2) for couple in couples_of_pair(pair) if couple % 2 == 1]
+
+
+def heads_leaving(pair):
+    qt = tile_of_pair(pair)
+    couples = couples_of_pair(pair)
+    if (qt, couples[0] // 2) == (Q_TILES - 1, GROUPS - 1):
+        return [((qt, GROUPS - 1), [couples[0] % 2])]
+    return [(group, [0, 1]) for group in groups_ended(pair)]
 
 
 def tile_groupqueryattention_pa_kernel(tc, q, k, v, causal_mask, padding_mask, Wo, bo, out):
@@ -108,8 +124,11 @@ def tile_groupqueryattention_pa_kernel(tc, q, k, v, causal_mask, padding_mask, W
         nc.sync.dma_start(out=q_raw[0][:, 0 : HID // 2], in_=q[0, 0:P, 0 : HID // 2])
         pad_all = keep.tile([P, S], BF16)
         nc.sync.dma_start(out=pad_all[:], in_=padding_mask[0].partition_broadcast(P))
-        causal_raw = keep.tile([P, P], BF16)
-        nc.sync.dma_start(out=causal_raw[:], in_=causal_mask[0, 0, 0:P, 0:P])
+        causal_raw = keep.tile([P, HALF], BF16)
+        for cls in range(2):
+            nc.sync.dma_start(
+                out=causal_raw[cls * HALF : (cls + 1) * HALF, :], in_=causal_mask[0, 0, 0:HALF, 0:HALF]
+            )
         nc.sync.dma_start(out=k_raw[:, 1:, :], in_=k[0, P:, :].rearrange("(t p) d -> p t d", p=P))
         nc.sync.dma_start(out=q_raw[0][:, HID // 2 :], in_=q[0, 0:P, HID // 2 :])
         v_raw_of = {}
@@ -149,19 +168,33 @@ def tile_groupqueryattention_pa_kernel(tc, q, k, v, causal_mask, padding_mask, W
             if n > 1:
                 nc.vector.memset(v_codes[:], 0)
             v_codes_of[n] = v_codes
-        e_zeroed = []
-        for i in range(E_ZEROED):
-            e_tile = keep.tile([P, 2 * S], BF16, name="e_zeroed%d" % i)
-            nc.vector.memset(e_tile[:].bitcast(F32), 0.0)
-            e_zeroed.append(e_tile)
+        ident_swap = keep.tile([P, P], F32)
+        for half in range(2):
+            nc.gpsimd.tensor_copy(
+                out=ident_swap[:, half * HALF : (half + 1) * HALF],
+                in_=ident_f32[:, (1 - half) * HALF : (2 - half) * HALF],
+            )
+        e_of_tile = {}
+        for qt in range(Q_TILES):
+            engine = nc.vector if qt == 0 else nc.gpsimd
+            blocks = qt + 1
+            couples = HEADS_PER_PASS[qt]
+            for i in range(E_TILES):
+                e_tile = keep.tile([P, 2 * S], BF16, name="e%d_%d" % (qt, i))
+                e_words = e_tile[:].bitcast(F32).rearrange("p (t u s c) -> p t u s c", t=2, u=2, s=SUB_BLOCKS)
+                engine.memset(e_words[:, 0, :, 2 * blocks - 1 : 2 * blocks * couples : 2 * blocks, :], 0.0)
+                if couples * blocks < QUARTERS:
+                    for t in range(2):
+                        engine.memset(e_words[:, t, :, 2 * blocks * couples :, :], 0.0)
+                e_of_tile[qt, i] = e_tile
 
         kT = keep.tile([P, S], BF16)
 
         def half_block(ap, first, end, u):
-            return ap.rearrange("p (t u w e) -> p t u w e", u=2, w=SUB, e=2)[:, first:end, u]
+            return ap.rearrange("p (s u w e) -> p s u w e", u=2, w=HALF // 4, e=2)[:, first:end, u]
 
         def half_read(ap, first, end, u):
-            return ap.rearrange("p (t w u e) -> p t w u e", w=SUB, u=2, e=2)[:, first:end, :, u, :]
+            return ap.rearrange("p (s w u e) -> p s w u e", w=HALF // 4, u=2, e=2)[:, first:end, :, u, :]
 
         def transpose_keys(first, end):
             kT_ps = psum_b.tile([P, Q_TILES, P], BF16, tag="bank")
@@ -171,7 +204,7 @@ def tile_groupqueryattention_pa_kernel(tc, q, k, v, causal_mask, padding_mask, W
             copy = nc.vector.tensor_copy if first == 0 else nc.scalar.copy
             for u in range(2):
                 copy(
-                    out=half_block(kT[:], first, end, u), in_=half_read(kT_cols, first, end, u)
+                    out=half_block(kT[:], 2 * first, 2 * end, u), in_=half_read(kT_cols, 2 * first, 2 * end, u)
                 )
 
         diagonal_neg = keep.tile([P, S], BF16)
@@ -180,9 +213,9 @@ def tile_groupqueryattention_pa_kernel(tc, q, k, v, causal_mask, padding_mask, W
         def make_diagonal_masks():
             for u in range(2):
                 nc.vector.tensor_tensor(
-                    out=half_block(diagonal_neg[:], 0, Q_TILES, u),
-                    in0=half_read(causal_raw[:], 0, 1, u).to_broadcast([P, Q_TILES, SUB, 2]),
-                    in1=half_read(pad_all[:], 0, Q_TILES, u),
+                    out=half_block(diagonal_neg[:], 0, SUB_BLOCKS, u),
+                    in0=half_read(causal_raw[:], 0, 1, u).to_broadcast([P, SUB_BLOCKS, HALF // 4, 2]),
+                    in1=half_read(pad_all[:], 0, SUB_BLOCKS, u),
                     op=ALU.add,
                 )
             nc.vector.tensor_scalar_mul(diagonal_neg[:], diagonal_neg[:], NEG)
@@ -190,7 +223,7 @@ def tile_groupqueryattention_pa_kernel(tc, q, k, v, causal_mask, padding_mask, W
         def make_padding_mask():
             for u in range(2):
                 nc.vector.tensor_scalar_mul(
-                    half_block(pad_neg[:], 0, Q_TILES, u), half_read(pad_all[:], 0, Q_TILES, u), NEG
+                    half_block(pad_neg[:], 0, SUB_BLOCKS, u), half_read(pad_all[:], 0, SUB_BLOCKS, u), NEG
                 )
 
         v_scales_of = {}
@@ -246,113 +279,111 @@ def tile_groupqueryattention_pa_kernel(tc, q, k, v, causal_mask, padding_mask, W
             if half == 0:
                 qT_new = work.tile([P, HID], BF16, name="qT", bufs=2)
                 qT_of[qt] = qT_new
-            qT_ps = psum_b.tile([P, 8, P], BF16, tag="bank")
-            for i in range(8):
-                h = 8 * half + i
-                nc.tensor.transpose(qT_ps[:, i, :], q_raw[qt][:, h * P : (h + 1) * P], ident_bf[:])
+            qT_ps = psum_b.tile([P, 4, 4, HALF], BF16, tag="bank")
+            for i in range(4):
+                for cls, quarters in enumerate((slice(0, 4, 3), slice(1, 3))):
+                    h = head_of(4 * half + i, cls)
+                    nc.tensor.transpose(
+                        qT_ps[:, i, quarters, :], q_raw[qt][:, h * P : (h + 1) * P], ident_bf[:]
+                    )
             qT_ps_of[qt] = qT_ps
 
         def copy_queries(qt, half):
             copy = nc.vector.tensor_copy if qt in VECTOR_QUERY_TILES else nc.scalar.copy
             copy(
-                out=qT_of[qt][:, half * 8 * P : (half + 1) * 8 * P], in_=qT_ps_of[qt][:].rearrange("p i c -> p (i c)")
+                out=qT_of[qt][:, half * 8 * P : (half + 1) * 8 * P], in_=qT_ps_of[qt][:].rearrange("p i c q -> p (i c q)")
             )
 
-        def score(pair, i):
+        def score(pair, t):
             qt = tile_of_pair(pair)
-            n_keys = P * (qt + 1)
-            heads = heads_of_bank(pair, i)
-            scores = psum_b.tile([P, len(heads), n_keys], F32, tag="bank")
-            for a, (h, turn, slot) in enumerate(heads):
+            couples = couples_of_pair(pair)
+            left = (2 * qt + t) * HALF
+            n_keys = left + HALF
+            scores = psum_b.tile([P, len(couples), n_keys], F32, tag="bank")
+            for a, couple in enumerate(couples):
+                first = (2 * couple + t) * P
                 nc.tensor.matmul(
-                    scores[:, a, :],
-                    lhsT=qT_of[qt][:, h * P : (h + 1) * P],
-                    rhs=kT[:, 0:n_keys],
-                    start=True,
-                    stop=False,
+                    scores[:, a, :], lhsT=qT_of[qt][:, first : first + P], rhs=kT[:, 0:n_keys], start=True, stop=False
                 )
-                if qt > 0:
-                    left = qt * P
+                if left > 0:
                     nc.tensor.matmul(
                         scores[:, a, 0:left], lhsT=ident_bf[:], rhs=pad_neg[:, 0:left], start=False, stop=False
                     )
                 nc.tensor.matmul(
-                    scores[:, a, qt * P :],
-                    lhsT=ident_bf[:],
-                    rhs=diagonal_neg[:, qt * P : (qt + 1) * P],
-                    start=False,
-                    stop=True,
+                    scores[:, a, left:], lhsT=ident_bf[:], rhs=diagonal_neg[:, left:n_keys], start=False, stop=True
                 )
-            scores_of[pair, i] = scores
+            scores_of[pair, t] = scores
 
-        def row_maxima(pair, i):
-            n = len(heads_of_bank(pair, i))
+        def row_maxima(pair, t):
+            n = len(couples_of_pair(pair))
             if n == 1:
                 shift = stats.tile([P, 1], F32, tag="shift1")
                 scaled = work.tile([P, BANK_F32], BF16, bufs=2)
                 nc.vector.tensor_scalar(
-                    out=scaled[:, 0 : scores_of[pair, i][:].shape[2]],
-                    in0=scores_of[pair, i][:, 0, :],
+                    out=scaled[:, 0 : scores_of[pair, t][:].shape[2]],
+                    in0=scores_of[pair, t][:, 0, :],
                     scalar1=-SCALE,
                     scalar2=None,
                     op0=ALU.mult,
                     op1=ALU.min,
                     accum_out=shift[:],
                 )
-                shift_of[pair, i] = shift
+                shift_of[pair, t] = shift
                 return
             top = stats.tile([P, n], F32, tag="top%d" % n)
-            nc.vector.tensor_reduce(out=top[:], in_=scores_of[pair, i][:], axis=mybir.AxisListType.X, op=ALU.max)
-            top_of[pair, i] = top
+            nc.vector.tensor_reduce(out=top[:], in_=scores_of[pair, t][:], axis=mybir.AxisListType.X, op=ALU.max)
+            top_of[pair, t] = top
 
-        def scale_maxima(pair, i):
-            n = len(heads_of_bank(pair, i))
+        def scale_maxima(pair, t):
+            n = len(couples_of_pair(pair))
             if n == 1:
                 return
             shift = stats.tile([P, n], F32, tag="shift%d" % n)
             nc.gpsimd.tensor_scalar(
-                out=shift[:], in0=top_of[pair, i][:], scalar1=-SCALE, scalar2=0.0, op0=ALU.mult, op1=ALU.add
+                out=shift[:], in0=top_of[pair, t][:], scalar1=-SCALE, scalar2=0.0, op0=ALU.mult, op1=ALU.add
             )
-            shift_of[pair, i] = shift
+            shift_of[pair, t] = shift
 
-        def exponentials(pair, i):
+        def exponentials(pair, t):
             qt = tile_of_pair(pair)
             blocks = qt + 1
-            if i == 0:
-                if qt == 2:
-                    e_pair = e_zeroed[pair % E_ZEROED]
-                else:
-                    e_pair = work.tile([P, 2 * S], BF16, name="e_pair", bufs=4)
-                e_pair_of[pair] = e_pair
-            e_view = e_pair_of[pair][:].rearrange("p (i u j c) -> p i j u c", i=2, u=2, j=QUARTERS)
-            for a, (h, turn, slot) in enumerate(heads_of_bank(pair, i)):
-                group = (qt, h // GROUP)
+            n_subs = 2 * qt + 1 + t
+            if t == 0:
+                e_pair_of[pair] = e_of_tile[qt, pair % E_TILES]
+            e_view = e_pair_of[pair][:].rearrange("p (t u s c) -> p t s u c", t=2, u=2, s=SUB_BLOCKS)
+            for a, couple in enumerate(couples_of_pair(pair)):
+                group = (qt, couple // 2)
                 if group not in rowsum_of:
-                    rowsum = stats.tile([P, GROUP], F32, bufs=9)
+                    rowsum = stats.tile([P, 4], F32, bufs=9)
                     rowsum_of[group] = rowsum
+                col = 2 * t + couple % 2
                 nc.scalar.activation(
-                    out=e_view[:, turn, slot * blocks : (slot + 1) * blocks],
-                    in_=scores_of[pair, i][:, a, :].rearrange("p (j u c) -> p j u c", u=2, c=HALF),
+                    out=e_view[:, t, 2 * blocks * a : 2 * blocks * a + n_subs],
+                    in_=scores_of[pair, t][:, a, :].rearrange("p (s u c) -> p s u c", u=2, c=HALF // 2),
                     func=ACT.Exp,
-                    bias=shift_of[pair, i][:, a : a + 1],
+                    bias=shift_of[pair, t][:, a : a + 1],
                     scale=SCALE,
-                    accum_out=rowsum_of[group][:, h % GROUP : h % GROUP + 1],
+                    accum_out=rowsum_of[group][:, col : col + 1],
                 )
 
         def transpose_e(pair):
             e_words = e_pair_of[pair][:].bitcast(F32)
-            eT_ps = psum_b.tile([P, 2, 2, P], F32, tag="bank")
-            for i in range(2):
+            eT_ps = psum_b.tile([P, 8, HALF], F32, tag="bank")
+            for t in range(2):
                 for u in range(2):
-                    first_word = (2 * i + u) * P
-                    nc.tensor.transpose(eT_ps[:, i, u, :], e_words[:, first_word : first_word + P], ident_f32[:])
+                    first_word = (2 * t + u) * P
+                    nc.tensor.transpose(
+                        eT_ps[:, 2 * u : 2 * u + 6 : 5, :] if t == 0 else eT_ps[:, 2 * u + 1 : 2 * u + 5 : 3, :],
+                        e_words[:, first_word : first_word + P],
+                        ident_f32[:] if t == 0 else ident_swap[:],
+                    )
             eT_ps_of[pair] = eT_ps
 
         def copy_e(pair):
             e_grouped = work.tile([P, 2 * P * 4], BF16, align_bytes=64)
             nc.scalar.copy(
                 out=e_grouped[:].bitcast(F32).rearrange("p (i r u) -> p i r u", i=2, u=2),
-                in_=eT_ps_of[pair][:].rearrange("p i u r -> p i r u"),
+                in_=eT_ps_of[pair][:].rearrange("p (i u h) r -> p i (h r) u", i=2, u=2),
             )
             e_grouped_of[pair] = e_grouped
 
@@ -363,62 +394,56 @@ def tile_groupqueryattention_pa_kernel(tc, q, k, v, causal_mask, padding_mask, W
             e_codes_of[pair] = (e_codes, e_scales)
 
         def attend_values(pair):
-            n_heads = HEADS_PER_PASS[tile_of_pair(pair)]
+            qt = tile_of_pair(pair)
+            n = HEADS_PER_PASS[qt]
             e_codes, e_scales = e_codes_of[pair]
-            v_codes, v_scales = v_codes_of[n_heads], v_scales_of[n_heads]
-            per_bank = GROUP if n_heads == GROUP else 2 * n_heads
-            for i in range(2):
-                first = (i * n_heads) % per_bank
-                if first == 0:
-                    o_ps = psum_b.tile([P, per_bank, P], F32, tag="bank")
-                    o_ps_of.setdefault(pair, []).append(o_ps)
-                for a in range(n_heads):
+            for a, couple in enumerate(couples_of_pair(pair)):
+                group = (qt, couple // 2)
+                if group not in o_ps_of:
+                    o_ps = psum_b.tile([P, 2, 2, P], F32, tag="bank")
+                    o_ps_of[group] = o_ps
+            for cls in range(2):
+                for a, couple in enumerate(couples_of_pair(pair)):
                     nc.tensor.matmul_mx(
-                        out=o_ps[:, first + a, :],
-                        lhsT=e_codes[:, i * P : (i + 1) * P].bitcast(FP8X4),
-                        lhsT_scale=e_scales[:, i * P : (i + 1) * P],
-                        rhs=v_codes[:, a * P : (a + 1) * P].bitcast(FP8X4),
-                        rhs_scale=v_scales[:],
+                        out=o_ps_of[qt, couple // 2][:, cls, couple % 2, :],
+                        lhsT=e_codes[:, cls * P : (cls + 1) * P].bitcast(FP8X4),
+                        lhsT_scale=e_scales[:, cls * P : (cls + 1) * P],
+                        rhs=v_codes_of[n][:, a * P : (a + 1) * P].bitcast(FP8X4),
+                        rhs_scale=v_scales_of[n][:],
                         start=True,
                         stop=True,
                     )
 
         def invert_row_sums(pair):
-            qt = tile_of_pair(pair)
-            h = heads_of_pass(pair, 0)[0]
-            n_heads = 2 * HEADS_PER_PASS[qt]
-            recips = []
-            for first in range(0, n_heads, GROUP):
-                n = min(GROUP, n_heads)
-                col = (h + first) % GROUP
-                recip = stats.tile([P, n], F32, tag="recip%d" % n, bufs=6)
-                nc.vector.reciprocal(recip[:], rowsum_of[qt, (h + first) // GROUP][:, col : col + n])
-                recips.append(recip)
-            recip_of[pair] = recips
+            for group, couples in heads_leaving(pair):
+                if group not in recip_of:
+                    recip = stats.tile([P, 2, 2], F32, bufs=6)
+                    recip_of[group] = recip
+                cols = slice(couples[0], couples[-1] + 1)
+                sums = rowsum_of[group][:].rearrange("p (t m) -> p t m", t=2)
+                nc.vector.reciprocal(recip_of[group][0:HALF, :, cols], sums[0:HALF, :, cols])
+                nc.vector.reciprocal(recip_of[group][HALF:, :, cols], sums[HALF:, ::-1, cols])
 
         def normalise(pair):
-            qt = tile_of_pair(pair)
-            h = heads_of_pass(pair, 0)[0]
-            for o_ps, recip in zip(o_ps_of[pair], recip_of[pair]):
-                n = o_ps[:].shape[1]
-                group = (qt, h // GROUP)
-                first = h % GROUP
-                if first == 0:
+            for group, couples in heads_leaving(pair):
+                if group not in o_sb_of:
                     o_sb_new = work.tile([P, GROUP * P], BF16, name="o_sb", bufs=4)
                     o_sb_of[group] = o_sb_new
+                cols = slice(couples[0], couples[-1] + 1)
                 nc.vector.tensor_tensor(
-                    out=o_sb_of[group][:, first * P : (first + n) * P].rearrange("p (t d) -> p t d", t=n),
-                    in0=o_ps[:],
-                    in1=recip[:].unsqueeze(2).to_broadcast([P, n, P]),
+                    out=o_sb_of[group][:].rearrange("p (i m d) -> p i m d", i=2, m=2)[:, :, cols, :],
+                    in0=o_ps_of[group][:, :, cols, :],
+                    in1=recip_of[group][:, :, cols].unsqueeze(3).to_broadcast([P, 2, len(couples), P]),
                     op=ALU.mult,
                 )
-                h += n
 
         def transpose_o(group):
             o_words = o_sb_of[group][:].bitcast(F32)
             oT_ps = psum_b.tile([P, 2, P], F32, tag="bank")
             for u in range(2):
-                nc.tensor.transpose(oT_ps[:, u, :], o_words[:, u * P : (u + 1) * P], ident_f32[:])
+                nc.tensor.transpose(
+                    oT_ps[:, u, :], o_words[:, u * P : (u + 1) * P], ident_f32[:] if u == 0 else ident_swap[:]
+                )
             oT_ps_of[group] = oT_ps
 
         def copy_o(group):
@@ -492,7 +517,7 @@ def tile_groupqueryattention_pa_kernel(tc, q, k, v, causal_mask, padding_mask, W
         def may_project(qt, n_slice, tick):
             last_pair = FIRST_PAIR[qt] + PAIRS_IN_TILE[qt] - 1
             units = (n_slice + 1) * WEIGHT_UNITS // N_SLICES
-            return tick // 2 >= last_pair + LAG_PROJECT and tick - WEIGHT_START - WEIGHT_QUANTISE_LAG >= units - 1
+            return tick // 2 >= last_pair + LAG_PROJECT and last_unit_by(tick - W_QUANT_LAG) >= units - 1
 
         to_project = [(qt, n_slice) for qt in range(Q_TILES - 1) for n_slice in range(N_SLICES)]
         y_waiting = []
@@ -503,6 +528,7 @@ def tile_groupqueryattention_pa_kernel(tc, q, k, v, causal_mask, padding_mask, W
         transpose_queries(0, 1)
         copy_queries(0, 1)
         make_diagonal_masks()
+        make_padding_mask()
         def staged(stage, pair):
             if due(pair, PAIRS):
                 stage(pair)
@@ -512,67 +538,106 @@ def tile_groupqueryattention_pa_kernel(tc, q, k, v, causal_mask, padding_mask, W
             preparations += [(group_v, (n,)), (quantise_v, (n,))]
             if n > 1:
                 preparations.append((spread_v, (n,)))
-        for tick in range(2 * PAIRS):
-            step, i = divmod(tick, 2)
-            if tick == KEYS_TICK:
-                transpose_keys(1, Q_TILES)
-                make_padding_mask()
-            if tick >= V_TICK:
-                first = (tick - V_TICK) * PREPARE_A_TICK
-                for prepare, argument in preparations[first : first + PREPARE_A_TICK]:
-                    prepare(*argument)
-            if i == 0:
-                staged(normalise, step - LAG_NORMALISE)
-            if due(tick - WEIGHT_START - WEIGHT_QUANTISE_LAG, WEIGHT_UNITS):
-                quantise_weights(tick - WEIGHT_START - WEIGHT_QUANTISE_LAG)
+        def weights_in(stage, lag, tick):
+            for unit in units_of(tick - lag):
+                stage(unit)
+
+        def stage_score(tick, step, i):
             score(step, i)
+
+        def stage_maxima(tick, step, i):
             row_maxima(step, i)
+
+        def stage_scale(tick, step, i):
+            scale_maxima(step, i)
+
+        def stage_q1(tick, step, i):
             if tick == 1:
                 for half in range(2):
                     transpose_queries(1, half)
                     copy_queries(1, half)
+
+        def stage_exp(tick, step, i):
             before = tick - EXP_LAG
             if before >= 0:
                 exponentials(before // 2, before % 2)
-            unit = tick - WEIGHT_START
-            if due(unit - 1, WEIGHT_UNITS):
-                copy_weights(unit - 1)
-            if i == 0:
-                staged(transpose_e, step - LAG_E)
-                staged(copy_e, step - LAG_E)
-            if i == 0 and due(unit, WEIGHT_UNITS):
-                transpose_weights(unit)
-            if i == 0:
-                for qt, n_slice, y_ps in y_waiting:
-                    add_bias_and_store(qt, n_slice, y_ps)
-                y_waiting = []
-            else:
-                for group in groups_ended(step - LAG_O):
-                    transpose_o(group)
-                    copy_o(group)
-                for qt in range(2, Q_TILES):
-                    half = step - (FIRST_PAIR[qt] - 2)
-                    if due(half, 2):
-                        transpose_queries(qt, half)
-                        copy_queries(qt, half)
-                staged(quantise_e, step - LAG_E)
-                staged(invert_row_sums, step - LAG_E)
-            if i == 0:
-                for group in groups_ended(step - LAG_O - 1):
-                    quantise_o(group)
-            else:
-                staged(attend_values, step - LAG_ATTEND)
-                jobs = [job for job in to_project if may_project(job[0], job[1], tick)]
-                for qt, n_slice in jobs[0:JOBS_A_STEP]:
-                    to_project.remove((qt, n_slice))
-                    y_waiting.append((qt, n_slice, project_slice(qt, n_slice)))
-            if i == 1 and due(unit, WEIGHT_UNITS):
-                transpose_weights(unit)
-            scale_maxima(step, i)
+
+        def stage_tr_e(tick, step, i):
+            staged(transpose_e, step - LAG_E)
+
+        def stage_cp_e(tick, step, i):
+            staged(copy_e, step - LAG_E)
+
+        def stage_q_e(tick, step, i):
+            staged(quantise_e, step - LAG_E)
+
+        def stage_inv(tick, step, i):
+            staged(invert_row_sums, step - LAG_INVERT)
+
+        def stage_norm(tick, step, i):
+            staged(normalise, step - LAG_NORMALISE)
+
+        def stage_attend(tick, step, i):
+            staged(attend_values, step - LAG_ATTEND)
+
+        def stage_tr_o(tick, step, i):
+            for group in groups_ended(step - LAG_O):
+                transpose_o(group)
+
+        def stage_cp_o(tick, step, i):
+            for group in groups_ended(step - LAG_O):
+                copy_o(group)
+
+        def stage_q_o(tick, step, i):
+            for group in groups_ended(step - LAG_O - 1):
+                quantise_o(group)
+
+        def stage_q23(tick, step, i):
+            for qt in range(2, Q_TILES):
+                half = step - (FIRST_PAIR[qt] - Q_EARLY)
+                if due(half, 2):
+                    transpose_queries(qt, half)
+                    copy_queries(qt, half)
+
+        def stage_bias(tick, step, i):
+            nonlocal_y = list(y_waiting)
+            y_waiting.clear()
+            for qt, n_slice, y_ps in nonlocal_y:
+                add_bias_and_store(qt, n_slice, y_ps)
+
+        def stage_project(tick, step, i):
+            jobs = [job for job in to_project if may_project(job[0], job[1], tick)]
+            for qt, n_slice in jobs[0:JOBS_A_STEP]:
+                to_project.remove((qt, n_slice))
+                y_waiting.append((qt, n_slice, project_slice(qt, n_slice)))
+
+        def stage_trw(tick, step, i):
+            weights_in(transpose_weights, 0, tick)
+
+        def stage_cpw(tick, step, i):
+            weights_in(copy_weights, W_COPY_LAG, tick)
+
+        def stage_qw(tick, step, i):
+            weights_in(quantise_weights, W_QUANT_LAG, tick)
+
+        def stage_prep(tick, step, i):
+            if tick == KEYS_TICK:
+                transpose_keys(1, Q_TILES)
+            if tick >= V_TICK:
+                first = (tick - V_TICK) * PREPARE_A_TICK
+                for prepare, argument in preparations[first : first + PREPARE_A_TICK]:
+                    prepare(*argument)
+
+        EVEN = (stage_prep, stage_norm, stage_qw, stage_score, stage_maxima, stage_inv, stage_exp, stage_cpw, stage_tr_e, stage_cp_e, stage_trw, stage_bias, stage_q_o, stage_scale)
+        ODD = (stage_prep, stage_qw, stage_score, stage_maxima, stage_q1, stage_exp, stage_cpw, stage_tr_o, stage_cp_o, stage_q23, stage_q_e, stage_attend, stage_project, stage_trw, stage_scale)
+        for tick in range(2 * PAIRS):
+            for stage in (EVEN, ODD)[tick % 2]:
+                stage(tick, tick // 2, tick % 2)
 
         last = PAIRS - 1
         last_tile = Q_TILES - 1
         normalise(last - 3)
+        invert_row_sums(last - 2)
         for late in range(2 * PAIRS - EXP_LAG, 2 * PAIRS):
             exponentials(late // 2, late % 2)
         transpose_e(last - 1)

@@ -168,6 +168,10 @@ def tile_groupqueryattention_pa_kernel(tc, q, k, v, causal_mask, padding_mask, W
             if n > 1:
                 nc.vector.memset(v_codes[:], 0)
             v_codes_of[n] = v_codes
+        half_is = keep.tile([P, 2], F32)
+        nc.vector.memset(half_is[:], 0.0)
+        for half in range(2):
+            nc.vector.memset(half_is[half * HALF : (half + 1) * HALF, half : half + 1], 1.0)
         ident_swap = keep.tile([P, P], F32)
         for half in range(2):
             nc.gpsimd.tensor_copy(
@@ -188,10 +192,10 @@ def tile_groupqueryattention_pa_kernel(tc, q, k, v, causal_mask, padding_mask, W
                         engine.memset(e_words[:, t, :, 2 * blocks * couples :, :], 0.0)
                 e_of_tile[qt, i] = e_tile
 
-        kT = keep.tile([P, S], BF16)
+        kT = keep.tile([P, 2, S // 2], BF16)
 
-        def half_block(ap, first, end, u):
-            return ap.rearrange("p (s u w e) -> p s u w e", u=2, w=HALF // 4, e=2)[:, first:end, u]
+        def half_block(tile, first, end, u):
+            return tile[:, u, first * SUB : end * SUB].rearrange("p (s w e) -> p s w e", w=HALF // 4, e=2)
 
         def half_read(ap, first, end, u):
             return ap.rearrange("p (s w u e) -> p s w u e", w=HALF // 4, u=2, e=2)[:, first:end, :, u, :]
@@ -204,27 +208,35 @@ def tile_groupqueryattention_pa_kernel(tc, q, k, v, causal_mask, padding_mask, W
             copy = nc.vector.tensor_copy if first == 0 else nc.scalar.copy
             for u in range(2):
                 copy(
-                    out=half_block(kT[:], 2 * first, 2 * end, u), in_=half_read(kT_cols, 2 * first, 2 * end, u)
+                    out=half_block(kT, 2 * first, 2 * end, u), in_=half_read(kT_cols, 2 * first, 2 * end, u)
                 )
 
-        diagonal_neg = keep.tile([P, S], BF16)
-        pad_neg = keep.tile([P, S], BF16)
+        diagonal_neg = keep.tile([P, 2, S // 2], BF16)
+        pad_neg = keep.tile([P, 2, S // 2], BF16)
+        mask_of = []
+        for s in range(SUB_BLOCKS):
+            mask = keep.tile([P, 2, (s + 1) * SUB], BF16, name="mask%d" % s)
+            mask_of.append(mask)
 
         def make_diagonal_masks():
             for u in range(2):
                 nc.vector.tensor_tensor(
-                    out=half_block(diagonal_neg[:], 0, SUB_BLOCKS, u),
+                    out=half_block(diagonal_neg, 0, SUB_BLOCKS, u),
                     in0=half_read(causal_raw[:], 0, 1, u).to_broadcast([P, SUB_BLOCKS, HALF // 4, 2]),
                     in1=half_read(pad_all[:], 0, SUB_BLOCKS, u),
                     op=ALU.add,
                 )
-            nc.vector.tensor_scalar_mul(diagonal_neg[:], diagonal_neg[:], NEG)
-
-        def make_padding_mask():
             for u in range(2):
                 nc.vector.tensor_scalar_mul(
-                    half_block(pad_neg[:], 0, SUB_BLOCKS, u), half_read(pad_all[:], 0, SUB_BLOCKS, u), NEG
+                    half_block(pad_neg, 0, SUB_BLOCKS, u), half_read(pad_all[:], 0, SUB_BLOCKS, u), NEG
                 )
+
+        def make_mask(s):
+            left = s * SUB
+            nc.vector.tensor_scalar_mul(mask_of[s][:, :, left:], diagonal_neg[:, :, left : left + SUB], NEG)
+            if s > 0:
+                copy = nc.vector.tensor_copy if s < 4 else nc.gpsimd.tensor_copy
+                copy(out=mask_of[s][:, :, 0:left], in_=pad_neg[:, :, 0:left])
 
         v_scales_of = {}
         v_grouped_of = {}
@@ -244,6 +256,8 @@ def tile_groupqueryattention_pa_kernel(tc, q, k, v, causal_mask, padding_mask, W
         oT_ps_of = {}
         wT_ps_of = {}
         rowsum_of = {}
+        aligned_of = {}
+        parts_of = {}
         e_pair_of = {}
         e_grouped_of = {}
         e_codes_of = {}
@@ -279,38 +293,41 @@ def tile_groupqueryattention_pa_kernel(tc, q, k, v, causal_mask, padding_mask, W
             if half == 0:
                 qT_new = work.tile([P, HID], BF16, name="qT", bufs=2)
                 qT_of[qt] = qT_new
-            qT_ps = psum_b.tile([P, 4, 4, HALF], BF16, tag="bank")
-            for i in range(4):
-                for cls, quarters in enumerate((slice(0, 4, 3), slice(1, 3))):
+            qT_ps = psum_b.tile([P, 2, 4, 2, HALF], BF16, tag="bank")
+            for cls in range(2):
+                for i in range(4):
                     h = head_of(4 * half + i, cls)
                     nc.tensor.transpose(
-                        qT_ps[:, i, quarters, :], q_raw[qt][:, h * P : (h + 1) * P], ident_bf[:]
+                        qT_ps[:, cls, i].rearrange("p t q -> p (t q)"), q_raw[qt][:, h * P : (h + 1) * P], ident_bf[:]
                     )
             qT_ps_of[qt] = qT_ps
 
         def copy_queries(qt, half):
             copy = nc.vector.tensor_copy if qt in VECTOR_QUERY_TILES else nc.scalar.copy
-            copy(
-                out=qT_of[qt][:, half * 8 * P : (half + 1) * 8 * P], in_=qT_ps_of[qt][:].rearrange("p i c q -> p (i c q)")
-            )
+            couples = qT_of[qt][:, half * 8 * P : (half + 1) * 8 * P].rearrange("p (i c q) -> p i c q", i=4, c=4)
+            for cls, parts in enumerate((slice(0, 4, 3), slice(1, 3))):
+                copy(out=couples[:, :, parts, :], in_=qT_ps_of[qt][:, cls])
 
         def score(pair, t):
             qt = tile_of_pair(pair)
             couples = couples_of_pair(pair)
-            left = (2 * qt + t) * HALF
-            n_keys = left + HALF
+            n_keys = (2 * qt + t + 1) * HALF
             scores = psum_b.tile([P, len(couples), n_keys], F32, tag="bank")
             for a, couple in enumerate(couples):
                 first = (2 * couple + t) * P
                 nc.tensor.matmul(
-                    scores[:, a, :], lhsT=qT_of[qt][:, first : first + P], rhs=kT[:, 0:n_keys], start=True, stop=False
+                    scores[:, a, :],
+                    lhsT=qT_of[qt][:, first : first + P],
+                    rhs=kT[:, :, 0 : n_keys // 2],
+                    start=True,
+                    stop=False,
                 )
-                if left > 0:
-                    nc.tensor.matmul(
-                        scores[:, a, 0:left], lhsT=ident_bf[:], rhs=pad_neg[:, 0:left], start=False, stop=False
-                    )
                 nc.tensor.matmul(
-                    scores[:, a, left:], lhsT=ident_bf[:], rhs=diagonal_neg[:, left:n_keys], start=False, stop=True
+                    scores[:, a, :],
+                    lhsT=ident_bf[:],
+                    rhs=mask_of[2 * qt + t][:].rearrange("p u c -> p (u c)"),
+                    start=False,
+                    stop=True,
                 )
             scores_of[pair, t] = scores
 
@@ -350,30 +367,56 @@ def tile_groupqueryattention_pa_kernel(tc, q, k, v, causal_mask, padding_mask, W
             n_subs = 2 * qt + 1 + t
             if t == 0:
                 e_pair_of[pair] = e_of_tile[qt, pair % E_TILES]
-            e_view = e_pair_of[pair][:].rearrange("p (t u s c) -> p t s u c", t=2, u=2, s=SUB_BLOCKS)
+            e_view = e_pair_of[pair][:].rearrange("p (t u c) -> p t u c", t=2, u=2)
             for a, couple in enumerate(couples_of_pair(pair)):
                 group = (qt, couple // 2)
                 if group not in rowsum_of:
                     rowsum = stats.tile([P, 4], F32, bufs=9)
                     rowsum_of[group] = rowsum
                 col = 2 * t + couple % 2
+                first = 2 * blocks * a * SUB
                 nc.scalar.activation(
-                    out=e_view[:, t, 2 * blocks * a : 2 * blocks * a + n_subs],
-                    in_=scores_of[pair, t][:, a, :].rearrange("p (s u c) -> p s u c", u=2, c=HALF // 2),
+                    out=e_view[:, t, :, first : first + n_subs * SUB],
+                    in_=scores_of[pair, t][:, a, :].rearrange("p (u c) -> p u c", u=2),
                     func=ACT.Exp,
                     bias=shift_of[pair, t][:, a : a + 1],
                     scale=SCALE,
                     accum_out=rowsum_of[group][:, col : col + 1],
                 )
 
+        def align_row_sums(pair):
+            for group, couples in heads_leaving(pair):
+                if group not in aligned_of:
+                    for name in range(3):
+                        part = stats.tile([P, 2, 2], F32, name="part%d" % name, bufs=6)
+                        parts_of[group, name] = part
+                    aligned_of[group] = parts_of[group, 2]
+                cols = slice(couples[0], couples[-1] + 1)
+                sums = rowsum_of[group][:].rearrange("p (t m) -> p t m", t=2)
+                for half in range(2):
+                    nc.gpsimd.tensor_scalar(
+                        out=parts_of[group, half][:, :, cols],
+                        in0=sums[:, :, cols],
+                        scalar1=half_is[:, half : half + 1],
+                        scalar2=0.0,
+                        op0=ALU.mult,
+                        op1=ALU.add,
+                    )
+                nc.gpsimd.tensor_tensor(
+                    out=aligned_of[group][:, :, cols],
+                    in0=parts_of[group, 0][:, :, cols],
+                    in1=parts_of[group, 1][:, ::-1, cols],
+                    op=ALU.add,
+                )
+
         def transpose_e(pair):
             e_words = e_pair_of[pair][:].bitcast(F32)
-            eT_ps = psum_b.tile([P, 8, HALF], F32, tag="bank")
+            eT_ps = psum_b.tile([P, 2, 2, P], F32, tag="bank")
             for t in range(2):
                 for u in range(2):
                     first_word = (2 * t + u) * P
                     nc.tensor.transpose(
-                        eT_ps[:, 2 * u : 2 * u + 6 : 5, :] if t == 0 else eT_ps[:, 2 * u + 1 : 2 * u + 5 : 3, :],
+                        eT_ps[:, t, u, :],
                         e_words[:, first_word : first_word + P],
                         ident_f32[:] if t == 0 else ident_swap[:],
                     )
@@ -381,10 +424,11 @@ def tile_groupqueryattention_pa_kernel(tc, q, k, v, causal_mask, padding_mask, W
 
         def copy_e(pair):
             e_grouped = work.tile([P, 2 * P * 4], BF16, align_bytes=64)
-            nc.scalar.copy(
-                out=e_grouped[:].bitcast(F32).rearrange("p (i r u) -> p i r u", i=2, u=2),
-                in_=eT_ps_of[pair][:].rearrange("p (i u h) r -> p i (h r) u", i=2, u=2),
-            )
+            columns = e_grouped[:].bitcast(F32).rearrange("p (x q u) -> p x q u", x=4, u=2)
+            for t, parts in enumerate((slice(0, 4, 3), slice(1, 3))):
+                nc.scalar.copy(
+                    out=columns[:, parts], in_=eT_ps_of[pair][:, t].rearrange("p u (h q) -> p h q u", h=2)
+                )
             e_grouped_of[pair] = e_grouped
 
         def quantise_e(pair):
@@ -420,9 +464,7 @@ def tile_groupqueryattention_pa_kernel(tc, q, k, v, causal_mask, padding_mask, W
                     recip = stats.tile([P, 2, 2], F32, bufs=6)
                     recip_of[group] = recip
                 cols = slice(couples[0], couples[-1] + 1)
-                sums = rowsum_of[group][:].rearrange("p (t m) -> p t m", t=2)
-                nc.vector.reciprocal(recip_of[group][0:HALF, :, cols], sums[0:HALF, :, cols])
-                nc.vector.reciprocal(recip_of[group][HALF:, :, cols], sums[HALF:, ::-1, cols])
+                nc.vector.reciprocal(recip_of[group][:, :, cols], aligned_of[group][:, :, cols])
 
         def normalise(pair):
             for group, couples in heads_leaving(pair):
@@ -528,12 +570,13 @@ def tile_groupqueryattention_pa_kernel(tc, q, k, v, causal_mask, padding_mask, W
         transpose_queries(0, 1)
         copy_queries(0, 1)
         make_diagonal_masks()
-        make_padding_mask()
+        for s in range(2):
+            make_mask(s)
         def staged(stage, pair):
             if due(pair, PAIRS):
                 stage(pair)
 
-        preparations = []
+        preparations = [(make_mask, (2,)), (make_mask, (3,))]
         for n in (4, 2, 1):
             preparations += [(group_v, (n,)), (quantise_v, (n,))]
             if n > 1:
@@ -573,6 +616,9 @@ def tile_groupqueryattention_pa_kernel(tc, q, k, v, causal_mask, padding_mask, W
 
         def stage_inv(tick, step, i):
             staged(invert_row_sums, step - LAG_INVERT)
+
+        def stage_align(tick, step, i):
+            staged(align_row_sums, step - LAG_E)
 
         def stage_norm(tick, step, i):
             staged(normalise, step - LAG_NORMALISE)
@@ -628,8 +674,9 @@ def tile_groupqueryattention_pa_kernel(tc, q, k, v, causal_mask, padding_mask, W
                 for prepare, argument in preparations[first : first + PREPARE_A_TICK]:
                     prepare(*argument)
 
-        EVEN = (stage_prep, stage_norm, stage_qw, stage_score, stage_maxima, stage_inv, stage_exp, stage_cpw, stage_tr_e, stage_cp_e, stage_trw, stage_bias, stage_q_o, stage_scale)
+        EVEN = (stage_prep, stage_norm, stage_qw, stage_score, stage_maxima, stage_inv, stage_exp, stage_cpw, stage_tr_e, stage_cp_e, stage_trw, stage_bias, stage_q_o, stage_scale, stage_align)
         ODD = (stage_prep, stage_qw, stage_score, stage_maxima, stage_q1, stage_exp, stage_cpw, stage_tr_o, stage_cp_o, stage_q23, stage_q_e, stage_attend, stage_project, stage_trw, stage_scale)
+        preparations += [(make_mask, (s,)) for s in range(4, SUB_BLOCKS)]
         for tick in range(2 * PAIRS):
             for stage in (EVEN, ODD)[tick % 2]:
                 stage(tick, tick // 2, tick % 2)
@@ -646,6 +693,7 @@ def tile_groupqueryattention_pa_kernel(tc, q, k, v, causal_mask, padding_mask, W
         for qt, n_slice, y_ps in y_waiting:
             add_bias_and_store(qt, n_slice, y_ps)
         y_waiting = []
+        align_row_sums(last - 1)
         quantise_e(last - 1)
         invert_row_sums(last - 1)
         for group in groups_ended(last - 4):
@@ -655,6 +703,7 @@ def tile_groupqueryattention_pa_kernel(tc, q, k, v, causal_mask, padding_mask, W
         transpose_e(last)
         copy_e(last)
         normalise(last - 2)
+        align_row_sums(last)
         quantise_e(last)
         invert_row_sums(last)
         attend_values(last - 1)

@@ -48,6 +48,8 @@ W_COPY_LAG = 1
 W_QUANT_LAG = 2
 Q_EARLY = 2
 W_DOUBLE = 0
+WARM_TICKS = range(4, 20, 2)
+WARM_HEAD = 4
 TAIL_EARLY = 1
 JOBS_A_STEP = 1
 VECTOR_UNITS = 4
@@ -158,6 +160,8 @@ def tile_groupqueryattention_pa_kernel(tc, q, k, v, causal_mask, padding_mask, W
             if qt < Q_TILES:
                 nc.sync.dma_start(out=q_raw[qt][:], in_=q[0, qt * P : (qt + 1) * P, :])
 
+        zeros = keep.tile([P, S], BF16)
+        nc.vector.memset(zeros[:].bitcast(F32), 0.0)
         ident_bf = keep.tile([P, P], BF16)
         make_identity(nc, ident_bf[:])
         ident_f32 = keep.tile([P, P], F32)
@@ -200,6 +204,11 @@ def tile_groupqueryattention_pa_kernel(tc, q, k, v, causal_mask, padding_mask, W
         def half_read(ap, first, end, u):
             return ap.rearrange("p (s w u e) -> p s w u e", w=HALF // 4, u=2, e=2)[:, first:end, :, u, :]
 
+        def keep_warm(moving, count):
+            for i in range(count):
+                unread = psum_b.tile([P, S], F32, tag="bank")
+                nc.tensor.matmul(unread[:], lhsT=moving[:, 0:P], rhs=moving[:, 0:S], start=True, stop=True)
+
         def transpose_keys(first, end):
             kT_ps = psum_b.tile([P, Q_TILES, P], BF16, tag="bank")
             for t in range(first, end):
@@ -235,8 +244,7 @@ def tile_groupqueryattention_pa_kernel(tc, q, k, v, causal_mask, padding_mask, W
             left = s * SUB
             nc.vector.tensor_scalar_mul(mask_of[s][:, :, left:], diagonal_neg[:, :, left : left + SUB], NEG)
             if s > 0:
-                copy = nc.vector.tensor_copy if s < 4 else nc.gpsimd.tensor_copy
-                copy(out=mask_of[s][:, :, 0:left], in_=pad_neg[:, :, 0:left])
+                nc.vector.tensor_copy(out=mask_of[s][:, :, 0:left], in_=pad_neg[:, :, 0:left])
 
         v_scales_of = {}
         v_grouped_of = {}
@@ -564,6 +572,7 @@ def tile_groupqueryattention_pa_kernel(tc, q, k, v, causal_mask, padding_mask, W
         to_project = [(qt, n_slice) for qt in range(Q_TILES - 1) for n_slice in range(N_SLICES)]
         y_waiting = []
         ctx.enter_context(tc.manual_schedule())
+        keep_warm(zeros[:], WARM_HEAD)
         transpose_keys(0, 1)
         transpose_queries(0, 0)
         copy_queries(0, 0)
@@ -666,6 +675,10 @@ def tile_groupqueryattention_pa_kernel(tc, q, k, v, causal_mask, padding_mask, W
         def stage_qw(tick, step, i):
             weights_in(quantise_weights, W_QUANT_LAG, tick)
 
+        def stage_warm(tick, step, i):
+            if tick in WARM_TICKS:
+                keep_warm(kT[:].rearrange("p u c -> p (u c)"), 1)
+
         def stage_prep(tick, step, i):
             if tick == KEYS_TICK:
                 transpose_keys(1, Q_TILES)
@@ -674,7 +687,7 @@ def tile_groupqueryattention_pa_kernel(tc, q, k, v, causal_mask, padding_mask, W
                 for prepare, argument in preparations[first : first + PREPARE_A_TICK]:
                     prepare(*argument)
 
-        EVEN = (stage_prep, stage_norm, stage_qw, stage_score, stage_maxima, stage_inv, stage_exp, stage_cpw, stage_tr_e, stage_cp_e, stage_trw, stage_bias, stage_q_o, stage_scale, stage_align)
+        EVEN = (stage_prep, stage_norm, stage_qw, stage_score, stage_maxima, stage_inv, stage_exp, stage_cpw, stage_tr_e, stage_cp_e, stage_warm, stage_trw, stage_bias, stage_q_o, stage_scale, stage_align)
         ODD = (stage_prep, stage_qw, stage_score, stage_maxima, stage_q1, stage_exp, stage_cpw, stage_tr_o, stage_cp_o, stage_q23, stage_q_e, stage_attend, stage_project, stage_trw, stage_scale)
         preparations += [(make_mask, (s,)) for s in range(4, SUB_BLOCKS)]
         for tick in range(2 * PAIRS):

@@ -172,16 +172,6 @@ def tile_groupqueryattention_pa_kernel(tc, q, k, v, causal_mask, padding_mask, W
             if n > 1:
                 nc.vector.memset(v_codes[:], 0)
             v_codes_of[n] = v_codes
-        half_is = keep.tile([P, 2], F32)
-        nc.vector.memset(half_is[:], 0.0)
-        for half in range(2):
-            nc.vector.memset(half_is[half * HALF : (half + 1) * HALF, half : half + 1], 1.0)
-        ident_swap = keep.tile([P, P], F32)
-        for half in range(2):
-            nc.gpsimd.tensor_copy(
-                out=ident_swap[:, half * HALF : (half + 1) * HALF],
-                in_=ident_f32[:, (1 - half) * HALF : (2 - half) * HALF],
-            )
         e_of_tile = {}
         for qt in range(Q_TILES):
             engine = nc.vector if qt == 0 else nc.gpsimd
@@ -264,8 +254,6 @@ def tile_groupqueryattention_pa_kernel(tc, q, k, v, causal_mask, padding_mask, W
         oT_ps_of = {}
         wT_ps_of = {}
         rowsum_of = {}
-        aligned_of = {}
-        parts_of = {}
         e_pair_of = {}
         e_grouped_of = {}
         e_codes_of = {}
@@ -301,20 +289,21 @@ def tile_groupqueryattention_pa_kernel(tc, q, k, v, causal_mask, padding_mask, W
             if half == 0:
                 qT_new = work.tile([P, HID], BF16, name="qT", bufs=2)
                 qT_of[qt] = qT_new
-            qT_ps = psum_b.tile([P, 2, 4, 2, HALF], BF16, tag="bank")
+            qT_ps = psum_b.tile([P, 2, 8, HALF], BF16, tag="bank")
             for cls in range(2):
                 for i in range(4):
                     h = head_of(4 * half + i, cls)
                     nc.tensor.transpose(
-                        qT_ps[:, cls, i].rearrange("p t q -> p (t q)"), q_raw[qt][:, h * P : (h + 1) * P], ident_bf[:]
+                        qT_ps[:, cls, 2 * i : 2 * i + 2].rearrange("p t q -> p (t q)"), q_raw[qt][:, h * P : (h + 1) * P], ident_bf[:]
                     )
             qT_ps_of[qt] = qT_ps
 
         def copy_queries(qt, half):
             copy = nc.vector.tensor_copy if qt in VECTOR_QUERY_TILES else nc.scalar.copy
-            couples = qT_of[qt][:, half * 8 * P : (half + 1) * 8 * P].rearrange("p (i c q) -> p i c q", i=4, c=4)
-            for cls, parts in enumerate((slice(0, 4, 3), slice(1, 3))):
-                copy(out=couples[:, :, parts, :], in_=qT_ps_of[qt][:, cls])
+            copy(
+                out=qT_of[qt][:, half * 8 * P : (half + 1) * 8 * P].rearrange("p (x c q) -> p c x q", c=2, q=HALF),
+                in_=qT_ps_of[qt][:],
+            )
 
         def score(pair, t):
             qt = tile_of_pair(pair)
@@ -392,51 +381,21 @@ def tile_groupqueryattention_pa_kernel(tc, q, k, v, causal_mask, padding_mask, W
                     accum_out=rowsum_of[group][:, col : col + 1],
                 )
 
-        def align_row_sums(pair):
-            for group, couples in heads_leaving(pair):
-                if group not in aligned_of:
-                    for name in range(3):
-                        part = stats.tile([P, 2, 2], F32, name="part%d" % name, bufs=6)
-                        parts_of[group, name] = part
-                    aligned_of[group] = parts_of[group, 2]
-                cols = slice(couples[0], couples[-1] + 1)
-                sums = rowsum_of[group][:].rearrange("p (t m) -> p t m", t=2)
-                for half in range(2):
-                    nc.gpsimd.tensor_scalar(
-                        out=parts_of[group, half][:, :, cols],
-                        in0=sums[:, :, cols],
-                        scalar1=half_is[:, half : half + 1],
-                        scalar2=0.0,
-                        op0=ALU.mult,
-                        op1=ALU.add,
-                    )
-                nc.gpsimd.tensor_tensor(
-                    out=aligned_of[group][:, :, cols],
-                    in0=parts_of[group, 0][:, :, cols],
-                    in1=parts_of[group, 1][:, ::-1, cols],
-                    op=ALU.add,
-                )
-
         def transpose_e(pair):
             e_words = e_pair_of[pair][:].bitcast(F32)
             eT_ps = psum_b.tile([P, 2, 2, P], F32, tag="bank")
             for t in range(2):
                 for u in range(2):
                     first_word = (2 * t + u) * P
-                    nc.tensor.transpose(
-                        eT_ps[:, t, u, :],
-                        e_words[:, first_word : first_word + P],
-                        ident_f32[:] if t == 0 else ident_swap[:],
-                    )
+                    nc.tensor.transpose(eT_ps[:, t, u, :], e_words[:, first_word : first_word + P], ident_f32[:])
             eT_ps_of[pair] = eT_ps
 
         def copy_e(pair):
             e_grouped = work.tile([P, 2 * P * 4], BF16, align_bytes=64)
-            columns = e_grouped[:].bitcast(F32).rearrange("p (x q u) -> p x q u", x=4, u=2)
-            for t, parts in enumerate((slice(0, 4, 3), slice(1, 3))):
-                nc.scalar.copy(
-                    out=columns[:, parts], in_=eT_ps_of[pair][:, t].rearrange("p u (h q) -> p h q u", h=2)
-                )
+            nc.scalar.copy(
+                out=e_grouped[:].bitcast(F32).rearrange("p (t r u) -> p t r u", t=2, u=2),
+                in_=eT_ps_of[pair][:].rearrange("p t u r -> p t r u"),
+            )
             e_grouped_of[pair] = e_grouped
 
         def quantise_e(pair):
@@ -454,12 +413,12 @@ def tile_groupqueryattention_pa_kernel(tc, q, k, v, causal_mask, padding_mask, W
                 if group not in o_ps_of:
                     o_ps = psum_b.tile([P, 2, 2, P], F32, tag="bank")
                     o_ps_of[group] = o_ps
-            for cls in range(2):
+            for t in range(2):
                 for a, couple in enumerate(couples_of_pair(pair)):
                     nc.tensor.matmul_mx(
-                        out=o_ps_of[qt, couple // 2][:, cls, couple % 2, :],
-                        lhsT=e_codes[:, cls * P : (cls + 1) * P].bitcast(FP8X4),
-                        lhsT_scale=e_scales[:, cls * P : (cls + 1) * P],
+                        out=o_ps_of[qt, couple // 2][:, t, couple % 2, :],
+                        lhsT=e_codes[:, t * P : (t + 1) * P].bitcast(FP8X4),
+                        lhsT_scale=e_scales[:, t * P : (t + 1) * P],
                         rhs=v_codes_of[n][:, a * P : (a + 1) * P].bitcast(FP8X4),
                         rhs_scale=v_scales_of[n][:],
                         start=True,
@@ -472,7 +431,10 @@ def tile_groupqueryattention_pa_kernel(tc, q, k, v, causal_mask, padding_mask, W
                     recip = stats.tile([P, 2, 2], F32, bufs=6)
                     recip_of[group] = recip
                 cols = slice(couples[0], couples[-1] + 1)
-                nc.vector.reciprocal(recip_of[group][:, :, cols], aligned_of[group][:, :, cols])
+                nc.vector.reciprocal(
+                    recip_of[group][:, :, cols],
+                    rowsum_of[group][:].rearrange("p (t m) -> p t m", t=2)[:, :, cols],
+                )
 
         def normalise(pair):
             for group, couples in heads_leaving(pair):
@@ -481,7 +443,7 @@ def tile_groupqueryattention_pa_kernel(tc, q, k, v, causal_mask, padding_mask, W
                     o_sb_of[group] = o_sb_new
                 cols = slice(couples[0], couples[-1] + 1)
                 nc.vector.tensor_tensor(
-                    out=o_sb_of[group][:].rearrange("p (i m d) -> p i m d", i=2, m=2)[:, :, cols, :],
+                    out=o_sb_of[group][:].rearrange("p (t m d) -> p t m d", t=2, m=2)[:, :, cols, :],
                     in0=o_ps_of[group][:, :, cols, :],
                     in1=recip_of[group][:, :, cols].unsqueeze(3).to_broadcast([P, 2, len(couples), P]),
                     op=ALU.mult,
@@ -490,17 +452,15 @@ def tile_groupqueryattention_pa_kernel(tc, q, k, v, causal_mask, padding_mask, W
         def transpose_o(group):
             o_words = o_sb_of[group][:].bitcast(F32)
             oT_ps = psum_b.tile([P, 2, P], F32, tag="bank")
-            for u in range(2):
-                nc.tensor.transpose(
-                    oT_ps[:, u, :], o_words[:, u * P : (u + 1) * P], ident_f32[:] if u == 0 else ident_swap[:]
-                )
+            for t in range(2):
+                nc.tensor.transpose(oT_ps[:, t, :], o_words[:, t * P : (t + 1) * P], ident_f32[:])
             oT_ps_of[group] = oT_ps
 
         def copy_o(group):
             o_grouped = work.tile([P, P * 4], BF16, align_bytes=64, bufs=4)
             nc.scalar.copy(
-                out=o_grouped[:].bitcast(F32).rearrange("p (r u) -> p r u", u=2),
-                in_=oT_ps_of[group][:].rearrange("p u r -> p r u"),
+                out=o_grouped[:].bitcast(F32).rearrange("p (t q u) -> p t q u", t=2, u=2),
+                in_=oT_ps_of[group][:].rearrange("p t (u q) -> p t q u", u=2),
             )
             o_grouped_of[group] = o_grouped
 
@@ -626,9 +586,6 @@ def tile_groupqueryattention_pa_kernel(tc, q, k, v, causal_mask, padding_mask, W
         def stage_inv(tick, step, i):
             staged(invert_row_sums, step - LAG_INVERT)
 
-        def stage_align(tick, step, i):
-            staged(align_row_sums, step - LAG_E)
-
         def stage_norm(tick, step, i):
             staged(normalise, step - LAG_NORMALISE)
 
@@ -687,7 +644,7 @@ def tile_groupqueryattention_pa_kernel(tc, q, k, v, causal_mask, padding_mask, W
                 for prepare, argument in preparations[first : first + PREPARE_A_TICK]:
                     prepare(*argument)
 
-        EVEN = (stage_prep, stage_norm, stage_qw, stage_score, stage_maxima, stage_inv, stage_exp, stage_cpw, stage_tr_e, stage_cp_e, stage_warm, stage_trw, stage_bias, stage_q_o, stage_scale, stage_align)
+        EVEN = (stage_prep, stage_norm, stage_qw, stage_score, stage_maxima, stage_inv, stage_exp, stage_cpw, stage_tr_e, stage_cp_e, stage_warm, stage_trw, stage_bias, stage_q_o, stage_scale)
         ODD = (stage_prep, stage_qw, stage_score, stage_maxima, stage_q1, stage_exp, stage_cpw, stage_tr_o, stage_cp_o, stage_q23, stage_q_e, stage_attend, stage_project, stage_trw, stage_scale)
         preparations += [(make_mask, (s,)) for s in range(4, SUB_BLOCKS)]
         for tick in range(2 * PAIRS):
@@ -706,7 +663,6 @@ def tile_groupqueryattention_pa_kernel(tc, q, k, v, causal_mask, padding_mask, W
         for qt, n_slice, y_ps in y_waiting:
             add_bias_and_store(qt, n_slice, y_ps)
         y_waiting = []
-        align_row_sums(last - 1)
         quantise_e(last - 1)
         invert_row_sums(last - 1)
         for group in groups_ended(last - 4):
@@ -716,7 +672,6 @@ def tile_groupqueryattention_pa_kernel(tc, q, k, v, causal_mask, padding_mask, W
         transpose_e(last)
         copy_e(last)
         normalise(last - 2)
-        align_row_sums(last)
         quantise_e(last)
         invert_row_sums(last)
         attend_values(last - 1)

@@ -48,7 +48,8 @@ W_COPY_LAG = 1
 W_QUANT_LAG = 2
 Q_EARLY = 2
 W_DOUBLE = 0
-WARM_TICKS = range(4, 20, 2)
+WARM_TICKS = range(12, 18, 2)
+BIAS_TICK = 4
 WARM_HEAD = 4
 TAIL_EARLY = 1
 JOBS_A_STEP = 1
@@ -124,8 +125,6 @@ def tile_groupqueryattention_pa_kernel(tc, q, k, v, causal_mask, padding_mask, W
             w_tile = keep.tile([P, HID], BF16, name="wo_raw%d" % nt)
             wo_raw.append(w_tile)
         nc.sync.dma_start(out=q_raw[0][:, 0 : HID // 2], in_=q[0, 0:P, 0 : HID // 2])
-        pad_all = keep.tile([P, S], BF16)
-        nc.sync.dma_start(out=pad_all[:], in_=padding_mask[0].partition_broadcast(P))
         causal_raw = keep.tile([P, HALF], BF16)
         for cls in range(2):
             nc.sync.dma_start(
@@ -149,19 +148,26 @@ def tile_groupqueryattention_pa_kernel(tc, q, k, v, causal_mask, padding_mask, W
         nc.sync.dma_start(out=q_raw[1][:], in_=q[0, P : 2 * P, :])
         for n in (4, 2, 1):
             load_v(n)
-        bias_all = keep.tile([P, HID], BF16)
         for n_slice in range(N_SLICES):
             for i in range(4):
                 nt = 4 * n_slice + i
                 nc.sync.dma_start(out=wo_raw[nt][:], in_=Wo[nt * P : (nt + 1) * P, :])
-            if n_slice == 0:
-                nc.sync.dma_start(out=bias_all[:], in_=bo.partition_broadcast(P))
             qt = n_slice + 2
             if qt < Q_TILES:
                 nc.sync.dma_start(out=q_raw[qt][:], in_=q[0, qt * P : (qt + 1) * P, :])
 
         zeros = keep.tile([P, S], BF16)
         nc.vector.memset(zeros[:].bitcast(F32), 0.0)
+        pad_row = keep.tile([P, S], BF16)
+        nc.vector.memset(pad_row[:].bitcast(F32), 0.0)
+        nc.scalar.dma_start(out=pad_row[0:1, :], in_=padding_mask[0:1, :])
+        first_row = keep.tile([P, P], BF16)
+        nc.vector.memset(first_row[:], 0.0)
+        nc.vector.memset(first_row[0:1, :], 1.0)
+        bias_row = keep.tile([P, HID], BF16)
+        nc.vector.memset(bias_row[:].bitcast(F32), 0.0)
+        nc.scalar.dma_start(out=bias_row[0:1, :], in_=bo.unsqueeze(0))
+        bias_all = keep.tile([P, HID], BF16)
         ident_bf = keep.tile([P, P], BF16)
         make_identity(nc, ident_bf[:])
         ident_f32 = keep.tile([P, P], F32)
@@ -218,16 +224,18 @@ def tile_groupqueryattention_pa_kernel(tc, q, k, v, causal_mask, padding_mask, W
             mask_of.append(mask)
 
         def make_diagonal_masks():
+            pad_ps = psum_b.tile([P, S], F32, tag="bank")
+            nc.tensor.matmul(pad_ps[:], lhsT=first_row[:], rhs=pad_row[:], start=True, stop=True)
             for u in range(2):
                 nc.vector.tensor_tensor(
                     out=half_block(diagonal_neg, 0, SUB_BLOCKS, u),
                     in0=half_read(causal_raw[:], 0, 1, u).to_broadcast([P, SUB_BLOCKS, HALF // 4, 2]),
-                    in1=half_read(pad_all[:], 0, SUB_BLOCKS, u),
+                    in1=half_read(pad_ps[:], 0, SUB_BLOCKS, u),
                     op=ALU.add,
                 )
             for u in range(2):
                 nc.vector.tensor_scalar_mul(
-                    half_block(pad_neg, 0, SUB_BLOCKS, u), half_read(pad_all[:], 0, SUB_BLOCKS, u), NEG
+                    half_block(pad_neg, 0, SUB_BLOCKS, u), half_read(pad_ps[:], 0, SUB_BLOCKS, u), NEG
                 )
 
         def make_mask(s):
@@ -518,6 +526,12 @@ def tile_groupqueryattention_pa_kernel(tc, q, k, v, causal_mask, padding_mask, W
                 project(qt, n_slice, g, y_ps)
             return y_ps
 
+        def spread_bias(n_slice):
+            n_cols = slice(n_slice * BANK_F32, (n_slice + 1) * BANK_F32)
+            bias_ps = psum_b.tile([P, BANK_F32], F32, tag="bank")
+            nc.tensor.matmul(bias_ps[:], lhsT=first_row[:], rhs=bias_row[:, n_cols], start=True, stop=True)
+            nc.scalar.copy(out=bias_all[:, n_cols], in_=bias_ps[:])
+
         def add_bias_and_store(qt, n_slice, y_ps):
             n_cols = slice(n_slice * BANK_F32, (n_slice + 1) * BANK_F32)
             y_sb = work.tile([P, BANK_F32], F32, bufs=6)
@@ -536,11 +550,11 @@ def tile_groupqueryattention_pa_kernel(tc, q, k, v, causal_mask, padding_mask, W
         transpose_keys(0, 1)
         transpose_queries(0, 0)
         copy_queries(0, 0)
-        transpose_queries(0, 1)
-        copy_queries(0, 1)
         make_diagonal_masks()
         for s in range(2):
             make_mask(s)
+        transpose_queries(0, 1)
+        copy_queries(0, 1)
         def staged(stage, pair):
             if due(pair, PAIRS):
                 stage(pair)
@@ -633,6 +647,9 @@ def tile_groupqueryattention_pa_kernel(tc, q, k, v, causal_mask, padding_mask, W
             weights_in(quantise_weights, W_QUANT_LAG, tick)
 
         def stage_warm(tick, step, i):
+            n_slice, odd = divmod(tick - BIAS_TICK, 2)
+            if odd == 0 and due(n_slice, N_SLICES):
+                spread_bias(n_slice)
             if tick in WARM_TICKS:
                 keep_warm(kT[:].rearrange("p u c -> p (u c)"), 1)
 

@@ -37,19 +37,26 @@ KEYS_TICK = 1
 V_TICK = 2
 PREPARE_A_TICK = 2
 EXP_LAG = 2
-LAG_E = 2
-LAG_INVERT = 3
-LAG_ATTEND = 3
-LAG_NORMALISE = 4
-LAG_O = 4
-LAG_PROJECT = 5
-WEIGHT_START = 5
+L_TRE = 4
+L_CPE = 4
+L_QE = 5
+L_INV = 6
+L_ATT = 7
+L_NORM = 8
+L_TRO = 9
+L_CPO = 9
+L_QO = 10
+L_PROJECT = 11
+JOB_PARITY = 1
+L_BIAS = 1
+L_Q23 = 4
+WEIGHT_START = 7
 W_COPY_LAG = 1
 W_QUANT_LAG = 2
 Q_EARLY = 2
 W_DOUBLE = 0
 WARM_TICKS = range(12, 18, 2)
-BIAS_TICK = 4
+BIAS_TICK = 8
 WARM_HEAD = 4
 TAIL_EARLY = 1
 JOBS_A_STEP = 1
@@ -114,6 +121,12 @@ def tile_groupqueryattention_pa_kernel(tc, q, k, v, causal_mask, padding_mask, W
         stats = ctx.enter_context(tc.tile_pool(name="stats", bufs=4))
         psum_b = ctx.enter_context(tc.psum_pool(name="psum_b", bufs=8))
 
+        pad_row = keep.tile([P, S], BF16)
+        nc.vector.memset(pad_row[:].bitcast(F32), 0.0)
+        zeros = keep.tile([P, S], BF16)
+        nc.vector.memset(zeros[:].bitcast(F32), 0.0)
+        bias_row = keep.tile([P, HID], BF16)
+        nc.vector.memset(bias_row[:].bitcast(F32), 0.0)
         k_raw = keep.tile([P, Q_TILES, P], BF16)
         nc.sync.dma_start(out=k_raw[:, 0, :], in_=k[0, 0:P, :])
         q_raw = []
@@ -125,6 +138,7 @@ def tile_groupqueryattention_pa_kernel(tc, q, k, v, causal_mask, padding_mask, W
             w_tile = keep.tile([P, HID], BF16, name="wo_raw%d" % nt)
             wo_raw.append(w_tile)
         nc.sync.dma_start(out=q_raw[0][:, 0 : HID // 2], in_=q[0, 0:P, 0 : HID // 2])
+        nc.sync.dma_start(out=pad_row[0:1, :], in_=padding_mask[0:1, :])
         causal_raw = keep.tile([P, HALF], BF16)
         for cls in range(2):
             nc.sync.dma_start(
@@ -146,6 +160,7 @@ def tile_groupqueryattention_pa_kernel(tc, q, k, v, causal_mask, padding_mask, W
                 )
 
         nc.sync.dma_start(out=q_raw[1][:], in_=q[0, P : 2 * P, :])
+        nc.sync.dma_start(out=bias_row[0:1, :], in_=bo.unsqueeze(0))
         for n in (4, 2, 1):
             load_v(n)
         for n_slice in range(N_SLICES):
@@ -156,17 +171,9 @@ def tile_groupqueryattention_pa_kernel(tc, q, k, v, causal_mask, padding_mask, W
             if qt < Q_TILES:
                 nc.sync.dma_start(out=q_raw[qt][:], in_=q[0, qt * P : (qt + 1) * P, :])
 
-        zeros = keep.tile([P, S], BF16)
-        nc.vector.memset(zeros[:].bitcast(F32), 0.0)
-        pad_row = keep.tile([P, S], BF16)
-        nc.vector.memset(pad_row[:].bitcast(F32), 0.0)
-        nc.scalar.dma_start(out=pad_row[0:1, :], in_=padding_mask[0:1, :])
         first_row = keep.tile([P, P], BF16)
         nc.vector.memset(first_row[:], 0.0)
         nc.vector.memset(first_row[0:1, :], 1.0)
-        bias_row = keep.tile([P, HID], BF16)
-        nc.vector.memset(bias_row[:].bitcast(F32), 0.0)
-        nc.scalar.dma_start(out=bias_row[0:1, :], in_=bo.unsqueeze(0))
         bias_all = keep.tile([P, HID], BF16)
         ident_bf = keep.tile([P, P], BF16)
         make_identity(nc, ident_bf[:])
@@ -526,11 +533,20 @@ def tile_groupqueryattention_pa_kernel(tc, q, k, v, causal_mask, padding_mask, W
                 project(qt, n_slice, g, y_ps)
             return y_ps
 
-        def spread_bias(n_slice):
-            n_cols = slice(n_slice * BANK_F32, (n_slice + 1) * BANK_F32)
-            bias_ps = psum_b.tile([P, BANK_F32], F32, tag="bank")
-            nc.tensor.matmul(bias_ps[:], lhsT=first_row[:], rhs=bias_row[:, n_cols], start=True, stop=True)
-            nc.scalar.copy(out=bias_all[:, n_cols], in_=bias_ps[:])
+        def spread_bias(half):
+            bias_ps = psum_b.tile([P, 2, BANK_F32], BF16, tag="bank")
+            for i in range(2):
+                n_slice = 2 * half + i
+                nc.tensor.matmul(
+                    bias_ps[:, i, :],
+                    lhsT=first_row[:],
+                    rhs=bias_row[:, n_slice * BANK_F32 : (n_slice + 1) * BANK_F32],
+                    start=True,
+                    stop=True,
+                )
+            nc.scalar.copy(
+                out=bias_all[:, half * HID // 2 : (half + 1) * HID // 2], in_=bias_ps[:].rearrange("p i n -> p (i n)")
+            )
 
         def add_bias_and_store(qt, n_slice, y_ps):
             n_cols = slice(n_slice * BANK_F32, (n_slice + 1) * BANK_F32)
@@ -541,7 +557,7 @@ def tile_groupqueryattention_pa_kernel(tc, q, k, v, causal_mask, padding_mask, W
         def may_project(qt, n_slice, tick):
             last_pair = FIRST_PAIR[qt] + PAIRS_IN_TILE[qt] - 1
             units = (n_slice + 1) * WEIGHT_UNITS // N_SLICES
-            return tick // 2 >= last_pair + LAG_PROJECT and last_unit_by(tick - W_QUANT_LAG) >= units - 1
+            return tick >= 2 * last_pair + L_PROJECT and last_unit_by(tick - W_QUANT_LAG) >= units - 1
 
         to_project = [(qt, n_slice) for qt in range(Q_TILES - 1) for n_slice in range(N_SLICES)]
         y_waiting = []
@@ -555,105 +571,33 @@ def tile_groupqueryattention_pa_kernel(tc, q, k, v, causal_mask, padding_mask, W
             make_mask(s)
         transpose_queries(0, 1)
         copy_queries(0, 1)
-        def staged(stage, pair):
-            if due(pair, PAIRS):
+        def of_pair(stage, tick, lag):
+            pair, odd = divmod(tick - lag, 2)
+            if odd == 0 and due(pair, PAIRS):
                 stage(pair)
+
+        def of_groups(stage, tick, lag):
+            pair, odd = divmod(tick - lag, 2)
+            if odd == 0:
+                for group in groups_ended(pair):
+                    stage(group)
+
+        def of_bank(stage, tick, lag):
+            if due(tick - lag, 2 * PAIRS):
+                stage((tick - lag) // 2, (tick - lag) % 2)
+
+        def of_units(stage, tick, lag):
+            for unit in units_of(tick - lag):
+                stage(unit)
 
         preparations = [(make_mask, (2,)), (make_mask, (3,))]
         for n in (4, 2, 1):
             preparations += [(group_v, (n,)), (quantise_v, (n,))]
             if n > 1:
                 preparations.append((spread_v, (n,)))
-        def weights_in(stage, lag, tick):
-            for unit in units_of(tick - lag):
-                stage(unit)
+        preparations += [(make_mask, (s,)) for s in range(4, SUB_BLOCKS)]
 
-        def stage_score(tick, step, i):
-            score(step, i)
-
-        def stage_maxima(tick, step, i):
-            row_maxima(step, i)
-
-        def stage_scale(tick, step, i):
-            scale_maxima(step, i)
-
-        def stage_q1(tick, step, i):
-            if tick == 1:
-                for half in range(2):
-                    transpose_queries(1, half)
-                    copy_queries(1, half)
-
-        def stage_exp(tick, step, i):
-            before = tick - EXP_LAG
-            if before >= 0:
-                exponentials(before // 2, before % 2)
-
-        def stage_tr_e(tick, step, i):
-            staged(transpose_e, step - LAG_E)
-
-        def stage_cp_e(tick, step, i):
-            staged(copy_e, step - LAG_E)
-
-        def stage_q_e(tick, step, i):
-            staged(quantise_e, step - LAG_E)
-
-        def stage_inv(tick, step, i):
-            staged(invert_row_sums, step - LAG_INVERT)
-
-        def stage_norm(tick, step, i):
-            staged(normalise, step - LAG_NORMALISE)
-
-        def stage_attend(tick, step, i):
-            staged(attend_values, step - LAG_ATTEND)
-
-        def stage_tr_o(tick, step, i):
-            for group in groups_ended(step - LAG_O):
-                transpose_o(group)
-
-        def stage_cp_o(tick, step, i):
-            for group in groups_ended(step - LAG_O):
-                copy_o(group)
-
-        def stage_q_o(tick, step, i):
-            for group in groups_ended(step - LAG_O - 1):
-                quantise_o(group)
-
-        def stage_q23(tick, step, i):
-            for qt in range(2, Q_TILES):
-                half = step - (FIRST_PAIR[qt] - Q_EARLY)
-                if due(half, 2):
-                    transpose_queries(qt, half)
-                    copy_queries(qt, half)
-
-        def stage_bias(tick, step, i):
-            nonlocal_y = list(y_waiting)
-            y_waiting.clear()
-            for qt, n_slice, y_ps in nonlocal_y:
-                add_bias_and_store(qt, n_slice, y_ps)
-
-        def stage_project(tick, step, i):
-            jobs = [job for job in to_project if may_project(job[0], job[1], tick)]
-            for qt, n_slice in jobs[0:JOBS_A_STEP]:
-                to_project.remove((qt, n_slice))
-                y_waiting.append((qt, n_slice, project_slice(qt, n_slice)))
-
-        def stage_trw(tick, step, i):
-            weights_in(transpose_weights, 0, tick)
-
-        def stage_cpw(tick, step, i):
-            weights_in(copy_weights, W_COPY_LAG, tick)
-
-        def stage_qw(tick, step, i):
-            weights_in(quantise_weights, W_QUANT_LAG, tick)
-
-        def stage_warm(tick, step, i):
-            n_slice, odd = divmod(tick - BIAS_TICK, 2)
-            if odd == 0 and due(n_slice, N_SLICES):
-                spread_bias(n_slice)
-            if tick in WARM_TICKS:
-                keep_warm(kT[:].rearrange("p u c -> p (u c)"), 1)
-
-        def stage_prep(tick, step, i):
+        def prep(tick):
             if tick == KEYS_TICK:
                 transpose_keys(1, Q_TILES)
             if tick >= V_TICK:
@@ -661,49 +605,71 @@ def tile_groupqueryattention_pa_kernel(tc, q, k, v, causal_mask, padding_mask, W
                 for prepare, argument in preparations[first : first + PREPARE_A_TICK]:
                     prepare(*argument)
 
-        EVEN = (stage_prep, stage_norm, stage_qw, stage_score, stage_maxima, stage_inv, stage_exp, stage_cpw, stage_tr_e, stage_cp_e, stage_warm, stage_trw, stage_bias, stage_q_o, stage_scale)
-        ODD = (stage_prep, stage_qw, stage_score, stage_maxima, stage_q1, stage_exp, stage_cpw, stage_tr_o, stage_cp_o, stage_q23, stage_q_e, stage_attend, stage_project, stage_trw, stage_scale)
-        preparations += [(make_mask, (s,)) for s in range(4, SUB_BLOCKS)]
-        for tick in range(2 * PAIRS):
-            for stage in (EVEN, ODD)[tick % 2]:
-                stage(tick, tick // 2, tick % 2)
+        def q1(tick):
+            if tick == 1:
+                for half in range(2):
+                    transpose_queries(1, half)
+                    copy_queries(1, half)
 
-        last = PAIRS - 1
+        def q23(tick):
+            for qt in range(2, Q_TILES):
+                half, odd = divmod(tick - (2 * FIRST_PAIR[qt] - L_Q23 + 1), 2)
+                if odd == 0 and due(half, 2):
+                    transpose_queries(qt, half)
+                    copy_queries(qt, half)
+
+        def warm(tick):
+            half, odd = divmod(tick - BIAS_TICK, 2)
+            if odd == 0 and due(half, 2):
+                spread_bias(half)
+            if tick in WARM_TICKS:
+                keep_warm(kT[:].rearrange("p u c -> p (u c)"), 1)
+
+        def jobs(tick):
+            if tick % 2 == JOB_PARITY:
+                ready = [job for job in to_project if may_project(job[0], job[1], tick)]
+                for qt, n_slice in ready[0:JOBS_A_STEP]:
+                    to_project.remove((qt, n_slice))
+                    y_waiting.append((tick, qt, n_slice, project_slice(qt, n_slice)))
+
+        def biases(tick):
+            for job in [job for job in y_waiting if job[0] <= tick - L_BIAS]:
+                y_waiting.remove(job)
+                add_bias_and_store(*job[1:])
+
+        stages = {
+            "prep": prep,
+            "norm": lambda tick: of_pair(normalise, tick, L_NORM),
+            "qw": lambda tick: of_units(quantise_weights, tick, W_QUANT_LAG),
+            "score": lambda tick: of_bank(score, tick, 0),
+            "maxima": lambda tick: of_bank(row_maxima, tick, 0),
+            "inv": lambda tick: of_pair(invert_row_sums, tick, L_INV),
+            "exp": lambda tick: of_bank(exponentials, tick, EXP_LAG),
+            "q1": q1,
+            "cpw": lambda tick: of_units(copy_weights, tick, W_COPY_LAG),
+            "tr_e": lambda tick: of_pair(transpose_e, tick, L_TRE),
+            "cp_e": lambda tick: of_pair(copy_e, tick, L_CPE),
+            "warm": warm,
+            "tr_o": lambda tick: of_groups(transpose_o, tick, L_TRO),
+            "cp_o": lambda tick: of_groups(copy_o, tick, L_CPO),
+            "q23": q23,
+            "q_e": lambda tick: of_pair(quantise_e, tick, L_QE),
+            "attend": lambda tick: of_pair(attend_values, tick, L_ATT),
+            "project": jobs,
+            "trw": lambda tick: of_units(transpose_weights, tick, 0),
+            "bias": biases,
+            "q_o": lambda tick: of_groups(quantise_o, tick, L_QO),
+            "scale": lambda tick: of_bank(scale_maxima, tick, 0),
+        }
+        ORDER = ("exp", "cpw", "norm", "prep", "qw", "q_o", "inv", "bias", "score", "tr_e", "trw", "warm", "tr_o", "maxima", "cp_o", "cp_e", "q_e", "q1", "q23", "attend", "project", "scale")
         last_tile = Q_TILES - 1
-        normalise(last - 3)
-        invert_row_sums(last - 2)
-        for late in range(2 * PAIRS - EXP_LAG, 2 * PAIRS):
-            exponentials(late // 2, late % 2)
-        transpose_e(last - 1)
-        copy_e(last - 1)
-        attend_values(last - 2)
-        for qt, n_slice, y_ps in y_waiting:
-            add_bias_and_store(qt, n_slice, y_ps)
-        y_waiting = []
-        quantise_e(last - 1)
-        invert_row_sums(last - 1)
-        for group in groups_ended(last - 4):
-            quantise_o(group)
-        for qt, n_slice in to_project[0:1]:
-            y_waiting.append((qt, n_slice, project_slice(qt, n_slice)))
-        transpose_e(last)
-        copy_e(last)
-        normalise(last - 2)
-        quantise_e(last)
-        invert_row_sums(last)
-        attend_values(last - 1)
-        for group in groups_ended(last - 2):
-            transpose_o(group)
-            copy_o(group)
-        for qt, n_slice in to_project[1:]:
-            y_waiting.append((qt, n_slice, project_slice(qt, n_slice)))
-        attend_values(last)
-        for group in groups_ended(last - 2):
-            quantise_o(group)
-        normalise(last - 1)
-        normalise(last)
-        for qt, n_slice, y_ps in y_waiting:
-            add_bias_and_store(qt, n_slice, y_ps)
+        for tick in range(2 * PAIRS - 1 + L_NORM):
+            for stage in ORDER:
+                stages[stage](tick)
+        for qt, n_slice in to_project:
+            add_bias_and_store(qt, n_slice, project_slice(qt, n_slice))
+        for job in y_waiting:
+            add_bias_and_store(*job[1:])
         last_y = []
         for n_slice in range(N_SLICES):
             y_ps = psum_b.tile([P, BANK_F32], F32, name="last_y", tag="bank")
@@ -711,10 +677,10 @@ def tile_groupqueryattention_pa_kernel(tc, q, k, v, causal_mask, padding_mask, W
         for g in range(TAIL_EARLY):
             for n_slice in range(N_SLICES):
                 project(last_tile, n_slice, g, last_y[n_slice])
-        for group in groups_ended(last):
-            transpose_o(group)
-            copy_o(group)
-            quantise_o(group)
+        last_group = (last_tile, GROUPS - 1)
+        transpose_o(last_group)
+        copy_o(last_group)
+        quantise_o(last_group)
         half = N_SLICES // 2
         for slices, groups in (
             (range(N_SLICES), range(TAIL_EARLY, GROUPS - 2)),

@@ -55,9 +55,11 @@ W_COPY_LAG = 1
 W_QUANT_LAG = 2
 Q_EARLY = 2
 W_DOUBLE = 0
-WARM_TICKS = range(12, 18, 2)
-BIAS_TICK = 8
-WARM_HEAD = 4
+WARM_TICKS = range(0)
+BIAS_TICK = 3
+BIAS_STEP = 2
+FIRST_QUERIES = ((), ((1, 0), (1, 1)))
+WARM_HEAD = 2
 TAIL_EARLY = 1
 JOBS_A_STEP = 1
 VECTOR_UNITS = 4
@@ -113,6 +115,10 @@ def heads_leaving(pair):
     return [(group, [0, 1]) for group in groups_ended(pair)]
 
 
+def pieces(pair):
+    return [slice(0, 1), slice(1, 2)] if pair == PAIRS - 1 else [slice(0, 2)]
+
+
 def tile_groupqueryattention_pa_kernel(tc, q, k, v, causal_mask, padding_mask, Wo, bo, out):
     nc = tc.nc
     with ExitStack() as ctx:
@@ -139,13 +145,14 @@ def tile_groupqueryattention_pa_kernel(tc, q, k, v, causal_mask, padding_mask, W
             wo_raw.append(w_tile)
         nc.sync.dma_start(out=q_raw[0][:, 0 : HID // 2], in_=q[0, 0:P, 0 : HID // 2])
         nc.sync.dma_start(out=pad_row[0:1, :], in_=padding_mask[0:1, :])
+        nc.sync.dma_start(out=bias_row[0:1, :], in_=bo.unsqueeze(0))
         causal_raw = keep.tile([P, HALF], BF16)
         for cls in range(2):
             nc.sync.dma_start(
                 out=causal_raw[cls * HALF : (cls + 1) * HALF, :], in_=causal_mask[0, 0, 0:HALF, 0:HALF]
             )
-        nc.sync.dma_start(out=k_raw[:, 1:, :], in_=k[0, P:, :].rearrange("(t p) d -> p t d", p=P))
         nc.sync.dma_start(out=q_raw[0][:, HID // 2 :], in_=q[0, 0:P, HID // 2 :])
+        nc.sync.dma_start(out=k_raw[:, 1:, :], in_=k[0, P:, :].rearrange("(t p) d -> p t d", p=P))
         v_raw_of = {}
         for n in (4, 2, 1):
             v_raw = keep.tile([P, 4, P], BF16, name="v_raw%d" % n)
@@ -160,7 +167,6 @@ def tile_groupqueryattention_pa_kernel(tc, q, k, v, causal_mask, padding_mask, W
                 )
 
         nc.sync.dma_start(out=q_raw[1][:], in_=q[0, P : 2 * P, :])
-        nc.sync.dma_start(out=bias_row[0:1, :], in_=bo.unsqueeze(0))
         for n in (4, 2, 1):
             load_v(n)
         for n_slice in range(N_SLICES):
@@ -225,21 +231,29 @@ def tile_groupqueryattention_pa_kernel(tc, q, k, v, causal_mask, padding_mask, W
 
         diagonal_neg = keep.tile([P, 2, S // 2], BF16)
         pad_neg = keep.tile([P, 2, S // 2], BF16)
+        pad_ps_of = {}
         mask_of = []
         for s in range(SUB_BLOCKS):
             mask = keep.tile([P, 2, (s + 1) * SUB], BF16, name="mask%d" % s)
             mask_of.append(mask)
 
-        def make_diagonal_masks():
+        def spread_padding():
             pad_ps = psum_b.tile([P, S], F32, tag="bank")
             nc.tensor.matmul(pad_ps[:], lhsT=first_row[:], rhs=pad_row[:], start=True, stop=True)
+            pad_ps_of["all"] = pad_ps
+
+        def make_diagonal_masks(first, end):
+            pad_ps = pad_ps_of["all"]
             for u in range(2):
                 nc.vector.tensor_tensor(
-                    out=half_block(diagonal_neg, 0, SUB_BLOCKS, u),
-                    in0=half_read(causal_raw[:], 0, 1, u).to_broadcast([P, SUB_BLOCKS, HALF // 4, 2]),
-                    in1=half_read(pad_ps[:], 0, SUB_BLOCKS, u),
+                    out=half_block(diagonal_neg, first, end, u),
+                    in0=half_read(causal_raw[:], 0, 1, u).to_broadcast([P, end - first, HALF // 4, 2]),
+                    in1=half_read(pad_ps[:], first, end, u),
                     op=ALU.add,
                 )
+
+        def make_padding_masks():
+            pad_ps = pad_ps_of["all"]
             for u in range(2):
                 nc.vector.tensor_scalar_mul(
                     half_block(pad_neg, 0, SUB_BLOCKS, u), half_read(pad_ps[:], 0, SUB_BLOCKS, u), NEG
@@ -407,16 +421,23 @@ def tile_groupqueryattention_pa_kernel(tc, q, k, v, causal_mask, padding_mask, W
 
         def copy_e(pair):
             e_grouped = work.tile([P, 2 * P * 4], BF16, align_bytes=64)
-            nc.scalar.copy(
-                out=e_grouped[:].bitcast(F32).rearrange("p (t r u) -> p t r u", t=2, u=2),
-                in_=eT_ps_of[pair][:].rearrange("p t u r -> p t r u"),
-            )
+            for ts in pieces(pair):
+                nc.scalar.copy(
+                    out=e_grouped[:].bitcast(F32).rearrange("p (t r u) -> p t r u", t=2, u=2)[:, ts],
+                    in_=eT_ps_of[pair][:].rearrange("p t u r -> p t r u")[:, ts],
+                )
             e_grouped_of[pair] = e_grouped
 
         def quantise_e(pair):
             e_codes = work.tile([P, 2 * P], U32, align_bytes=64)
             e_scales = work.tile([P, 2 * P], U8, align_bytes=64)
-            nc.vector.quantize_mx(out=e_codes[:].bitcast(FP8X4), scales=e_scales[:], in_=e_grouped_of[pair][:])
+            for ts in pieces(pair):
+                cols = slice(ts.start * P, ts.stop * P)
+                nc.vector.quantize_mx(
+                    out=e_codes[:, cols].bitcast(FP8X4),
+                    scales=e_scales[:, cols],
+                    in_=e_grouped_of[pair][:, 4 * ts.start * P : 4 * ts.stop * P],
+                )
             e_codes_of[pair] = (e_codes, e_scales)
 
         def attend_values(pair):
@@ -457,12 +478,15 @@ def tile_groupqueryattention_pa_kernel(tc, q, k, v, causal_mask, padding_mask, W
                     o_sb_new = work.tile([P, GROUP * P], BF16, name="o_sb", bufs=4)
                     o_sb_of[group] = o_sb_new
                 cols = slice(couples[0], couples[-1] + 1)
-                nc.vector.tensor_tensor(
-                    out=o_sb_of[group][:].rearrange("p (t m d) -> p t m d", t=2, m=2)[:, :, cols, :],
-                    in0=o_ps_of[group][:, :, cols, :],
-                    in1=recip_of[group][:, :, cols].unsqueeze(3).to_broadcast([P, 2, len(couples), P]),
-                    op=ALU.mult,
-                )
+                for ts in pieces(pair):
+                    nc.vector.tensor_tensor(
+                        out=o_sb_of[group][:].rearrange("p (t m d) -> p t m d", t=2, m=2)[:, ts, cols, :],
+                        in0=o_ps_of[group][:, ts, cols, :],
+                        in1=recip_of[group][:, ts, cols]
+                        .unsqueeze(3)
+                        .to_broadcast([P, ts.stop - ts.start, len(couples), P]),
+                        op=ALU.mult,
+                    )
 
         def transpose_o(group):
             o_words = o_sb_of[group][:].bitcast(F32)
@@ -473,10 +497,11 @@ def tile_groupqueryattention_pa_kernel(tc, q, k, v, causal_mask, padding_mask, W
 
         def copy_o(group):
             o_grouped = work.tile([P, P * 4], BF16, align_bytes=64, bufs=4)
-            nc.scalar.copy(
-                out=o_grouped[:].bitcast(F32).rearrange("p (t q u) -> p t q u", t=2, u=2),
-                in_=oT_ps_of[group][:].rearrange("p t (u q) -> p t q u", u=2),
-            )
+            for ts in pieces(PAIRS - 1 if group == (Q_TILES - 1, GROUPS - 1) else 0):
+                nc.scalar.copy(
+                    out=o_grouped[:].bitcast(F32).rearrange("p (t q u) -> p t q u", t=2, u=2)[:, ts],
+                    in_=oT_ps_of[group][:].rearrange("p t (u q) -> p t q u", u=2)[:, ts],
+                )
             o_grouped_of[group] = o_grouped
 
         def quantise_o(group):
@@ -549,10 +574,14 @@ def tile_groupqueryattention_pa_kernel(tc, q, k, v, causal_mask, padding_mask, W
             )
 
         def add_bias_and_store(qt, n_slice, y_ps):
-            n_cols = slice(n_slice * BANK_F32, (n_slice + 1) * BANK_F32)
             y_sb = work.tile([P, BANK_F32], F32, bufs=6)
-            nc.vector.tensor_tensor(out=y_sb[:], in0=y_ps[:], in1=bias_all[:, n_cols], op=ALU.add)
-            nc.sync.dma_start(out=out[0, qt * P : (qt + 1) * P, n_cols], in_=y_sb[:])
+            n_parts = 2 if (qt, n_slice) == (Q_TILES - 1, N_SLICES - 1) else 1
+            width = BANK_F32 // n_parts
+            for i in range(n_parts):
+                part = slice(i * width, (i + 1) * width)
+                n_cols = slice(n_slice * BANK_F32 + i * width, n_slice * BANK_F32 + (i + 1) * width)
+                nc.vector.tensor_tensor(out=y_sb[:, part], in0=y_ps[:, part], in1=bias_all[:, n_cols], op=ALU.add)
+                nc.sync.dma_start(out=out[0, qt * P : (qt + 1) * P, n_cols], in_=y_sb[:, part])
 
         def may_project(qt, n_slice, tick):
             last_pair = FIRST_PAIR[qt] + PAIRS_IN_TILE[qt] - 1
@@ -566,11 +595,14 @@ def tile_groupqueryattention_pa_kernel(tc, q, k, v, causal_mask, padding_mask, W
         transpose_keys(0, 1)
         transpose_queries(0, 0)
         copy_queries(0, 0)
-        make_diagonal_masks()
-        for s in range(2):
-            make_mask(s)
+        spread_padding()
         transpose_queries(0, 1)
         copy_queries(0, 1)
+        make_diagonal_masks(0, 1)
+        make_mask(0)
+        make_padding_masks()
+        make_diagonal_masks(1, SUB_BLOCKS)
+        make_mask(1)
         def of_pair(stage, tick, lag):
             pair, odd = divmod(tick - lag, 2)
             if odd == 0 and due(pair, PAIRS):
@@ -606,10 +638,10 @@ def tile_groupqueryattention_pa_kernel(tc, q, k, v, causal_mask, padding_mask, W
                     prepare(*argument)
 
         def q1(tick):
-            if tick == 1:
-                for half in range(2):
-                    transpose_queries(1, half)
-                    copy_queries(1, half)
+            if due(tick, len(FIRST_QUERIES)):
+                for qt, half in FIRST_QUERIES[tick]:
+                    transpose_queries(qt, half)
+                    copy_queries(qt, half)
 
         def q23(tick):
             for qt in range(2, Q_TILES):
@@ -619,8 +651,8 @@ def tile_groupqueryattention_pa_kernel(tc, q, k, v, causal_mask, padding_mask, W
                     copy_queries(qt, half)
 
         def warm(tick):
-            half, odd = divmod(tick - BIAS_TICK, 2)
-            if odd == 0 and due(half, 2):
+            half, rest = divmod(tick - BIAS_TICK, BIAS_STEP)
+            if rest == 0 and due(half, 2):
                 spread_bias(half)
             if tick in WARM_TICKS:
                 keep_warm(kT[:].rearrange("p u c -> p (u c)"), 1)

import math
from contextlib import ExitStack

import concourse.mybir as mybir
from concourse.masks import make_identity

BF16 = mybir.dt.bfloat16
F32 = mybir.dt.float32
U32 = mybir.dt.uint32
U8 = mybir.dt.uint8
FP8X4 = mybir.dt.float8_e4m3fn_x4
ALU = mybir.AluOpType
ACT = mybir.ActivationFunctionType

P = 128
S = 512
HEADS = 16
HID = HEADS * P
Q_TILES = S // P
GROUP = 4
GROUPS = HEADS // GROUP
BANK_F32 = 512
N_SLICES = HID // BANK_F32
NEG = -1.0e9
SCALE = 1.0 / math.sqrt(P)
SUB = 32
QUARTERS = P // SUB
HALF = P // 2
SUB_BLOCKS = S // HALF
E_TILES = 3
HEADS_PER_PASS = (4, 2, 1, 1)
PAIRS_IN_TILE = tuple(HEADS // (2 * n) for n in HEADS_PER_PASS)
FIRST_PAIR = tuple(sum(PAIRS_IN_TILE[:qt]) for qt in range(Q_TILES))
PAIRS = sum(PAIRS_IN_TILE)
WEIGHT_UNITS = HID // (2 * P) * GROUPS
KEYS_TICK = 1
V_TICK = 2
PREPARE_A_TICK = 2
EXP_LAG = 2
L_TRE = 4
L_CPE = 4
L_QE = 5
L_INV = 6
L_ATT = 7
L_NORM = 8
L_TRO = 9
L_CPO = 9
L_QO = 10
L_PROJECT = 11
JOB_PARITY = 1
L_BIAS = 1
L_Q23 = 4
WEIGHT_START = 7
W_COPY_LAG = 1
W_QUANT_LAG = 2
Q_EARLY = 2
W_DOUBLE = 0
WARM_TICKS = range(0)
BIAS_TICK = 3
BIAS_STEP = 2
FIRST_QUERIES = ((), ((1, 0), (1, 1)))
WARM_HEAD = 2
TAIL_EARLY = 1
JOBS_A_STEP = 1
VECTOR_UNITS = 4
VECTOR_QUERY_TILES = ()
SCALAR_NORMALISE = ()

FLOPS = 2 * 2 * HEADS * S * S * P + 2 * S * HID * HID


def units_of(tick):
    n = tick - WEIGHT_START
    if n < 0:
        return []
    first = 2 * min(n, W_DOUBLE) + max(0, n - W_DOUBLE)
    return [u for u in range(first, first + (2 if n < W_DOUBLE else 1)) if u < WEIGHT_UNITS]


def last_unit_by(tick):
    n = tick - WEIGHT_START
    return 2 * min(n, W_DOUBLE - 1) + 1 + max(0, n - W_DOUBLE + 1) if n < W_DOUBLE else 2 * W_DOUBLE + n - W_DOUBLE


def due(index, count):
    return 0 <= index < count


def tile_of_pair(pair):
    return max(qt for qt in range(Q_TILES) if FIRST_PAIR[qt] <= pair)


def couples_of_pair(pair):
    qt = tile_of_pair(pair)
    n = HEADS_PER_PASS[qt]
    first = (pair - FIRST_PAIR[qt]) * n
    return list(range(first, first + n))


def head_of(couple, cls):
    return couple // 2 * GROUP + couple % 2 + 2 * cls


def groups_ended(pair):
    if not due(pair, PAIRS):
        return []
    return [(tile_of_pair(pair), couple // 2) for couple in couples_of_pair(pair) if couple % 2 == 1]


def heads_leaving(pair):
    qt = tile_of_pair(pair)
    couples = couples_of_pair(pair)
    if (qt, couples[0] // 2) == (Q_TILES - 1, GROUPS - 1):
        return [((qt, GROUPS - 1), [couples[0] % 2])]
    return [(group, [0, 1]) for group in groups_ended(pair)]


def pieces(pair):
    return [slice(0, 1), slice(1, 2)] if pair == PAIRS - 1 else [slice(0, 2)]


def tile_groupqueryattention_pa_kernel(tc, q, k, v, causal_mask, padding_mask, Wo, bo, out):
    nc = tc.nc
    with ExitStack() as ctx:
        keep = ctx.enter_context(tc.tile_pool(name="keep", bufs=1))
        work = ctx.enter_context(tc.tile_pool(name="work", bufs=3))
        stats = ctx.enter_context(tc.tile_pool(name="stats", bufs=4))
        psum_b = ctx.enter_context(tc.psum_pool(name="psum_b", bufs=8))

        pad_row = keep.tile([P, S], BF16)
        nc.vector.memset(pad_row[:].bitcast(F32), 0.0)
        zeros = keep.tile([P, S], BF16)
        nc.vector.memset(zeros[:].bitcast(F32), 0.0)
        bias_row = keep.tile([P, HID], BF16)
        nc.vector.memset(bias_row[:].bitcast(F32), 0.0)
        k_raw = keep.tile([P, Q_TILES, P], BF16)
        nc.sync.dma_start(out=k_raw[:, 0, :], in_=k[0, 0:P, :])
        q_raw = []
        for qt in range(Q_TILES):
            q_tile = keep.tile([P, HID], BF16, name="q_raw%d" % qt)
            q_raw.append(q_tile)
        wo_raw = []
        for nt in range(HID // P):
            w_tile = keep.tile([P, HID], BF16, name="wo_raw%d" % nt)
            wo_raw.append(w_tile)
        nc.sync.dma_start(out=q_raw[0][:, 0 : HID // 2], in_=q[0, 0:P, 0 : HID // 2])
        nc.sync.dma_start(out=pad_row[0:1, :], in_=padding_mask[0:1, :])
        nc.sync.dma_start(out=bias_row[0:1, :], in_=bo.unsqueeze(0))
        causal_raw = keep.tile([P, HALF], BF16)
        for cls in range(2):
            nc.sync.dma_start(
                out=causal_raw[cls * HALF : (cls + 1) * HALF, :], in_=causal_mask[0, 0, 0:HALF, 0:HALF]
            )
        nc.sync.dma_start(out=q_raw[0][:, HID // 2 :], in_=q[0, 0:P, HID // 2 :])
        nc.sync.dma_start(out=k_raw[:, 1:, :], in_=k[0, P:, :].rearrange("(t p) d -> p t d", p=P))
        v_raw_of = {}
        for n in (4, 2, 1):
            v_raw = keep.tile([P, 4, P], BF16, name="v_raw%d" % n)
            v_raw_of[n] = v_raw

        def load_v(n):
            rows = P // n
            for i in range(n):
                nc.sync.dma_start(
                    out=v_raw_of[n][i * rows : (i + 1) * rows].rearrange("p t d -> p (t d)"),
                    in_=v[0, 0 : 4 * rows].rearrange("(p t) d -> p (t d)", t=4),
                )

        nc.sync.dma_start(out=q_raw[1][:], in_=q[0, P : 2 * P, :])
        for n in (4, 2, 1):
            load_v(n)
        for n_slice in range(N_SLICES):
            for i in range(4):
                nt = 4 * n_slice + i
                nc.sync.dma_start(out=wo_raw[nt][:], in_=Wo[nt * P : (nt + 1) * P, :])
            qt = n_slice + 2
            if qt < Q_TILES:
                nc.sync.dma_start(out=q_raw[qt][:], in_=q[0, qt * P : (qt + 1) * P, :])

        first_row = keep.tile([P, P], BF16)
        nc.vector.memset(first_row[:], 0.0)
        nc.vector.memset(first_row[0:1, :], 1.0)
        bias_all = keep.tile([P, HID], BF16)
        ident_bf = keep.tile([P, P], BF16)
        make_identity(nc, ident_bf[:])
        ident_f32 = keep.tile([P, P], F32)
        make_identity(nc, ident_f32[:])
        v_codes_of = {}
        for n in (4, 2, 1):
            v_codes = keep.tile([P, n * P], U32, align_bytes=64, name="v_codes%d" % n)
            if n > 1:
                nc.vector.memset(v_codes[:], 0)
            v_codes_of[n] = v_codes
        e_of_tile = {}
        for qt in range(Q_TILES):
            engine = nc.vector if qt == 0 else nc.gpsimd
            blocks = qt + 1
            couples = HEADS_PER_PASS[qt]
            for i in range(E_TILES):
                e_tile = keep.tile([P, 2 * S], BF16, name="e%d_%d" % (qt, i))
                e_words = e_tile[:].bitcast(F32).rearrange("p (t u s c) -> p t u s c", t=2, u=2, s=SUB_BLOCKS)
                engine.memset(e_words[:, 0, :, 2 * blocks - 1 : 2 * blocks * couples : 2 * blocks, :], 0.0)
                if couples * blocks < QUARTERS:
                    for t in range(2):
                        engine.memset(e_words[:, t, :, 2 * blocks * couples :, :], 0.0)
                e_of_tile[qt, i] = e_tile

        kT = keep.tile([P, 2, S // 2], BF16)

        def half_block(tile, first, end, u):
            return tile[:, u, first * SUB : end * SUB].rearrange("p (s w e) -> p s w e", w=HALF // 4, e=2)

        def half_read(ap, first, end, u):
            return ap.rearrange("p (s w u e) -> p s w u e", w=HALF // 4, u=2, e=2)[:, first:end, :, u, :]

        def keep_warm(moving, count):
            for i in range(count):
                unread = psum_b.tile([P, S], F32, tag="bank")
                nc.tensor.matmul(unread[:], lhsT=moving[:, 0:P], rhs=moving[:, 0:S], start=True, stop=True)

        def transpose_keys(first, end):
            kT_ps = psum_b.tile([P, Q_TILES, P], BF16, tag="bank")
            for t in range(first, end):
                nc.tensor.transpose(kT_ps[:, t, :], k_raw[:, t, :], ident_bf[:])
            kT_cols = kT_ps[:].rearrange("p t c -> p (t c)")
            copy = nc.vector.tensor_copy if first == 0 else nc.scalar.copy
            for u in range(2):
                copy(
                    out=half_block(kT, 2 * first, 2 * end, u), in_=half_read(kT_cols, 2 * first, 2 * end, u)
                )

        diagonal_neg = keep.tile([P, 2, S // 2], BF16)
        pad_neg = keep.tile([P, 2, S // 2], BF16)
        pad_ps_of = {}
        mask_of = []
        for s in range(SUB_BLOCKS):
            mask = keep.tile([P, 2, (s + 1) * SUB], BF16, name="mask%d" % s)
            mask_of.append(mask)

        def spread_padding():
            pad_ps = psum_b.tile([P, S], F32, tag="bank")
            nc.tensor.matmul(pad_ps[:], lhsT=first_row[:], rhs=pad_row[:], start=True, stop=True)
            pad_ps_of["all"] = pad_ps

        def make_diagonal_masks(first, end):
            pad_ps = pad_ps_of["all"]
            for u in range(2):
                nc.vector.tensor_tensor(
                    out=half_block(diagonal_neg, first, end, u),
                    in0=half_read(causal_raw[:], 0, 1, u).to_broadcast([P, end - first, HALF // 4, 2]),
                    in1=half_read(pad_ps[:], first, end, u),
                    op=ALU.add,
                )

        def make_padding_masks():
            pad_ps = pad_ps_of["all"]
            for u in range(2):
                nc.vector.tensor_scalar_mul(
                    half_block(pad_neg, 0, SUB_BLOCKS, u), half_read(pad_ps[:], 0, SUB_BLOCKS, u), NEG
                )

        def make_mask(s):
            left = s * SUB
            nc.vector.tensor_scalar_mul(mask_of[s][:, :, left:], diagonal_neg[:, :, left : left + SUB], NEG)
            if s > 0:
                nc.vector.tensor_copy(out=mask_of[s][:, :, 0:left], in_=pad_neg[:, :, 0:left])

        v_scales_of = {}
        v_grouped_of = {}
        v_dense_of = {}
        o_codes = keep.tile([P, GROUPS * S], U32, align_bytes=64)
        o_scales = keep.tile([P, GROUPS * S], U8, align_bytes=64)
        w_codes = keep.tile([P, GROUPS * HID], U32, align_bytes=64)
        w_scales = keep.tile([P, GROUPS * HID], U8, align_bytes=64)

        qT_of = {}
        qT_ps_of = {}
        scores_of = {}
        top_of = {}
        shift_of = {}
        recip_of = {}
        eT_ps_of = {}
        oT_ps_of = {}
        wT_ps_of = {}
        rowsum_of = {}
        e_pair_of = {}
        e_grouped_of = {}
        e_codes_of = {}
        o_ps_of = {}
        o_sb_of = {}
        o_grouped_of = {}
        w_grouped_of = {}

        def group_v(n):
            v_grouped = work.tile([P, P * 4], BF16, align_bytes=64, bufs=2)
            nc.vector.tensor_copy(
                out=v_grouped[:].rearrange("p (d t) -> p d t", t=4), in_=v_raw_of[n][:].rearrange("p t d -> p d t")
            )
            v_grouped_of[n] = v_grouped

        def quantise_v(n):
            v_scales = keep.tile([P, P], U8, align_bytes=64, name="v_scales%d" % n)
            v_dense = v_codes_of[1]
            if n > 1:
                v_dense = keep.tile([P, P], U32, align_bytes=64, name="v_dense%d" % n)
            nc.vector.quantize_mx(out=v_dense[:].bitcast(FP8X4), scales=v_scales[:], in_=v_grouped_of[n][:])
            v_scales_of[n] = v_scales
            v_dense_of[n] = v_dense

        def spread_v(n):
            for head in range(n):
                part = slice(head * P // n, (head + 1) * P // n)
                nc.vector.tensor_copy(
                    out=v_codes_of[n][part, head * P : (head + 1) * P], in_=v_dense_of[n][part]
                )

        def transpose_queries(qt, half):
            if half == 0:
                qT_new = work.tile([P, HID], BF16, name="qT", bufs=2)
                qT_of[qt] = qT_new
            qT_ps = psum_b.tile([P, 2, 8, HALF], BF16, tag="bank")
            for cls in range(2):
                for i in range(4):
                    h = head_of(4 * half + i, cls)
                    nc.tensor.transpose(
                        qT_ps[:, cls, 2 * i : 2 * i + 2].rearrange("p t q -> p (t q)"), q_raw[qt][:, h * P : (h + 1) * P], ident_bf[:]
                    )
            qT_ps_of[qt] = qT_ps

        def copy_queries(qt, half):
            copy = nc.vector.tensor_copy if qt in VECTOR_QUERY_TILES else nc.scalar.copy
            copy(
                out=qT_of[qt][:, half * 8 * P : (half + 1) * 8 * P].rearrange("p (x c q) -> p c x q", c=2, q=HALF),
                in_=qT_ps_of[qt][:],
            )

        def score(pair, t):
            qt = tile_of_pair(pair)
            couples = couples_of_pair(pair)
            n_keys = (2 * qt + t + 1) * HALF
            scores = psum_b.tile([P, len(couples), n_keys], F32, tag="bank")
            for a, couple in enumerate(couples):
                first = (2 * couple + t) * P
                nc.tensor.matmul(
                    scores[:, a, :],
                    lhsT=qT_of[qt][:, first : first + P],
                    rhs=kT[:, :, 0 : n_keys // 2],
                    start=True,
                    stop=False,
                )
                nc.tensor.matmul(
                    scores[:, a, :],
                    lhsT=ident_bf[:],
                    rhs=mask_of[2 * qt + t][:].rearrange("p u c -> p (u c)"),
                    start=False,
                    stop=True,
                )
            scores_of[pair, t] = scores

        def row_maxima(pair, t):
            n = len(couples_of_pair(pair))
            if n == 1:
                shift = stats.tile([P, 1], F32, tag="shift1")
                scaled = work.tile([P, BANK_F32], BF16, bufs=2)
                nc.vector.tensor_scalar(
                    out=scaled[:, 0 : scores_of[pair, t][:].shape[2]],
                    in0=scores_of[pair, t][:, 0, :],
                    scalar1=-SCALE,
                    scalar2=None,
                    op0=ALU.mult,
                    op1=ALU.min,
                    accum_out=shift[:],
                )
                shift_of[pair, t] = shift
                return
            top = stats.tile([P, n], F32, tag="top%d" % n)
            nc.vector.tensor_reduce(out=top[:], in_=scores_of[pair, t][:], axis=mybir.AxisListType.X, op=ALU.max)
            top_of[pair, t] = top

        def scale_maxima(pair, t):
            n = len(couples_of_pair(pair))
            if n == 1:
                return
            shift = stats.tile([P, n], F32, tag="shift%d" % n)
            nc.gpsimd.tensor_scalar(
                out=shift[:], in0=top_of[pair, t][:], scalar1=-SCALE, scalar2=0.0, op0=ALU.mult, op1=ALU.add
            )
            shift_of[pair, t] = shift

        def exponentials(pair, t):
            qt = tile_of_pair(pair)
            blocks = qt + 1
            n_subs = 2 * qt + 1 + t
            if t == 0:
                e_pair_of[pair] = e_of_tile[qt, pair % E_TILES]
            e_view = e_pair_of[pair][:].rearrange("p (t u c) -> p t u c", t=2, u=2)
            for a, couple in enumerate(couples_of_pair(pair)):
                group = (qt, couple // 2)
                if group not in rowsum_of:
                    rowsum = stats.tile([P, 4], F32, bufs=9)
                    rowsum_of[group] = rowsum
                col = 2 * t + couple % 2
                first = 2 * blocks * a * SUB
                nc.scalar.activation(
                    out=e_view[:, t, :, first : first + n_subs * SUB],
                    in_=scores_of[pair, t][:, a, :].rearrange("p (u c) -> p u c", u=2),
                    func=ACT.Exp,
                    bias=shift_of[pair, t][:, a : a + 1],
                    scale=SCALE,
                    accum_out=rowsum_of[group][:, col : col + 1],
                )

        def transpose_e(pair):
            e_words = e_pair_of[pair][:].bitcast(F32)
            eT_ps = psum_b.tile([P, 2, 2, P], F32, tag="bank")
            for t in range(2):
                for u in range(2):
                    first_word = (2 * t + u) * P
                    nc.tensor.transpose(eT_ps[:, t, u, :], e_words[:, first_word : first_word + P], ident_f32[:])
            eT_ps_of[pair] = eT_ps

        def copy_e(pair):
            e_grouped = work.tile([P, 2 * P * 4], BF16, align_bytes=64)
            for ts in pieces(pair):
                nc.scalar.copy(
                    out=e_grouped[:].bitcast(F32).rearrange("p (t r u) -> p t r u", t=2, u=2)[:, ts],
                    in_=eT_ps_of[pair][:].rearrange("p t u r -> p t r u")[:, ts],
                )
            e_grouped_of[pair] = e_grouped

        def quantise_e(pair):
            e_codes = work.tile([P, 2 * P], U32, align_bytes=64)
            e_scales = work.tile([P, 2 * P], U8, align_bytes=64)
            for ts in pieces(pair):
                cols = slice(ts.start * P, ts.stop * P)
                nc.vector.quantize_mx(
                    out=e_codes[:, cols].bitcast(FP8X4),
                    scales=e_scales[:, cols],
                    in_=e_grouped_of[pair][:, 4 * ts.start * P : 4 * ts.stop * P],
                )
            e_codes_of[pair] = (e_codes, e_scales)

        def attend_values(pair):
            qt = tile_of_pair(pair)
            n = HEADS_PER_PASS[qt]
            e_codes, e_scales = e_codes_of[pair]
            for a, couple in enumerate(couples_of_pair(pair)):
                group = (qt, couple // 2)
                if group not in o_ps_of:
                    o_ps = psum_b.tile([P, 2, 2, P], F32, tag="bank")
                    o_ps_of[group] = o_ps
            for t in range(2):
                for a, couple in enumerate(couples_of_pair(pair)):
                    nc.tensor.matmul_mx(
                        out=o_ps_of[qt, couple // 2][:, t, couple % 2, :],
                        lhsT=e_codes[:, t * P : (t + 1) * P].bitcast(FP8X4),
                        lhsT_scale=e_scales[:, t * P : (t + 1) * P],
                        rhs=v_codes_of[n][:, a * P : (a + 1) * P].bitcast(FP8X4),
                        rhs_scale=v_scales_of[n][:],
                        start=True,
                        stop=True,
                    )

        def invert_row_sums(pair):
            for group, couples in heads_leaving(pair):
                if group not in recip_of:
                    recip = stats.tile([P, 2, 2], F32, bufs=6)
                    recip_of[group] = recip
                cols = slice(couples[0], couples[-1] + 1)
                nc.vector.reciprocal(
                    recip_of[group][:, :, cols],
                    rowsum_of[group][:].rearrange("p (t m) -> p t m", t=2)[:, :, cols],
                )

        def normalise(pair):
            for group, couples in heads_leaving(pair):
                if group not in o_sb_of:
                    o_sb_new = work.tile([P, GROUP * P], BF16, name="o_sb", bufs=4)
                    o_sb_of[group] = o_sb_new
                cols = slice(couples[0], couples[-1] + 1)
                for ts in pieces(pair):
                    nc.vector.tensor_tensor(
                        out=o_sb_of[group][:].rearrange("p (t m d) -> p t m d", t=2, m=2)[:, ts, cols, :],
                        in0=o_ps_of[group][:, ts, cols, :],
                        in1=recip_of[group][:, ts, cols]
                        .unsqueeze(3)
                        .to_broadcast([P, ts.stop - ts.start, len(couples), P]),
                        op=ALU.mult,
                    )

        def transpose_o(group):
            o_words = o_sb_of[group][:].bitcast(F32)
            oT_ps = psum_b.tile([P, 2, P], F32, tag="bank")
            for t in range(2):
                nc.tensor.transpose(oT_ps[:, t, :], o_words[:, t * P : (t + 1) * P], ident_f32[:])
            oT_ps_of[group] = oT_ps

        def copy_o(group):
            o_grouped = work.tile([P, P * 4], BF16, align_bytes=64, bufs=4)
            for ts in pieces(PAIRS - 1 if group == (Q_TILES - 1, GROUPS - 1) else 0):
                nc.scalar.copy(
                    out=o_grouped[:].bitcast(F32).rearrange("p (t q u) -> p t q u", t=2, u=2)[:, ts],
                    in_=oT_ps_of[group][:].rearrange("p t (u q) -> p t q u", u=2)[:, ts],
                )
            o_grouped_of[group] = o_grouped

        def quantise_o(group):
            qt, g = group
            cols = slice(g * S + qt * P, g * S + (qt + 1) * P)
            nc.vector.quantize_mx(
                out=o_codes[:, cols].bitcast(FP8X4), scales=o_scales[:, cols], in_=o_grouped_of[group][:]
            )

        def transpose_weights(unit):
            row_pair, g = divmod(unit, GROUPS)
            wT_ps = psum_b.tile([P, 2, 2, P], F32, tag="bank")
            for i in range(2):
                words = wo_raw[2 * row_pair + i][:].bitcast(F32)
                for u in range(2):
                    first_word = g * 2 * P + u * P
                    nc.tensor.transpose(wT_ps[:, i, u, :], words[:, first_word : first_word + P], ident_f32[:])
            wT_ps_of[unit] = wT_ps

        def copy_weights(unit):
            w_grouped = work.tile([P, 2 * P * 4], BF16, align_bytes=64)
            copy = nc.vector.tensor_copy if unit % 2 == 1 and unit < VECTOR_UNITS else nc.scalar.copy
            copy(
                out=w_grouped[:].bitcast(F32).rearrange("p (i n u) -> p i n u", i=2, u=2),
                in_=wT_ps_of[unit][:].rearrange("p i u n -> p i n u"),
            )
            w_grouped_of[unit] = w_grouped

        def quantise_weights(unit):
            row_pair, g = divmod(unit, GROUPS)
            first = g * HID + row_pair * 2 * P
            nc.vector.quantize_mx(
                out=w_codes[:, first : first + 2 * P].bitcast(FP8X4),
                scales=w_scales[:, first : first + 2 * P],
                in_=w_grouped_of[unit][:],
            )

        def project(qt, n_slice, g, y_ps):
            o_cols = slice(g * S + qt * P, g * S + (qt + 1) * P)
            w_cols = slice(g * HID + n_slice * BANK_F32, g * HID + (n_slice + 1) * BANK_F32)
            nc.tensor.matmul_mx(
                out=y_ps[:],
                lhsT=o_codes[:, o_cols].bitcast(FP8X4),
                lhsT_scale=o_scales[:, o_cols],
                rhs=w_codes[:, w_cols].bitcast(FP8X4),
                rhs_scale=w_scales[:, w_cols],
                start=(g == 0),
                stop=(g == GROUPS - 1),
            )

        def project_slice(qt, n_slice):
            y_ps = psum_b.tile([P, BANK_F32], F32, tag="bank")
            for g in range(GROUPS):
                project(qt, n_slice, g, y_ps)
            return y_ps

        def spread_bias(half):
            bias_ps = psum_b.tile([P, 2, BANK_F32], BF16, tag="bank")
            for i in range(2):
                n_slice = 2 * half + i
                nc.tensor.matmul(
                    bias_ps[:, i, :],
                    lhsT=first_row[:],
                    rhs=bias_row[:, n_slice * BANK_F32 : (n_slice + 1) * BANK_F32],
                    start=True,
                    stop=True,
                )
            nc.scalar.copy(
                out=bias_all[:, half * HID // 2 : (half + 1) * HID // 2], in_=bias_ps[:].rearrange("p i n -> p (i n)")
            )

        def add_bias_and_store(qt, n_slice, y_ps):
            y_sb = work.tile([P, BANK_F32], F32, bufs=6)
            n_parts = 2 if (qt, n_slice) == (Q_TILES - 1, N_SLICES - 1) else 1
            width = BANK_F32 // n_parts
            for i in range(n_parts):
                part = slice(i * width, (i + 1) * width)
                n_cols = slice(n_slice * BANK_F32 + i * width, n_slice * BANK_F32 + (i + 1) * width)
                nc.vector.tensor_tensor(out=y_sb[:, part], in0=y_ps[:, part], in1=bias_all[:, n_cols], op=ALU.add)
                nc.sync.dma_start(out=out[0, qt * P : (qt + 1) * P, n_cols], in_=y_sb[:, part])

        def may_project(qt, n_slice, tick):
            last_pair = FIRST_PAIR[qt] + PAIRS_IN_TILE[qt] - 1
            units = (n_slice + 1) * WEIGHT_UNITS // N_SLICES
            return tick >= 2 * last_pair + L_PROJECT and last_unit_by(tick - W_QUANT_LAG) >= units - 1

        to_project = [(qt, n_slice) for qt in range(Q_TILES - 1) for n_slice in range(N_SLICES)]
        y_waiting = []
        ctx.enter_context(tc.manual_schedule())
        keep_warm(zeros[:], WARM_HEAD)
        transpose_keys(0, 1)
        transpose_queries(0, 0)
        copy_queries(0, 0)
        spread_padding()
        transpose_queries(0, 1)
        copy_queries(0, 1)
        make_diagonal_masks(0, 1)
        make_mask(0)
        make_padding_masks()
        make_diagonal_masks(1, SUB_BLOCKS)
        make_mask(1)
        def of_pair(stage, tick, lag):
            pair, odd = divmod(tick - lag, 2)
            if odd == 0 and due(pair, PAIRS):
                stage(pair)

        def of_groups(stage, tick, lag):
            pair, odd = divmod(tick - lag, 2)
            if odd == 0:
                for group in groups_ended(pair):
                    stage(group)

        def of_bank(stage, tick, lag):
            if due(tick - lag, 2 * PAIRS):
                stage((tick - lag) // 2, (tick - lag) % 2)

        def of_units(stage, tick, lag):
            for unit in units_of(tick - lag):
                stage(unit)

        preparations = [(make_mask, (2,)), (make_mask, (3,))]
        for n in (4, 2, 1):
            preparations += [(group_v, (n,)), (quantise_v, (n,))]
            if n > 1:
                preparations.append((spread_v, (n,)))
        preparations += [(make_mask, (s,)) for s in range(4, SUB_BLOCKS)]

        def prep(tick):
            if tick == KEYS_TICK:
                transpose_keys(1, Q_TILES)
            if tick >= V_TICK:
                first = (tick - V_TICK) * PREPARE_A_TICK
                for prepare, argument in preparations[first : first + PREPARE_A_TICK]:
                    prepare(*argument)

        def q1(tick):
            if due(tick, len(FIRST_QUERIES)):
                for qt, half in FIRST_QUERIES[tick]:
                    transpose_queries(qt, half)
                    copy_queries(qt, half)

        def q23(tick):
            for qt in range(2, Q_TILES):
                half, odd = divmod(tick - (2 * FIRST_PAIR[qt] - L_Q23 + 1), 2)
                if odd == 0 and due(half, 2):
                    transpose_queries(qt, half)
                    copy_queries(qt, half)

        def warm(tick):
            half, rest = divmod(tick - BIAS_TICK, BIAS_STEP)
            if rest == 0 and due(half, 2):
                spread_bias(half)
            if tick in WARM_TICKS:
                keep_warm(kT[:].rearrange("p u c -> p (u c)"), 1)

        def jobs(tick):
            if tick % 2 == JOB_PARITY:
                ready = [job for job in to_project if may_project(job[0], job[1], tick)]
                for qt, n_slice in ready[0:JOBS_A_STEP]:
                    to_project.remove((qt, n_slice))
                    y_waiting.append((tick, qt, n_slice, project_slice(qt, n_slice)))

        def biases(tick):
            for job in [job for job in y_waiting if job[0] <= tick - L_BIAS]:
                y_waiting.remove(job)
                add_bias_and_store(*job[1:])

        stages = {
            "prep": prep,
            "norm": lambda tick: of_pair(normalise, tick, L_NORM),
            "qw": lambda tick: of_units(quantise_weights, tick, W_QUANT_LAG),
            "score": lambda tick: of_bank(score, tick, 0),
            "maxima": lambda tick: of_bank(row_maxima, tick, 0),
            "inv": lambda tick: of_pair(invert_row_sums, tick, L_INV),
            "exp": lambda tick: of_bank(exponentials, tick, EXP_LAG),
            "q1": q1,
            "cpw": lambda tick: of_units(copy_weights, tick, W_COPY_LAG),
            "tr_e": lambda tick: of_pair(transpose_e, tick, L_TRE),
            "cp_e": lambda tick: of_pair(copy_e, tick, L_CPE),
            "warm": warm,
            "tr_o": lambda tick: of_groups(transpose_o, tick, L_TRO),
            "cp_o": lambda tick: of_groups(copy_o, tick, L_CPO),
            "q23": q23,
            "q_e": lambda tick: of_pair(quantise_e, tick, L_QE),
            "attend": lambda tick: of_pair(attend_values, tick, L_ATT),
            "project": jobs,
            "trw": lambda tick: of_units(transpose_weights, tick, 0),
            "bias": biases,
            "q_o": lambda tick: of_groups(quantise_o, tick, L_QO),
            "scale": lambda tick: of_bank(scale_maxima, tick, 0),
        }
        ORDER = ("exp", "cpw", "norm", "prep", "qw", "q_o", "inv", "bias", "score", "tr_e", "trw", "warm", "tr_o", "maxima", "cp_o", "cp_e", "q_e", "q1", "q23", "attend", "project", "scale")
        last_tile = Q_TILES - 1
        for tick in range(2 * PAIRS - 1 + L_NORM):
            for stage in ORDER:
                stages[stage](tick)
        for qt, n_slice in to_project:
            add_bias_and_store(qt, n_slice, project_slice(qt, n_slice))
        for job in y_waiting:
            add_bias_and_store(*job[1:])
        last_y = []
        for n_slice in range(N_SLICES):
            y_ps = psum_b.tile([P, BANK_F32], F32, name="last_y", tag="bank")
            last_y.append(y_ps)
        for g in range(TAIL_EARLY):
            for n_slice in range(N_SLICES):
                project(last_tile, n_slice, g, last_y[n_slice])
        last_group = (last_tile, GROUPS - 1)
        transpose_o(last_group)
        copy_o(last_group)
        quantise_o(last_group)
        half = N_SLICES // 2
        for slices, groups in (
            (range(N_SLICES), range(TAIL_EARLY, GROUPS - 2)),
            (range(half), range(GROUPS - 2, GROUPS - 1)),
            (range(half), range(GROUPS - 1, GROUPS)),
        ):
            for g in groups:
                for n_slice in slices:
                    project(last_tile, n_slice, g, last_y[n_slice])
        for n_slice in range(half, N_SLICES):
            for g in range(GROUPS - 2, GROUPS):
                project(last_tile, n_slice, g, last_y[n_slice])
        for n_slice in range(N_SLICES):
            add_bias_and_store(last_tile, n_slice, last_y[n_slice])
